import numpy as np
import ml_dtypes


def mxq(x, axis, fmt="e4m3"):
    dtype, down = {"e4m3": (ml_dtypes.float8_e4m3fn, 7), "e5m2": (ml_dtypes.float8_e5m2, 14)}[fmt]
    v = np.moveaxis(np.asarray(x, np.float32).astype(ml_dtypes.bfloat16).astype(np.float64), axis, -1)
    blocks = v.reshape(v.shape[:-1] + (-1, 32))
    amax = np.abs(blocks).max(-1, keepdims=True)
    byte = np.maximum(np.where(amax > 0, np.frexp(amax)[1] - 1 + 127, 0) - down, 1)
    scale = np.exp2(byte - 127.0)
    codes = (blocks / scale).astype(np.float32).astype(dtype).astype(np.float64)
    return np.moveaxis((codes * scale).reshape(v.shape), -1, axis)


WIDE = False


def mx_kscale(k):
    if not WIDE:
        return np.ones(k)
    levels = np.array([10, -10, 5, -5, 0])
    a = np.random.permutation(np.resize(levels, k // 512 * 4)).reshape(k // 512, 4)
    idx = np.arange(k)
    return np.exp2(a[idx // 512, idx % 128 // 32])


BF16 = ml_dtypes.bfloat16


def bf(x):
    return np.asarray(x, np.float32).astype(BF16)


def f64(x):
    return np.asarray(x).astype(np.float64)


B, S, D, H = 4, 512, 1024, 8
HD = D // H
NEG_INF = -1e30


def alibi_causal_mask():
    i = np.arange(S)[:, None]
    j = np.arange(S)[None, :]
    return np.where(j <= i, -f64(i - j), NEG_INF)


def setup_inputs():
    t = mx_kscale(D)
    return {"q": bf(np.random.standard_normal((B, H, S, HD)) * 1.5),
            "k": bf(np.random.standard_normal((B, H, S, HD)) * 1.5),
            "v": bf(np.random.standard_normal((B, H, S, HD)) * 1.5 * t.reshape(H, 1, HD)),
            "w_out": bf(np.random.standard_normal((D, D)) / np.sqrt(D) / t[None, :]),
            "b_out": bf(np.random.standard_normal(D) * 0.1)}


def reference(q, k, v, w_out, b_out):
    s = f64(q) @ f64(k).transpose(0, 1, 3, 2) / np.sqrt(HD) + alibi_causal_mask()
    e = np.exp(s - s.max(-1, keepdims=True))
    o = (mxq(e, 3, "e4m3") @ mxq(f64(v), 2, "e4m3")) / e.sum(-1, keepdims=True)
    a = o.transpose(0, 2, 1, 3).reshape(B, S, D)
    return (mxq(a, 2, "e4m3") @ mxq(f64(w_out), 1, "e4m3").T) + f64(b_out)

@@ -1,0 +1,287 @@
+import math
+from contextlib import ExitStack
+
+import concourse.mybir as mybir
+from concourse.masks import make_identity
+
+F32 = mybir.dt.float32
+BF16 = mybir.dt.bfloat16
+U32 = mybir.dt.uint32
+U8 = mybir.dt.uint8
+FP8X4 = mybir.dt.float8_e4m3fn_x4
+ALU = mybir.AluOpType
+ACT = mybir.ActivationFunctionType
+AXIS_X = mybir.AxisListType.X
+
+B, H, S, HD = 4, 8, 512, 128
+D = H * HD
+P = 128
+PACK = 4
+BANK = 512
+QB = S // P
+GROUPS = H // PACK
+N_HEADS = B * H
+SCALE = 1.0 / math.sqrt(HD)
+FAR = 1.0e30
+
+FLOPS = 2 * (2 * B * H * S * S * HD) + 2 * B * S * D * D
+
+SEG_ORDER = (3, 2, 0, 1)
+SEG_START = {3: 0, 2: 512, 0: 896, 1: 1024}
+SEG_COLS = 1280
+SEG_BLOCKS = SEG_COLS // P
+LOAD_AHEAD = 3
+
+
+def tile_alibiattention_pa_kernel(tc, q, k, v, w_out, b_out, out):
+    nc = tc.nc
+    with ExitStack() as ctx:
+        const = ctx.enter_context(tc.tile_pool(name="const", bufs=1))
+        loads = ctx.enter_context(tc.tile_pool(name="loads", bufs=LOAD_AHEAD + 2))
+        work = ctx.enter_context(tc.tile_pool(name="work", bufs=2))
+        keep = ctx.enter_context(tc.tile_pool(name="keep", bufs=4))
+        psum = ctx.enter_context(tc.psum_pool(name="psum", bufs=1))
+
+        pair_tiles = {}
+
+        def load_pair(pair):
+            b, h0 = pair // (H // 2), 2 * (pair % (H // 2))
+            q_sb = loads.tile([P, 2, QB, HD], BF16)
+            k_sb = loads.tile([P, 2, QB, HD], BF16)
+            v_sb = loads.tile([P, 2, QB, HD], BF16)
+            for dst, src in ((q_sb, q), (k_sb, k), (v_sb, v)):
+                nc.sync.dma_start(out=dst[:], in_=src[b, h0 : h0 + 2].rearrange("h (t p) d -> p h t d", p=P))
+            pair_tiles[pair] = (q_sb, k_sb, v_sb)
+
+        for pair in range(LOAD_AHEAD):
+            load_pair(pair)
+
+        w_sb = const.tile([P, D // P, D], BF16)
+        nc.scalar.dma_start(out=w_sb[:], in_=w_out.rearrange("(nb p) f -> p nb f", p=P))
+        bias = const.tile([P, D], BF16)
+        nc.scalar.dma_start(out=bias[:], in_=b_out.partition_broadcast(P))
+
+        ident = const.tile([P, P], BF16)
+        make_identity(nc, ident[:])
+
+        negmask = const.tile([P, SEG_COLS], F32)
+        nc.gpsimd.iota(
+            negmask[:, 0:S],
+            pattern=[[-1, S]],
+            base=S - P,
+            channel_multiplier=1,
+            allow_small_or_imprecise_dtypes=True,
+        )
+        nc.gpsimd.affine_select(
+            out=negmask[:, 0:S],
+            in_=negmask[:, 0:S],
+            pattern=[[-1, S]],
+            compare_op=ALU.is_ge,
+            fill=FAR,
+            base=S - P,
+            channel_multiplier=1,
+        )
+        for qi in (2, 0, 1):
+            n = (qi + 1) * P
+            nc.vector.tensor_copy(out=negmask[:, SEG_START[qi] : SEG_START[qi] + n], in_=negmask[:, S - n : S])
+
+        grouped_e = []
+        for parity in range(2):
+            ge = const.tile([P, S, PACK], BF16, name="ge%d" % parity, align_bytes=64)
+            nc.vector.memset(ge[:], 0.0)
+            grouped_e.append(ge)
+
+        w_codes = const.tile([P, GROUPS, D], U32, align_bytes=64)
+        w_scales = const.tile([P, GROUPS, D], U8, align_bytes=64)
+
+        transposed = {}
+        v_operands = {}
+        probs = {}
+        e_operands = {}
+        a_tiles = {}
+        a_operands = {}
+
+        def prepare_w(piece):
+            g, nb0 = piece // (D // P // 2), 2 * (piece % (D // P // 2))
+            wT = psum.tile([P, 2, PACK, P], BF16, tag="misc")
+            for j in range(2):
+                for t in range(PACK):
+                    f0 = (PACK * g + t) * P
+                    nc.tensor.transpose(wT[:, j, t, :], w_sb[:, nb0 + j, f0 : f0 + P], ident[:])
+            gw = work.tile([P, 2, P, PACK], BF16, align_bytes=64)
+            nc.scalar.copy(out=gw[:], in_=wT[:].rearrange("p j t n -> p j n t"))
+            cols = slice(nb0 * P, (nb0 + 2) * P)
+            nc.vector.quantize_mx(
+                out=w_codes[:, g, cols].bitcast(FP8X4),
+                scales=w_scales[:, g, cols],
+                in_=gw[:].rearrange("p j n t -> p (j n t)"),
+            )
+
+        def prepare_head(i):
+            pair, j = i // 2, i % 2
+            if j == 0 and pair + LOAD_AHEAD < N_HEADS // 2:
+                load_pair(pair + LOAD_AHEAD)
+            q_sb, k_sb, v_sb = pair_tiles[pair]
+            qkT_ps = psum.tile([P, 2, S], BF16, tag="qkT")
+            for which, src in enumerate((q_sb, k_sb)):
+                for t in range(QB):
+                    nc.tensor.transpose(qkT_ps[:, which, t * P : (t + 1) * P], src[:, j, t, :], ident[:])
+            qkT = work.tile([P, 2, S], BF16)
+            nc.scalar.copy(out=qkT[:], in_=qkT_ps[:])
+            transposed[i] = qkT
+            if j == 0:
+                gv = work.tile([P, 2, HD, PACK], BF16, align_bytes=64)
+                for jj in range(2):
+                    nc.vector.tensor_copy(out=gv[:, jj], in_=v_sb[:, jj].rearrange("p t d -> p d t"))
+                v_codes = keep.tile([P, 2, HD], U32, align_bytes=64)
+                v_scales = keep.tile([P, 2, HD], U8, align_bytes=64)
+                nc.vector.quantize_mx(
+                    out=v_codes[:].rearrange("p j d -> p (j d)").bitcast(FP8X4),
+                    scales=v_scales[:].rearrange("p j d -> p (j d)"),
+                    in_=gv[:].rearrange("p j d t -> p (j d t)"),
+                )
+                v_operands[pair] = (v_codes, v_scales)
+
+        def scores(i):
+            qkT = transposed[i]
+            s_a = psum.tile([P, BANK], F32, tag="s_a")
+            s_b = psum.tile([P, BANK], F32, tag="s_b")
+            s_c = psum.tile([P, BANK], F32, tag="s_c")
+            banks = (s_a, s_b, s_c)
+            for qi in SEG_ORDER:
+                n = (qi + 1) * P
+                col = SEG_START[qi] % BANK
+                nc.tensor.matmul(
+                    out=banks[SEG_START[qi] // BANK][:, col : col + n],
+                    lhsT=qkT[:, 0, qi * P : (qi + 1) * P],
+                    rhs=qkT[:, 1, 0:n],
+                    start=True,
+                    stop=True,
+                )
+            x = work.tile([P, SEG_COLS], F32)
+            for index, bank in enumerate(banks):
+                width = min(BANK, SEG_COLS - index * BANK)
+                cols = slice(index * BANK, index * BANK + width)
+                nc.vector.scalar_tensor_tensor(
+                    out=x[:, cols], in0=bank[:, 0:width], scalar=-SCALE, in1=negmask[:, cols], op0=ALU.mult, op1=ALU.add
+                )
+            negmax = work.tile([P, QB], F32)
+            rowsum = keep.tile([P, QB], F32)
+            e_sb = keep.tile([P, SEG_COLS], BF16)
+            for qi in SEG_ORDER:
+                cols = slice(SEG_START[qi], SEG_START[qi] + (qi + 1) * P)
+                nc.vector.tensor_reduce(out=negmax[:, qi : qi + 1], in_=x[:, cols], axis=AXIS_X, op=ALU.min)
+                nc.scalar.activation(
+                    out=e_sb[:, cols],
+                    in_=x[:, cols],
+                    func=ACT.Exp,
+                    scale=-1.0,
+                    bias=negmax[:, qi : qi + 1],
+                    accum_out=rowsum[:, qi : qi + 1],
+                )
+            probs[i] = (e_sb, rowsum)
+
+        def quantise_e(i):
+            e_sb = probs[i][0]
+            eT_x = psum.tile([P, 8, P], BF16, tag="eT_x")
+            eT_y = psum.tile([P, SEG_BLOCKS - 8, P], BF16, tag="eT_y")
+            for block in range(SEG_BLOCKS):
+                dst = eT_x[:, block, :] if block < 8 else eT_y[:, block - 8, :]
+                nc.tensor.transpose(dst, e_sb[:, block * P : (block + 1) * P], ident[:])
+            ge = grouped_e[i % 2]
+            for qi in SEG_ORDER:
+                first = SEG_START[qi] // P
+                src = eT_x[:, first : first + qi + 1, :] if first < 8 else eT_y[:, first - 8 : first - 8 + qi + 1, :]
+                nc.scalar.copy(out=ge[:, qi * P : (qi + 1) * P, 0 : qi + 1], in_=src.rearrange("p t q -> p q t"))
+            e_codes = keep.tile([P, S], U32, align_bytes=64)
+            e_scales = keep.tile([P, S], U8, align_bytes=64)
+            nc.vector.quantize_mx(
+                out=e_codes[:].bitcast(FP8X4), scales=e_scales[:], in_=ge[:].rearrange("p q t -> p (q t)")
+            )
+            e_operands[i] = (e_codes, e_scales)
+
+        def attend(i):
+            b, h = i // H, i % H
+            g, t = h // PACK, h % PACK
+            e_codes, e_scales = e_operands[i]
+            v_codes, v_scales = v_operands[i // 2]
+            rowsum = probs[i][1]
+            o_ps = psum.tile([P, QB, HD], F32, tag="o")
+            for qi in range(QB):
+                cols = slice(qi * P, (qi + 1) * P)
+                nc.tensor.matmul_mx(
+                    out=o_ps[:, qi, :],
+                    lhsT=e_codes[:, cols].bitcast(FP8X4),
+                    lhsT_scale=e_scales[:, cols],
+                    rhs=v_codes[:, i % 2, :].bitcast(FP8X4),
+                    rhs_scale=v_scales[:, i % 2, :],
+                    start=True,
+                    stop=True,
+                )
+            rinv = work.tile([P, QB], F32)
+            nc.vector.reciprocal(out=rinv[:], in_=rowsum[:])
+            if t == 0:
+                a_new = work.tile([P, PACK, QB, HD], BF16)
+                a_tiles[(b, g)] = a_new
+            a_sb = a_tiles[(b, g)]
+            nc.vector.tensor_tensor(
+                out=a_sb[:, t], in0=o_ps[:], in1=rinv[:].unsqueeze(2).to_broadcast([P, QB, HD]), op=ALU.mult
+            )
+
+        def quantise_a(b, g):
+            a_sb = a_tiles[(b, g)]
+            if g == 0:
+                a_codes = work.tile([P, GROUPS, S], U32, align_bytes=64)
+                a_scales = work.tile([P, GROUPS, S], U8, align_bytes=64)
+                a_operands[b] = (a_codes, a_scales)
+            a_codes, a_scales = a_operands[b]
+            ga = work.tile([P, QB, P, PACK], BF16, align_bytes=64)
+            for half in range(QB // 2):
+                aT = psum.tile([P, 2, PACK, P], BF16, tag="misc")
+                for j in range(2):
+                    for t in range(PACK):
+                        nc.tensor.transpose(aT[:, j, t, :], a_sb[:, t, 2 * half + j, :], ident[:])
+                nc.scalar.copy(out=ga[:, 2 * half : 2 * half + 2], in_=aT[:].rearrange("p j t q -> p j q t"))
+            nc.vector.quantize_mx(
+                out=a_codes[:, g, :].bitcast(FP8X4),
+                scales=a_scales[:, g, :],
+                in_=ga[:].rearrange("p c q t -> p (c q t)"),
+            )
+
+        def project(b):
+            a_codes, a_scales = a_operands[b]
+            for tb in range(QB):
+                out_sb = work.tile([P, D], F32, bufs=3)
+                for nh in range(D // BANK):
+                    acc = psum.tile([P, BANK], F32, tag="s_a" if nh == 0 else "s_b")
+                    n_cols = slice(nh * BANK, (nh + 1) * BANK)
+                    for g in range(GROUPS):
+                        nc.tensor.matmul_mx(
+                            out=acc[:],
+                            lhsT=a_codes[:, g, tb * P : (tb + 1) * P].bitcast(FP8X4),
+                            lhsT_scale=a_scales[:, g, tb * P : (tb + 1) * P],
+                            rhs=w_codes[:, g, n_cols].bitcast(FP8X4),
+                            rhs_scale=w_scales[:, g, n_cols],
+                            start=(g == 0),
+                            stop=(g == GROUPS - 1),
+                        )
+                    nc.vector.tensor_tensor(out=out_sb[:, n_cols], in0=acc[:], in1=bias[:, n_cols], op=ALU.add)
+                nc.gpsimd.dma_start(out=out[b, tb * P : (tb + 1) * P, :], in_=out_sb[:])
+
+        W_PIECES = GROUPS * (D // P // 2)
+        for step in range(N_HEADS + 3):
+            done = step - 3
+            if 0 <= done:
+                attend(done)
+                if done % PACK == PACK - 1:
+                    quantise_a(done // H, (done % H) // PACK)
+                if done % H == H - 1:
+                    project(done // H)
+            if 0 <= step - 2 < N_HEADS:
+                quantise_e(step - 2)
+            if 0 <= step - 1 < N_HEADS:
+                scores(step - 1)
+            if step < N_HEADS:
+                prepare_head(step)
+            if step < W_PIECES:
+                prepare_w(step)

@@ -11,7 +11,6 @@ U8 = mybir.dt.uint8
 FP8X4 = mybir.dt.float8_e4m3fn_x4
 ALU = mybir.AluOpType
 ACT = mybir.ActivationFunctionType
-AXIS_X = mybir.AxisListType.X
 
 B, H, S, HD = 4, 8, 512, 128
 D = H * HD
@@ -21,6 +20,7 @@ BANK = 512
 QB = S // P
 GROUPS = H // PACK
 N_HEADS = B * H
+N_PAIRS = N_HEADS // 2
 SCALE = 1.0 / math.sqrt(HD)
 FAR = 1.0e30
 
@@ -31,11 +31,22 @@ SEG_START = {3: 0, 2: 512, 0: 896, 1: 1024}
 SEG_COLS = 1280
 SEG_BLOCKS = SEG_COLS // P
 LOAD_AHEAD = 3
+W_PIECES = GROUPS * (D // P // 2)
+OUT_TILES = QB * (D // BANK)
+
+
+def seg(qi):
+    return slice(SEG_START[qi], SEG_START[qi] + (qi + 1) * P)
+
+
+def live(i):
+    return 0 <= i < N_HEADS
 
 
 def tile_alibiattention_pa_kernel(tc, q, k, v, w_out, b_out, out):
     nc = tc.nc
     with ExitStack() as ctx:
+        ctx.enter_context(tc.manual_schedule())
         const = ctx.enter_context(tc.tile_pool(name="const", bufs=1))
         loads = ctx.enter_context(tc.tile_pool(name="loads", bufs=LOAD_AHEAD + 2))
         work = ctx.enter_context(tc.tile_pool(name="work", bufs=2))
@@ -53,13 +64,13 @@ def tile_alibiattention_pa_kernel(tc, q, k, v, w_out, b_out, out):
                 nc.sync.dma_start(out=dst[:], in_=src[b, h0 : h0 + 2].rearrange("h (t p) d -> p h t d", p=P))
             pair_tiles[pair] = (q_sb, k_sb, v_sb)
 
-        for pair in range(LOAD_AHEAD):
-            load_pair(pair)
-
+        load_pair(0)
+        load_pair(1)
         w_sb = const.tile([P, D // P, D], BF16)
-        nc.scalar.dma_start(out=w_sb[:], in_=w_out.rearrange("(nb p) f -> p nb f", p=P))
+        nc.sync.dma_start(out=w_sb[:], in_=w_out.rearrange("(nb p) f -> p nb f", p=P))
         bias = const.tile([P, D], BF16)
-        nc.scalar.dma_start(out=bias[:], in_=b_out.partition_broadcast(P))
+        nc.sync.dma_start(out=bias[:], in_=b_out.partition_broadcast(P))
+        load_pair(2)
 
         ident = const.tile([P, P], BF16)
         make_identity(nc, ident[:])
@@ -82,8 +93,7 @@ def tile_alibiattention_pa_kernel(tc, q, k, v, w_out, b_out, out):
             channel_multiplier=1,
         )
         for qi in (2, 0, 1):
-            n = (qi + 1) * P
-            nc.vector.tensor_copy(out=negmask[:, SEG_START[qi] : SEG_START[qi] + n], in_=negmask[:, S - n : S])
+            nc.vector.tensor_copy(out=negmask[:, seg(qi)], in_=negmask[:, S - (qi + 1) * P : S])
 
         grouped_e = []
         for parity in range(2):
@@ -94,16 +104,230 @@ def tile_alibiattention_pa_kernel(tc, q, k, v, w_out, b_out, out):
         w_codes = const.tile([P, GROUPS, D], U32, align_bytes=64)
         w_scales = const.tile([P, GROUPS, D], U8, align_bytes=64)
 
-        transposed = {}
-        v_operands = {}
-        probs = {}
+        qkT_banks = {}
+        qkT_tiles = {}
+        score_banks = {}
+        x_tiles = {}
+        e_tiles = {}
+        rowsums = {}
+        eT_banks = {}
         e_operands = {}
+        v_operands = {}
+        o_banks = {}
         a_tiles = {}
+        ga_tiles = {}
         a_operands = {}
+        acc_banks = {}
+
+        def transpose_qk(i):
+            q_sb, k_sb, v_sb = pair_tiles[i // 2]
+            qkT_ps = psum.tile([P, 2, S], BF16, tag="qkT")
+            for which, src in enumerate((q_sb, k_sb)):
+                for t in range(QB):
+                    nc.tensor.transpose(qkT_ps[:, which, t * P : (t + 1) * P], src[:, i % 2, t, :], ident[:])
+            qkT_banks[i] = qkT_ps
+
+        def score_block(i, qi, bank):
+            n = (qi + 1) * P
+            col = SEG_START[qi] % BANK
+            qkT = qkT_tiles[i]
+            nc.tensor.matmul(
+                out=bank[:, col : col + n],
+                lhsT=qkT[:, 0, qi * P : (qi + 1) * P],
+                rhs=qkT[:, 1, 0:n],
+                start=True,
+                stop=True,
+            )
+
+        def scores_first_banks(i):
+            s_a = psum.tile([P, BANK], F32, tag="s_a")
+            s_b = psum.tile([P, BANK], F32, tag="s_b")
+            score_block(i, 3, s_a)
+            score_block(i, 2, s_b)
+            score_block(i, 0, s_b)
+            score_banks[(i, 0)] = s_a
+            score_banks[(i, 1)] = s_b
+
+        def scores_last_bank(i):
+            s_c = psum.tile([P, BANK], F32, tag="s_a")
+            score_block(i, 1, s_c)
+            score_banks[(i, 2)] = s_c
+
+        def transpose_e(i):
+            e_sb = e_tiles[i]
+            eT_x = psum.tile([P, 8, P], BF16, tag="eT_x")
+            eT_y = psum.tile([P, SEG_BLOCKS - 8, P], BF16, tag="eT_y")
+            for block in range(SEG_BLOCKS):
+                dst = eT_x[:, block, :] if block < 8 else eT_y[:, block - 8, :]
+                nc.tensor.transpose(dst, e_sb[:, block * P : (block + 1) * P], ident[:])
+            eT_banks[i] = (eT_x, eT_y)
+
+        def attend(i):
+            e_codes, e_scales = e_operands[i]
+            v_codes, v_scales = v_operands[i // 2]
+            o_ps = psum.tile([P, QB, HD], F32, tag="o")
+            for qi in range(QB):
+                cols = slice(qi * P, (qi + 1) * P)
+                nc.tensor.matmul_mx(
+                    out=o_ps[:, qi, :],
+                    lhsT=e_codes[:, cols].bitcast(FP8X4),
+                    lhsT_scale=e_scales[:, cols],
+                    rhs=v_codes[:, i % 2, :].bitcast(FP8X4),
+                    rhs_scale=v_scales[:, i % 2, :],
+                    start=True,
+                    stop=True,
+                )
+            o_banks[i] = o_ps
+
+        def project(b, r):
+            tb, nh = r // (D // BANK), r % (D // BANK)
+            a_codes, a_scales = a_operands[b]
+            acc = psum.tile([P, BANK], F32, tag="misc", bufs=2)
+            for g in range(GROUPS):
+                nc.tensor.matmul_mx(
+                    out=acc[:],
+                    lhsT=a_codes[:, g, tb * P : (tb + 1) * P].bitcast(FP8X4),
+                    lhsT_scale=a_scales[:, g, tb * P : (tb + 1) * P],
+                    rhs=w_codes[:, g, nh * BANK : (nh + 1) * BANK].bitcast(FP8X4),
+                    rhs_scale=w_scales[:, g, nh * BANK : (nh + 1) * BANK],
+                    start=(g == 0),
+                    stop=(g == GROUPS - 1),
+                )
+            acc_banks[(b, r)] = acc
+
+        def copy_qk(i):
+            qkT = work.tile([P, 2, S], BF16)
+            nc.scalar.copy(out=qkT[:], in_=qkT_banks[i][:])
+            qkT_tiles[i] = qkT
+
+        def add_mask(i, bank):
+            if bank == 0:
+                x_new = work.tile([P, SEG_COLS], F32)
+                negmax_new = work.tile([P, QB], F32)
+                x_tiles[i] = (x_new, negmax_new)
+            x = x_tiles[i][0]
+            width = min(BANK, SEG_COLS - bank * BANK)
+            cols = slice(bank * BANK, bank * BANK + width)
+            nc.vector.scalar_tensor_tensor(
+                out=x[:, cols],
+                in0=score_banks[(i, bank)][:, 0:width],
+                scalar=-SCALE,
+                in1=negmask[:, cols],
+                op0=ALU.mult,
+                op1=ALU.add,
+            )
+
+        def row_min(i, qi):
+            x, negmax = x_tiles[i]
+            nc.vector.tensor_scalar(
+                out=x[:, seg(qi)],
+                in0=x[:, seg(qi)],
+                scalar1=1.0,
+                scalar2=None,
+                op0=ALU.mult,
+                op1=ALU.min,
+                accum_out=negmax[:, qi : qi + 1],
+            )
+
+        def exponentials(i):
+            x, negmax = x_tiles[i]
+            rowsum = keep.tile([P, QB], F32)
+            e_sb = work.tile([P, SEG_COLS], BF16)
+            for qi in SEG_ORDER:
+                nc.scalar.activation(
+                    out=e_sb[:, seg(qi)],
+                    in_=x[:, seg(qi)],
+                    func=ACT.Exp,
+                    scale=-1.0,
+                    bias=negmax[:, qi : qi + 1],
+                    accum_out=rowsum[:, qi : qi + 1],
+                )
+            e_tiles[i] = e_sb
+            rowsums[i] = rowsum
+
+        def regroup_e(i):
+            eT_x, eT_y = eT_banks[i]
+            ge = grouped_e[i % 2]
+            for qi in SEG_ORDER:
+                first = SEG_START[qi] // P
+                src = eT_x[:, first : first + qi + 1, :] if first < 8 else eT_y[:, first - 8 : first - 8 + qi + 1, :]
+                nc.scalar.copy(out=ge[:, qi * P : (qi + 1) * P, 0 : qi + 1], in_=src.rearrange("p t q -> p q t"))
+
+        def quantise_e(i):
+            e_codes = work.tile([P, S], U32, align_bytes=64)
+            e_scales = work.tile([P, S], U8, align_bytes=64)
+            nc.vector.quantize_mx(
+                out=e_codes[:].bitcast(FP8X4),
+                scales=e_scales[:],
+                in_=grouped_e[i % 2][:].rearrange("p q t -> p (q t)"),
+            )
+            e_operands[i] = (e_codes, e_scales)
+
+        def quantise_v(pair):
+            v_sb = pair_tiles[pair][2]
+            gv = work.tile([P, 2, HD, PACK], BF16, align_bytes=64)
+            for j in range(2):
+                nc.vector.tensor_copy(
+                    out=gv[:, j].rearrange("p (c i) t -> p c t i", i=4),
+                    in_=v_sb[:, j].rearrange("p t (c i) -> p c t i", i=4),
+                )
+            v_codes = keep.tile([P, 2, HD], U32, align_bytes=64)
+            v_scales = keep.tile([P, 2, HD], U8, align_bytes=64)
+            nc.vector.quantize_mx(
+                out=v_codes[:].rearrange("p j d -> p (j d)").bitcast(FP8X4),
+                scales=v_scales[:].rearrange("p j d -> p (j d)"),
+                in_=gv[:].rearrange("p j d t -> p (j d t)"),
+            )
+            v_operands[pair] = (v_codes, v_scales)
+
+        def normalise(i):
+            b, g, t = i // H, (i % H) // PACK, i % PACK
+            rinv = work.tile([P, QB], F32)
+            nc.vector.reciprocal(out=rinv[:], in_=rowsums[i][:])
+            if t == 0:
+                a_new = work.tile([P, PACK, QB, HD], BF16)
+                a_tiles[(b, g)] = a_new
+            nc.vector.tensor_tensor(
+                out=a_tiles[(b, g)][:, t],
+                in0=o_banks[i][:],
+                in1=rinv[:].unsqueeze(2).to_broadcast([P, QB, HD]),
+                op=ALU.mult,
+            )
+
+        def regroup_a(b, g, half):
+            if half == 0:
+                ga_new = work.tile([P, QB, P, PACK], BF16, align_bytes=64)
+                ga_tiles[(b, g)] = ga_new
+            aT = psum.tile([P, 2, PACK, P], BF16, tag="misc", bufs=2)
+            for j in range(2):
+                for t in range(PACK):
+                    nc.tensor.transpose(aT[:, j, t, :], a_tiles[(b, g)][:, t, 2 * half + j, :], ident[:])
+            nc.scalar.copy(
+                out=ga_tiles[(b, g)][:, 2 * half : 2 * half + 2], in_=aT[:].rearrange("p j t q -> p j q t")
+            )
+
+        def quantise_a(b, g):
+            if g == 0:
+                a_codes_new = work.tile([P, GROUPS, S], U32, align_bytes=64)
+                a_scales_new = work.tile([P, GROUPS, S], U8, align_bytes=64)
+                a_operands[b] = (a_codes_new, a_scales_new)
+            a_codes, a_scales = a_operands[b]
+            nc.vector.quantize_mx(
+                out=a_codes[:, g, :].bitcast(FP8X4),
+                scales=a_scales[:, g, :],
+                in_=ga_tiles[(b, g)][:].rearrange("p c q t -> p (c q t)"),
+            )
+
+        def add_bias_and_store(b, r):
+            tb, nh = r // (D // BANK), r % (D // BANK)
+            n_cols = slice(nh * BANK, (nh + 1) * BANK)
+            out_sb = work.tile([P, BANK], F32, bufs=3)
+            nc.vector.tensor_tensor(out=out_sb[:], in0=acc_banks[(b, r)][:], in1=bias[:, n_cols], op=ALU.add)
+            nc.gpsimd.dma_start(out=out[b, tb * P : (tb + 1) * P, n_cols], in_=out_sb[:])
 
         def prepare_w(piece):
             g, nb0 = piece // (D // P // 2), 2 * (piece % (D // P // 2))
-            wT = psum.tile([P, 2, PACK, P], BF16, tag="misc")
+            wT = psum.tile([P, 2, PACK, P], BF16, tag="misc", bufs=2)
             for j in range(2):
                 for t in range(PACK):
                     f0 = (PACK * g + t) * P
@@ -117,171 +341,46 @@ def tile_alibiattention_pa_kernel(tc, q, k, v, w_out, b_out, out):
                 in_=gw[:].rearrange("p j n t -> p (j n t)"),
             )
 
-        def prepare_head(i):
-            pair, j = i // 2, i % 2
-            if j == 0 and pair + LOAD_AHEAD < N_HEADS // 2:
-                load_pair(pair + LOAD_AHEAD)
-            q_sb, k_sb, v_sb = pair_tiles[pair]
-            qkT_ps = psum.tile([P, 2, S], BF16, tag="qkT")
-            for which, src in enumerate((q_sb, k_sb)):
-                for t in range(QB):
-                    nc.tensor.transpose(qkT_ps[:, which, t * P : (t + 1) * P], src[:, j, t, :], ident[:])
-            qkT = work.tile([P, 2, S], BF16)
-            nc.scalar.copy(out=qkT[:], in_=qkT_ps[:])
-            transposed[i] = qkT
-            if j == 0:
-                gv = work.tile([P, 2, HD, PACK], BF16, align_bytes=64)
-                for jj in range(2):
-                    nc.vector.tensor_copy(out=gv[:, jj], in_=v_sb[:, jj].rearrange("p t d -> p d t"))
-                v_codes = keep.tile([P, 2, HD], U32, align_bytes=64)
-                v_scales = keep.tile([P, 2, HD], U8, align_bytes=64)
-                nc.vector.quantize_mx(
-                    out=v_codes[:].rearrange("p j d -> p (j d)").bitcast(FP8X4),
-                    scales=v_scales[:].rearrange("p j d -> p (j d)"),
-                    in_=gv[:].rearrange("p j d t -> p (j d t)"),
-                )
-                v_operands[pair] = (v_codes, v_scales)
-
-        def scores(i):
-            qkT = transposed[i]
-            s_a = psum.tile([P, BANK], F32, tag="s_a")
-            s_b = psum.tile([P, BANK], F32, tag="s_b")
-            s_c = psum.tile([P, BANK], F32, tag="s_c")
-            banks = (s_a, s_b, s_c)
-            for qi in SEG_ORDER:
-                n = (qi + 1) * P
-                col = SEG_START[qi] % BANK
-                nc.tensor.matmul(
-                    out=banks[SEG_START[qi] // BANK][:, col : col + n],
-                    lhsT=qkT[:, 0, qi * P : (qi + 1) * P],
-                    rhs=qkT[:, 1, 0:n],
-                    start=True,
-                    stop=True,
-                )
-            x = work.tile([P, SEG_COLS], F32)
-            for index, bank in enumerate(banks):
-                width = min(BANK, SEG_COLS - index * BANK)
-                cols = slice(index * BANK, index * BANK + width)
-                nc.vector.scalar_tensor_tensor(
-                    out=x[:, cols], in0=bank[:, 0:width], scalar=-SCALE, in1=negmask[:, cols], op0=ALU.mult, op1=ALU.add
-                )
-            negmax = work.tile([P, QB], F32)
-            rowsum = keep.tile([P, QB], F32)
-            e_sb = keep.tile([P, SEG_COLS], BF16)
-            for qi in SEG_ORDER:
-                cols = slice(SEG_START[qi], SEG_START[qi] + (qi + 1) * P)
-                nc.vector.tensor_reduce(out=negmax[:, qi : qi + 1], in_=x[:, cols], axis=AXIS_X, op=ALU.min)
-                nc.scalar.activation(
-                    out=e_sb[:, cols],
-                    in_=x[:, cols],
-                    func=ACT.Exp,
-                    scale=-1.0,
-                    bias=negmax[:, qi : qi + 1],
-                    accum_out=rowsum[:, qi : qi + 1],
-                )
-            probs[i] = (e_sb, rowsum)
-
-        def quantise_e(i):
-            e_sb = probs[i][0]
-            eT_x = psum.tile([P, 8, P], BF16, tag="eT_x")
-            eT_y = psum.tile([P, SEG_BLOCKS - 8, P], BF16, tag="eT_y")
-            for block in range(SEG_BLOCKS):
-                dst = eT_x[:, block, :] if block < 8 else eT_y[:, block - 8, :]
-                nc.tensor.transpose(dst, e_sb[:, block * P : (block + 1) * P], ident[:])
-            ge = grouped_e[i % 2]
-            for qi in SEG_ORDER:
-                first = SEG_START[qi] // P
-                src = eT_x[:, first : first + qi + 1, :] if first < 8 else eT_y[:, first - 8 : first - 8 + qi + 1, :]
-                nc.scalar.copy(out=ge[:, qi * P : (qi + 1) * P, 0 : qi + 1], in_=src.rearrange("p t q -> p q t"))
-            e_codes = keep.tile([P, S], U32, align_bytes=64)
-            e_scales = keep.tile([P, S], U8, align_bytes=64)
-            nc.vector.quantize_mx(
-                out=e_codes[:].bitcast(FP8X4), scales=e_scales[:], in_=ge[:].rearrange("p q t -> p (q t)")
-            )
-            e_operands[i] = (e_codes, e_scales)
-
-        def attend(i):
-            b, h = i // H, i % H
-            g, t = h // PACK, h % PACK
-            e_codes, e_scales = e_operands[i]
-            v_codes, v_scales = v_operands[i // 2]
-            rowsum = probs[i][1]
-            o_ps = psum.tile([P, QB, HD], F32, tag="o")
-            for qi in range(QB):
-                cols = slice(qi * P, (qi + 1) * P)
-                nc.tensor.matmul_mx(
-                    out=o_ps[:, qi, :],
-                    lhsT=e_codes[:, cols].bitcast(FP8X4),
-                    lhsT_scale=e_scales[:, cols],
-                    rhs=v_codes[:, i % 2, :].bitcast(FP8X4),
-                    rhs_scale=v_scales[:, i % 2, :],
-                    start=True,
-                    stop=True,
-                )
-            rinv = work.tile([P, QB], F32)
-            nc.vector.reciprocal(out=rinv[:], in_=rowsum[:])
-            if t == 0:
-                a_new = work.tile([P, PACK, QB, HD], BF16)
-                a_tiles[(b, g)] = a_new
-            a_sb = a_tiles[(b, g)]
-            nc.vector.tensor_tensor(
-                out=a_sb[:, t], in0=o_ps[:], in1=rinv[:].unsqueeze(2).to_broadcast([P, QB, HD]), op=ALU.mult
-            )
-
-        def quantise_a(b, g):
-            a_sb = a_tiles[(b, g)]
-            if g == 0:
-                a_codes = work.tile([P, GROUPS, S], U32, align_bytes=64)
-                a_scales = work.tile([P, GROUPS, S], U8, align_bytes=64)
-                a_operands[b] = (a_codes, a_scales)
-            a_codes, a_scales = a_operands[b]
-            ga = work.tile([P, QB, P, PACK], BF16, align_bytes=64)
-            for half in range(QB // 2):
-                aT = psum.tile([P, 2, PACK, P], BF16, tag="misc")
-                for j in range(2):
-                    for t in range(PACK):
-                        nc.tensor.transpose(aT[:, j, t, :], a_sb[:, t, 2 * half + j, :], ident[:])
-                nc.scalar.copy(out=ga[:, 2 * half : 2 * half + 2], in_=aT[:].rearrange("p j t q -> p j q t"))
-            nc.vector.quantize_mx(
-                out=a_codes[:, g, :].bitcast(FP8X4),
-                scales=a_scales[:, g, :],
-                in_=ga[:].rearrange("p c q t -> p (c q t)"),
-            )
-
-        def project(b):
-            a_codes, a_scales = a_operands[b]
-            for tb in range(QB):
-                out_sb = work.tile([P, D], F32, bufs=3)
-                for nh in range(D // BANK):
-                    acc = psum.tile([P, BANK], F32, tag="s_a" if nh == 0 else "s_b")
-                    n_cols = slice(nh * BANK, (nh + 1) * BANK)
-                    for g in range(GROUPS):
-                        nc.tensor.matmul_mx(
-                            out=acc[:],
-                            lhsT=a_codes[:, g, tb * P : (tb + 1) * P].bitcast(FP8X4),
-                            lhsT_scale=a_scales[:, g, tb * P : (tb + 1) * P],
-                            rhs=w_codes[:, g, n_cols].bitcast(FP8X4),
-                            rhs_scale=w_scales[:, g, n_cols],
-                            start=(g == 0),
-                            stop=(g == GROUPS - 1),
-                        )
-                    nc.vector.tensor_tensor(out=out_sb[:, n_cols], in0=acc[:], in1=bias[:, n_cols], op=ALU.add)
-                nc.gpsimd.dma_start(out=out[b, tb * P : (tb + 1) * P, :], in_=out_sb[:])
-
-        W_PIECES = GROUPS * (D // P // 2)
-        for step in range(N_HEADS + 3):
-            done = step - 3
-            if 0 <= done:
-                attend(done)
-                if done % PACK == PACK - 1:
-                    quantise_a(done // H, (done % H) // PACK)
-                if done % H == H - 1:
-                    project(done // H)
-            if 0 <= step - 2 < N_HEADS:
-                quantise_e(step - 2)
-            if 0 <= step - 1 < N_HEADS:
-                scores(step - 1)
-            if step < N_HEADS:
-                prepare_head(step)
-            if step < W_PIECES:
-                prepare_w(step)
+        LAST_STEP = N_HEADS + 2 + 9 + 1
+        for i in range(-2, LAST_STEP):
+            f = i - 2
+            tile_now = f - 9
+            if live(i):
+                add_mask(i, 0)
+                add_mask(i, 1)
+                scores_last_bank(i)
+                row_min(i, 3)
+                row_min(i, 2)
+                row_min(i, 0)
+                add_mask(i, 2)
+                row_min(i, 1)
+                exponentials(i)
+            if live(i + 2):
+                if i % 2 == 0 and (i + 2) // 2 + LOAD_AHEAD < N_PAIRS:
+                    load_pair((i + 2) // 2 + LOAD_AHEAD)
+                transpose_qk(i + 2)
+                copy_qk(i + 2)
+            if live(i + 1):
+                scores_first_banks(i + 1)
+            if 0 <= tile_now - 1 < B * OUT_TILES:
+                add_bias_and_store((tile_now - 1) // OUT_TILES, (tile_now - 1) % OUT_TILES)
+            if live(i - 1):
+                quantise_e(i - 1)
+            if live(i):
+                transpose_e(i)
+                regroup_e(i)
+            if live(f):
+                normalise(f)
+            if live(i - 1):
+                attend(i - 1)
+            if live(i + 2) and i % 2 == 0:
+                quantise_v((i + 2) // 2)
+            if 0 <= tile_now < B * OUT_TILES:
+                project(tile_now // OUT_TILES, tile_now % OUT_TILES)
+            if live(f) and f % PACK == PACK - 1:
+                regroup_a(f // H, (f % H) // PACK, 0)
+            if live(f - 1) and f % PACK == 0:
+                regroup_a((f - 1) // H, ((f - 1) % H) // PACK, 1)
+                quantise_a((f - 1) // H, ((f - 1) % H) // PACK)
+            if 0 <= i < W_PIECES:
+                prepare_w(i)

@@ -20,7 +20,6 @@ BANK = 512
 QB = S // P
 GROUPS = H // PACK
 N_HEADS = B * H
-N_PAIRS = N_HEADS // 2
 SCALE = 1.0 / math.sqrt(HD)
 FAR = 1.0e30
 
@@ -31,22 +30,11 @@ SEG_START = {3: 0, 2: 512, 0: 896, 1: 1024}
 SEG_COLS = 1280
 SEG_BLOCKS = SEG_COLS // P
 LOAD_AHEAD = 3
-W_PIECES = GROUPS * (D // P // 2)
-OUT_TILES = QB * (D // BANK)
-
-
-def seg(qi):
-    return slice(SEG_START[qi], SEG_START[qi] + (qi + 1) * P)
-
-
-def live(i):
-    return 0 <= i < N_HEADS
 
 
 def tile_alibiattention_pa_kernel(tc, q, k, v, w_out, b_out, out):
     nc = tc.nc
     with ExitStack() as ctx:
-        ctx.enter_context(tc.manual_schedule())
         const = ctx.enter_context(tc.tile_pool(name="const", bufs=1))
         loads = ctx.enter_context(tc.tile_pool(name="loads", bufs=LOAD_AHEAD + 2))
         work = ctx.enter_context(tc.tile_pool(name="work", bufs=2))
@@ -64,36 +52,37 @@ def tile_alibiattention_pa_kernel(tc, q, k, v, w_out, b_out, out):
                 nc.sync.dma_start(out=dst[:], in_=src[b, h0 : h0 + 2].rearrange("h (t p) d -> p h t d", p=P))
             pair_tiles[pair] = (q_sb, k_sb, v_sb)
 
-        load_pair(0)
-        load_pair(1)
+        for pair in range(LOAD_AHEAD):
+            load_pair(pair)
+
         w_sb = const.tile([P, D // P, D], BF16)
-        nc.sync.dma_start(out=w_sb[:], in_=w_out.rearrange("(nb p) f -> p nb f", p=P))
+        nc.scalar.dma_start(out=w_sb[:], in_=w_out.rearrange("(nb p) f -> p nb f", p=P))
         bias = const.tile([P, D], BF16)
-        nc.sync.dma_start(out=bias[:], in_=b_out.partition_broadcast(P))
-        load_pair(2)
+        nc.scalar.dma_start(out=bias[:], in_=b_out.partition_broadcast(P))
 
         ident = const.tile([P, P], BF16)
         make_identity(nc, ident[:])
 
-        negmask = const.tile([P, SEG_COLS], F32)
+        ident_f32 = const.tile([P, P], F32)
+        make_identity(nc, ident_f32[:])
+        maskT = const.tile([P, QB, P], F32)
         nc.gpsimd.iota(
-            negmask[:, 0:S],
-            pattern=[[-1, S]],
-            base=S - P,
+            maskT[:],
+            pattern=[[-P, QB], [-1, P]],
+            base=0,
             channel_multiplier=1,
             allow_small_or_imprecise_dtypes=True,
         )
         nc.gpsimd.affine_select(
-            out=negmask[:, 0:S],
-            in_=negmask[:, 0:S],
-            pattern=[[-1, S]],
+            out=maskT[:, 0, :],
+            in_=maskT[:, 0, :],
+            pattern=[[1, P]],
             compare_op=ALU.is_ge,
-            fill=FAR,
-            base=S - P,
-            channel_multiplier=1,
+            fill=-FAR,
+            base=0,
+            channel_multiplier=-1,
         )
-        for qi in (2, 0, 1):
-            nc.vector.tensor_copy(out=negmask[:, seg(qi)], in_=negmask[:, S - (qi + 1) * P : S])
+        nc.vector.tensor_scalar_mul(out=maskT[:], in0=maskT[:], scalar1=math.sqrt(HD))
 
         grouped_e = []
         for parity in range(2):
@@ -104,230 +93,16 @@ def tile_alibiattention_pa_kernel(tc, q, k, v, w_out, b_out, out):
         w_codes = const.tile([P, GROUPS, D], U32, align_bytes=64)
         w_scales = const.tile([P, GROUPS, D], U8, align_bytes=64)
 
-        qkT_banks = {}
-        qkT_tiles = {}
-        score_banks = {}
-        x_tiles = {}
-        e_tiles = {}
-        rowsums = {}
-        eT_banks = {}
-        e_operands = {}
+        transposed = {}
         v_operands = {}
-        o_banks = {}
+        probs = {}
+        e_operands = {}
         a_tiles = {}
-        ga_tiles = {}
         a_operands = {}
-        acc_banks = {}
-
-        def transpose_qk(i):
-            q_sb, k_sb, v_sb = pair_tiles[i // 2]
-            qkT_ps = psum.tile([P, 2, S], BF16, tag="qkT")
-            for which, src in enumerate((q_sb, k_sb)):
-                for t in range(QB):
-                    nc.tensor.transpose(qkT_ps[:, which, t * P : (t + 1) * P], src[:, i % 2, t, :], ident[:])
-            qkT_banks[i] = qkT_ps
-
-        def score_block(i, qi, bank):
-            n = (qi + 1) * P
-            col = SEG_START[qi] % BANK
-            qkT = qkT_tiles[i]
-            nc.tensor.matmul(
-                out=bank[:, col : col + n],
-                lhsT=qkT[:, 0, qi * P : (qi + 1) * P],
-                rhs=qkT[:, 1, 0:n],
-                start=True,
-                stop=True,
-            )
-
-        def scores_first_banks(i):
-            s_a = psum.tile([P, BANK], F32, tag="s_a")
-            s_b = psum.tile([P, BANK], F32, tag="s_b")
-            score_block(i, 3, s_a)
-            score_block(i, 2, s_b)
-            score_block(i, 0, s_b)
-            score_banks[(i, 0)] = s_a
-            score_banks[(i, 1)] = s_b
-
-        def scores_last_bank(i):
-            s_c = psum.tile([P, BANK], F32, tag="s_a")
-            score_block(i, 1, s_c)
-            score_banks[(i, 2)] = s_c
-
-        def transpose_e(i):
-            e_sb = e_tiles[i]
-            eT_x = psum.tile([P, 8, P], BF16, tag="eT_x")
-            eT_y = psum.tile([P, SEG_BLOCKS - 8, P], BF16, tag="eT_y")
-            for block in range(SEG_BLOCKS):
-                dst = eT_x[:, block, :] if block < 8 else eT_y[:, block - 8, :]
-                nc.tensor.transpose(dst, e_sb[:, block * P : (block + 1) * P], ident[:])
-            eT_banks[i] = (eT_x, eT_y)
-
-        def attend(i):
-            e_codes, e_scales = e_operands[i]
-            v_codes, v_scales = v_operands[i // 2]
-            o_ps = psum.tile([P, QB, HD], F32, tag="o")
-            for qi in range(QB):
-                cols = slice(qi * P, (qi + 1) * P)
-                nc.tensor.matmul_mx(
-                    out=o_ps[:, qi, :],
-                    lhsT=e_codes[:, cols].bitcast(FP8X4),
-                    lhsT_scale=e_scales[:, cols],
-                    rhs=v_codes[:, i % 2, :].bitcast(FP8X4),
-                    rhs_scale=v_scales[:, i % 2, :],
-                    start=True,
-                    stop=True,
-                )
-            o_banks[i] = o_ps
-
-        def project(b, r):
-            tb, nh = r // (D // BANK), r % (D // BANK)
-            a_codes, a_scales = a_operands[b]
-            acc = psum.tile([P, BANK], F32, tag="misc", bufs=2)
-            for g in range(GROUPS):
-                nc.tensor.matmul_mx(
-                    out=acc[:],
-                    lhsT=a_codes[:, g, tb * P : (tb + 1) * P].bitcast(FP8X4),
-                    lhsT_scale=a_scales[:, g, tb * P : (tb + 1) * P],
-                    rhs=w_codes[:, g, nh * BANK : (nh + 1) * BANK].bitcast(FP8X4),
-                    rhs_scale=w_scales[:, g, nh * BANK : (nh + 1) * BANK],
-                    start=(g == 0),
-                    stop=(g == GROUPS - 1),
-                )
-            acc_banks[(b, r)] = acc
-
-        def copy_qk(i):
-            qkT = work.tile([P, 2, S], BF16)
-            nc.scalar.copy(out=qkT[:], in_=qkT_banks[i][:])
-            qkT_tiles[i] = qkT
-
-        def add_mask(i, bank):
-            if bank == 0:
-                x_new = work.tile([P, SEG_COLS], F32)
-                negmax_new = work.tile([P, QB], F32)
-                x_tiles[i] = (x_new, negmax_new)
-            x = x_tiles[i][0]
-            width = min(BANK, SEG_COLS - bank * BANK)
-            cols = slice(bank * BANK, bank * BANK + width)
-            nc.vector.scalar_tensor_tensor(
-                out=x[:, cols],
-                in0=score_banks[(i, bank)][:, 0:width],
-                scalar=-SCALE,
-                in1=negmask[:, cols],
-                op0=ALU.mult,
-                op1=ALU.add,
-            )
-
-        def row_min(i, qi):
-            x, negmax = x_tiles[i]
-            nc.vector.tensor_scalar(
-                out=x[:, seg(qi)],
-                in0=x[:, seg(qi)],
-                scalar1=1.0,
-                scalar2=None,
-                op0=ALU.mult,
-                op1=ALU.min,
-                accum_out=negmax[:, qi : qi + 1],
-            )
-
-        def exponentials(i):
-            x, negmax = x_tiles[i]
-            rowsum = keep.tile([P, QB], F32)
-            e_sb = work.tile([P, SEG_COLS], BF16)
-            for qi in SEG_ORDER:
-                nc.scalar.activation(
-                    out=e_sb[:, seg(qi)],
-                    in_=x[:, seg(qi)],
-                    func=ACT.Exp,
-                    scale=-1.0,
-                    bias=negmax[:, qi : qi + 1],
-                    accum_out=rowsum[:, qi : qi + 1],
-                )
-            e_tiles[i] = e_sb
-            rowsums[i] = rowsum
-
-        def regroup_e(i):
-            eT_x, eT_y = eT_banks[i]
-            ge = grouped_e[i % 2]
-            for qi in SEG_ORDER:
-                first = SEG_START[qi] // P
-                src = eT_x[:, first : first + qi + 1, :] if first < 8 else eT_y[:, first - 8 : first - 8 + qi + 1, :]
-                nc.scalar.copy(out=ge[:, qi * P : (qi + 1) * P, 0 : qi + 1], in_=src.rearrange("p t q -> p q t"))
-
-        def quantise_e(i):
-            e_codes = work.tile([P, S], U32, align_bytes=64)
-            e_scales = work.tile([P, S], U8, align_bytes=64)
-            nc.vector.quantize_mx(
-                out=e_codes[:].bitcast(FP8X4),
-                scales=e_scales[:],
-                in_=grouped_e[i % 2][:].rearrange("p q t -> p (q t)"),
-            )
-            e_operands[i] = (e_codes, e_scales)
-
-        def quantise_v(pair):
-            v_sb = pair_tiles[pair][2]
-            gv = work.tile([P, 2, HD, PACK], BF16, align_bytes=64)
-            for j in range(2):
-                nc.vector.tensor_copy(
-                    out=gv[:, j].rearrange("p (c i) t -> p c t i", i=4),
-                    in_=v_sb[:, j].rearrange("p t (c i) -> p c t i", i=4),
-                )
-            v_codes = keep.tile([P, 2, HD], U32, align_bytes=64)
-            v_scales = keep.tile([P, 2, HD], U8, align_bytes=64)
-            nc.vector.quantize_mx(
-                out=v_codes[:].rearrange("p j d -> p (j d)").bitcast(FP8X4),
-                scales=v_scales[:].rearrange("p j d -> p (j d)"),
-                in_=gv[:].rearrange("p j d t -> p (j d t)"),
-            )
-            v_operands[pair] = (v_codes, v_scales)
-
-        def normalise(i):
-            b, g, t = i // H, (i % H) // PACK, i % PACK
-            rinv = work.tile([P, QB], F32)
-            nc.vector.reciprocal(out=rinv[:], in_=rowsums[i][:])
-            if t == 0:
-                a_new = work.tile([P, PACK, QB, HD], BF16)
-                a_tiles[(b, g)] = a_new
-            nc.vector.tensor_tensor(
-                out=a_tiles[(b, g)][:, t],
-                in0=o_banks[i][:],
-                in1=rinv[:].unsqueeze(2).to_broadcast([P, QB, HD]),
-                op=ALU.mult,
-            )
-
-        def regroup_a(b, g, half):
-            if half == 0:
-                ga_new = work.tile([P, QB, P, PACK], BF16, align_bytes=64)
-                ga_tiles[(b, g)] = ga_new
-            aT = psum.tile([P, 2, PACK, P], BF16, tag="misc", bufs=2)
-            for j in range(2):
-                for t in range(PACK):
-                    nc.tensor.transpose(aT[:, j, t, :], a_tiles[(b, g)][:, t, 2 * half + j, :], ident[:])
-            nc.scalar.copy(
-                out=ga_tiles[(b, g)][:, 2 * half : 2 * half + 2], in_=aT[:].rearrange("p j t q -> p j q t")
-            )
-
-        def quantise_a(b, g):
-            if g == 0:
-                a_codes_new = work.tile([P, GROUPS, S], U32, align_bytes=64)
-                a_scales_new = work.tile([P, GROUPS, S], U8, align_bytes=64)
-                a_operands[b] = (a_codes_new, a_scales_new)
-            a_codes, a_scales = a_operands[b]
-            nc.vector.quantize_mx(
-                out=a_codes[:, g, :].bitcast(FP8X4),
-                scales=a_scales[:, g, :],
-                in_=ga_tiles[(b, g)][:].rearrange("p c q t -> p (c q t)"),
-            )
-
-        def add_bias_and_store(b, r):
-            tb, nh = r // (D // BANK), r % (D // BANK)
-            n_cols = slice(nh * BANK, (nh + 1) * BANK)
-            out_sb = work.tile([P, BANK], F32, bufs=3)
-            nc.vector.tensor_tensor(out=out_sb[:], in0=acc_banks[(b, r)][:], in1=bias[:, n_cols], op=ALU.add)
-            nc.gpsimd.dma_start(out=out[b, tb * P : (tb + 1) * P, n_cols], in_=out_sb[:])
 
         def prepare_w(piece):
             g, nb0 = piece // (D // P // 2), 2 * (piece % (D // P // 2))
-            wT = psum.tile([P, 2, PACK, P], BF16, tag="misc", bufs=2)
+            wT = psum.tile([P, 2, PACK, P], BF16, tag="misc")
             for j in range(2):
                 for t in range(PACK):
                     f0 = (PACK * g + t) * P
@@ -341,46 +116,183 @@ def tile_alibiattention_pa_kernel(tc, q, k, v, w_out, b_out, out):
                 in_=gw[:].rearrange("p j n t -> p (j n t)"),
             )
 
-        LAST_STEP = N_HEADS + 2 + 9 + 1
-        for i in range(-2, LAST_STEP):
-            f = i - 2
-            tile_now = f - 9
-            if live(i):
-                add_mask(i, 0)
-                add_mask(i, 1)
-                scores_last_bank(i)
-                row_min(i, 3)
-                row_min(i, 2)
-                row_min(i, 0)
-                add_mask(i, 2)
-                row_min(i, 1)
-                exponentials(i)
-            if live(i + 2):
-                if i % 2 == 0 and (i + 2) // 2 + LOAD_AHEAD < N_PAIRS:
-                    load_pair((i + 2) // 2 + LOAD_AHEAD)
-                transpose_qk(i + 2)
-                copy_qk(i + 2)
-            if live(i + 1):
-                scores_first_banks(i + 1)
-            if 0 <= tile_now - 1 < B * OUT_TILES:
-                add_bias_and_store((tile_now - 1) // OUT_TILES, (tile_now - 1) % OUT_TILES)
-            if live(i - 1):
-                quantise_e(i - 1)
-            if live(i):
-                transpose_e(i)
-                regroup_e(i)
-            if live(f):
-                normalise(f)
-            if live(i - 1):
-                attend(i - 1)
-            if live(i + 2) and i % 2 == 0:
-                quantise_v((i + 2) // 2)
-            if 0 <= tile_now < B * OUT_TILES:
-                project(tile_now // OUT_TILES, tile_now % OUT_TILES)
-            if live(f) and f % PACK == PACK - 1:
-                regroup_a(f // H, (f % H) // PACK, 0)
-            if live(f - 1) and f % PACK == 0:
-                regroup_a((f - 1) // H, ((f - 1) % H) // PACK, 1)
-                quantise_a((f - 1) // H, ((f - 1) % H) // PACK)
-            if 0 <= i < W_PIECES:
-                prepare_w(i)
+        def prepare_head(i):
+            pair, j = i // 2, i % 2
+            if j == 0 and pair + LOAD_AHEAD < N_HEADS // 2:
+                load_pair(pair + LOAD_AHEAD)
+            q_sb, k_sb, v_sb = pair_tiles[pair]
+            qkT_ps = psum.tile([P, 2, S], BF16, tag="qkT")
+            for which, src in enumerate((q_sb, k_sb)):
+                for t in range(QB):
+                    nc.tensor.transpose(qkT_ps[:, which, t * P : (t + 1) * P], src[:, j, t, :], ident[:])
+            qkT = work.tile([P, 2, S], BF16)
+            nc.scalar.copy(out=qkT[:], in_=qkT_ps[:])
+            transposed[i] = qkT
+            if j == 0:
+                gv = work.tile([P, 2, HD, PACK], BF16, align_bytes=64)
+                for jj in range(2):
+                    nc.vector.tensor_copy(out=gv[:, jj], in_=v_sb[:, jj].rearrange("p t d -> p d t"))
+                v_codes = keep.tile([P, 2, HD], U32, align_bytes=64)
+                v_scales = keep.tile([P, 2, HD], U8, align_bytes=64)
+                nc.vector.quantize_mx(
+                    out=v_codes[:].rearrange("p j d -> p (j d)").bitcast(FP8X4),
+                    scales=v_scales[:].rearrange("p j d -> p (j d)"),
+                    in_=gv[:].rearrange("p j d t -> p (j d t)"),
+                )
+                v_operands[pair] = (v_codes, v_scales)
+
+        def scores(i):
+            qkT = transposed[i]
+            s_a = psum.tile([P, BANK], F32, tag="s_a")
+            s_b = psum.tile([P, BANK], F32, tag="s_b")
+            s_c = psum.tile([P, BANK], F32, tag="s_c")
+            banks = (s_a, s_b, s_c)
+            for qi in SEG_ORDER:
+                bank = banks[SEG_START[qi] // BANK]
+                for kb in range(qi + 1):
+                    col = SEG_START[qi] % BANK + kb * P
+                    nc.tensor.matmul(
+                        out=bank[:, col : col + P],
+                        lhsT=maskT[:, qi - kb, :],
+                        rhs=ident_f32[:],
+                        is_transpose=True,
+                        start=True,
+                        stop=False,
+                    )
+                    nc.tensor.matmul(
+                        out=bank[:, col : col + P],
+                        lhsT=qkT[:, 0, qi * P : (qi + 1) * P],
+                        rhs=qkT[:, 1, kb * P : (kb + 1) * P],
+                        start=False,
+                        stop=True,
+                    )
+            x = work.tile([P, SEG_COLS], F32)
+            negmax = work.tile([P, QB], F32)
+            rowsum = keep.tile([P, QB], F32)
+            e_sb = keep.tile([P, SEG_COLS], BF16)
+            for qi in SEG_ORDER:
+                cols = slice(SEG_START[qi], SEG_START[qi] + (qi + 1) * P)
+                col = SEG_START[qi] % BANK
+                nc.vector.tensor_scalar(
+                    out=x[:, cols],
+                    in0=banks[SEG_START[qi] // BANK][:, col : col + (qi + 1) * P],
+                    scalar1=-SCALE,
+                    scalar2=None,
+                    op0=ALU.mult,
+                    op1=ALU.min,
+                    accum_out=negmax[:, qi : qi + 1],
+                )
+                nc.scalar.activation(
+                    out=e_sb[:, cols],
+                    in_=x[:, cols],
+                    func=ACT.Exp,
+                    scale=-1.0,
+                    bias=negmax[:, qi : qi + 1],
+                    accum_out=rowsum[:, qi : qi + 1],
+                )
+            probs[i] = (e_sb, rowsum)
+
+        def quantise_e(i):
+            e_sb = probs[i][0]
+            eT_x = psum.tile([P, 8, P], BF16, tag="eT_x")
+            eT_y = psum.tile([P, SEG_BLOCKS - 8, P], BF16, tag="eT_y")
+            for block in range(SEG_BLOCKS):
+                dst = eT_x[:, block, :] if block < 8 else eT_y[:, block - 8, :]
+                nc.tensor.transpose(dst, e_sb[:, block * P : (block + 1) * P], ident[:])
+            ge = grouped_e[i % 2]
+            for qi in SEG_ORDER:
+                first = SEG_START[qi] // P
+                src = eT_x[:, first : first + qi + 1, :] if first < 8 else eT_y[:, first - 8 : first - 8 + qi + 1, :]
+                nc.scalar.copy(out=ge[:, qi * P : (qi + 1) * P, 0 : qi + 1], in_=src.rearrange("p t q -> p q t"))
+            e_codes = keep.tile([P, S], U32, align_bytes=64)
+            e_scales = keep.tile([P, S], U8, align_bytes=64)
+            nc.vector.quantize_mx(
+                out=e_codes[:].bitcast(FP8X4), scales=e_scales[:], in_=ge[:].rearrange("p q t -> p (q t)")
+            )
+            e_operands[i] = (e_codes, e_scales)
+
+        def attend(i):
+            b, h = i // H, i % H
+            g, t = h // PACK, h % PACK
+            e_codes, e_scales = e_operands[i]
+            v_codes, v_scales = v_operands[i // 2]
+            rowsum = probs[i][1]
+            o_ps = psum.tile([P, QB, HD], F32, tag="o")
+            for qi in range(QB):
+                cols = slice(qi * P, (qi + 1) * P)
+                nc.tensor.matmul_mx(
+                    out=o_ps[:, qi, :],
+                    lhsT=e_codes[:, cols].bitcast(FP8X4),
+                    lhsT_scale=e_scales[:, cols],
+                    rhs=v_codes[:, i % 2, :].bitcast(FP8X4),
+                    rhs_scale=v_scales[:, i % 2, :],
+                    start=True,
+                    stop=True,
+                )
+            rinv = work.tile([P, QB], F32)
+            nc.vector.reciprocal(out=rinv[:], in_=rowsum[:])
+            if t == 0:
+                a_new = work.tile([P, PACK, QB, HD], BF16)
+                a_tiles[(b, g)] = a_new
+            a_sb = a_tiles[(b, g)]
+            nc.vector.tensor_tensor(
+                out=a_sb[:, t], in0=o_ps[:], in1=rinv[:].unsqueeze(2).to_broadcast([P, QB, HD]), op=ALU.mult
+            )
+
+        def quantise_a(b, g):
+            a_sb = a_tiles[(b, g)]
+            if g == 0:
+                a_codes = work.tile([P, GROUPS, S], U32, align_bytes=64)
+                a_scales = work.tile([P, GROUPS, S], U8, align_bytes=64)
+                a_operands[b] = (a_codes, a_scales)
+            a_codes, a_scales = a_operands[b]
+            ga = work.tile([P, QB, P, PACK], BF16, align_bytes=64)
+            for half in range(QB // 2):
+                aT = psum.tile([P, 2, PACK, P], BF16, tag="misc")
+                for j in range(2):
+                    for t in range(PACK):
+                        nc.tensor.transpose(aT[:, j, t, :], a_sb[:, t, 2 * half + j, :], ident[:])
+                nc.scalar.copy(out=ga[:, 2 * half : 2 * half + 2], in_=aT[:].rearrange("p j t q -> p j q t"))
+            nc.vector.quantize_mx(
+                out=a_codes[:, g, :].bitcast(FP8X4),
+                scales=a_scales[:, g, :],
+                in_=ga[:].rearrange("p c q t -> p (c q t)"),
+            )
+
+        def project(b):
+            a_codes, a_scales = a_operands[b]
+            for tb in range(QB):
+                out_sb = work.tile([P, D], F32, bufs=3)
+                for nh in range(D // BANK):
+                    acc = psum.tile([P, BANK], F32, tag="s_a" if nh == 0 else "s_b")
+                    n_cols = slice(nh * BANK, (nh + 1) * BANK)
+                    for g in range(GROUPS):
+                        nc.tensor.matmul_mx(
+                            out=acc[:],
+                            lhsT=a_codes[:, g, tb * P : (tb + 1) * P].bitcast(FP8X4),
+                            lhsT_scale=a_scales[:, g, tb * P : (tb + 1) * P],
+                            rhs=w_codes[:, g, n_cols].bitcast(FP8X4),
+                            rhs_scale=w_scales[:, g, n_cols],
+                            start=(g == 0),
+                            stop=(g == GROUPS - 1),
+                        )
+                    nc.vector.tensor_tensor(out=out_sb[:, n_cols], in0=acc[:], in1=bias[:, n_cols], op=ALU.add)
+                nc.gpsimd.dma_start(out=out[b, tb * P : (tb + 1) * P, :], in_=out_sb[:])
+
+        W_PIECES = GROUPS * (D // P // 2)
+        for step in range(N_HEADS + 3):
+            done = step - 3
+            if 0 <= done:
+                attend(done)
+                if done % PACK == PACK - 1:
+                    quantise_a(done // H, (done % H) // PACK)
+                if done % H == H - 1:
+                    project(done // H)
+            if 0 <= step - 2 < N_HEADS:
+                quantise_e(step - 2)
+            if 0 <= step - 1 < N_HEADS:
+                scores(step - 1)
+            if step < N_HEADS:
+                prepare_head(step)
+            if step < W_PIECES:
+                prepare_w(step)

@@ -20,6 +20,7 @@ BANK = 512
 QB = S // P
 GROUPS = H // PACK
 N_HEADS = B * H
+N_PAIRS = N_HEADS // 2
 SCALE = 1.0 / math.sqrt(HD)
 FAR = 1.0e30
 
@@ -28,17 +29,29 @@ FLOPS = 2 * (2 * B * H * S * S * HD) + 2 * B * S * D * D
 SEG_ORDER = (3, 2, 0, 1)
 SEG_START = {3: 0, 2: 512, 0: 896, 1: 1024}
 SEG_COLS = 1280
-SEG_BLOCKS = SEG_COLS // P
+X_BLOCKS = 8
 LOAD_AHEAD = 3
+W_PIECES = GROUPS * (D // P // 2)
+N_HALVES = D // BANK
+N_TILES = B * QB * N_HALVES
+N_QUARTERS = B * GROUPS * QB
+
+
+def seg(qi):
+    return slice(SEG_START[qi], SEG_START[qi] + (qi + 1) * P)
+
+
+def live(i):
+    return 0 <= i < N_HEADS
 
 
 def tile_alibiattention_pa_kernel(tc, q, k, v, w_out, b_out, out):
     nc = tc.nc
     with ExitStack() as ctx:
+        ctx.enter_context(tc.manual_schedule())
         const = ctx.enter_context(tc.tile_pool(name="const", bufs=1))
-        loads = ctx.enter_context(tc.tile_pool(name="loads", bufs=LOAD_AHEAD + 2))
-        work = ctx.enter_context(tc.tile_pool(name="work", bufs=2))
-        keep = ctx.enter_context(tc.tile_pool(name="keep", bufs=4))
+        loads = ctx.enter_context(tc.tile_pool(name="loads", bufs=LOAD_AHEAD + 3))
+        work = ctx.enter_context(tc.tile_pool(name="work", bufs=3))
         psum = ctx.enter_context(tc.psum_pool(name="psum", bufs=1))
 
         pair_tiles = {}
@@ -52,19 +65,19 @@ def tile_alibiattention_pa_kernel(tc, q, k, v, w_out, b_out, out):
                 nc.sync.dma_start(out=dst[:], in_=src[b, h0 : h0 + 2].rearrange("h (t p) d -> p h t d", p=P))
             pair_tiles[pair] = (q_sb, k_sb, v_sb)
 
-        for pair in range(LOAD_AHEAD):
-            load_pair(pair)
-
+        load_pair(0)
+        load_pair(1)
         w_sb = const.tile([P, D // P, D], BF16)
-        nc.scalar.dma_start(out=w_sb[:], in_=w_out.rearrange("(nb p) f -> p nb f", p=P))
+        nc.sync.dma_start(out=w_sb[:], in_=w_out.rearrange("(nb p) f -> p nb f", p=P))
         bias = const.tile([P, D], BF16)
-        nc.scalar.dma_start(out=bias[:], in_=b_out.partition_broadcast(P))
+        nc.sync.dma_start(out=bias[:], in_=b_out.partition_broadcast(P))
+        load_pair(2)
 
         ident = const.tile([P, P], BF16)
         make_identity(nc, ident[:])
-
         ident_f32 = const.tile([P, P], F32)
         make_identity(nc, ident_f32[:])
+
         maskT = const.tile([P, QB, P], F32)
         nc.gpsimd.iota(
             maskT[:],
@@ -93,130 +106,86 @@ def tile_alibiattention_pa_kernel(tc, q, k, v, w_out, b_out, out):
         w_codes = const.tile([P, GROUPS, D], U32, align_bytes=64)
         w_scales = const.tile([P, GROUPS, D], U8, align_bytes=64)
 
-        transposed = {}
-        v_operands = {}
-        probs = {}
+        qkT_banks = {}
+        qkT_tiles = {}
+        score_banks = {}
+        x_tiles = {}
+        e_tiles = {}
+        rowsums = {}
+        eT_banks = {}
         e_operands = {}
+        gv_tiles = {}
+        v_operands = {}
+        o_banks = {}
         a_tiles = {}
+        aT_banks = {}
+        ga_tiles = {}
         a_operands = {}
+        wT_banks = {}
+        gw_tiles = {}
+        acc_banks = {}
 
-        def prepare_w(piece):
+        def transpose_qk(i):
+            q_sb, k_sb, v_sb = pair_tiles[i // 2]
+            qkT_ps = psum.tile([P, 2, S], BF16, tag="qkT")
+            for which, src in enumerate((q_sb, k_sb)):
+                for t in range(QB):
+                    nc.tensor.transpose(qkT_ps[:, which, t * P : (t + 1) * P], src[:, i % 2, t, :], ident[:])
+            qkT_banks[i] = qkT_ps
+
+        def new_score_bank(i, tag, blocks):
+            bank = psum.tile([P, BANK], F32, tag=tag)
+            for qi in blocks:
+                score_banks[(i, qi)] = bank
+
+        def score_blocks(i, qi):
+            qkT = qkT_tiles[i]
+            bank = score_banks[(i, qi)]
+            for kb in range(qi + 1):
+                col = SEG_START[qi] % BANK + kb * P
+                nc.tensor.matmul(
+                    out=bank[:, col : col + P],
+                    lhsT=maskT[:, qi - kb, :],
+                    rhs=ident_f32[:],
+                    is_transpose=True,
+                    start=True,
+                    stop=False,
+                )
+                nc.tensor.matmul(
+                    out=bank[:, col : col + P],
+                    lhsT=qkT[:, 0, qi * P : (qi + 1) * P],
+                    rhs=qkT[:, 1, kb * P : (kb + 1) * P],
+                    start=False,
+                    stop=True,
+                )
+
+        def transpose_e(i, bank, first_block, blocks):
+            e_sb = e_tiles[i]
+            for qi in blocks:
+                at = SEG_START[qi] // P - first_block
+                for t in range(qi + 1):
+                    col = SEG_START[qi] + t * P
+                    nc.tensor.transpose(bank[:, at + t, :], e_sb[:, col : col + P], ident[:])
+                eT_banks[(i, qi)] = bank[:, at : at + qi + 1, :]
+
+        def transpose_a(quarter, bank):
+            group, qi = quarter // QB, quarter % QB
+            for t in range(PACK):
+                nc.tensor.transpose(bank[:, t, :], a_tiles[group][:, t, qi, :], ident[:])
+            aT_banks[quarter] = bank
+
+        def transpose_w(piece):
             g, nb0 = piece // (D // P // 2), 2 * (piece % (D // P // 2))
-            wT = psum.tile([P, 2, PACK, P], BF16, tag="misc")
+            wT = psum.tile([P, 2, PACK, P], BF16, tag="acc")
             for j in range(2):
                 for t in range(PACK):
                     f0 = (PACK * g + t) * P
                     nc.tensor.transpose(wT[:, j, t, :], w_sb[:, nb0 + j, f0 : f0 + P], ident[:])
-            gw = work.tile([P, 2, P, PACK], BF16, align_bytes=64)
-            nc.scalar.copy(out=gw[:], in_=wT[:].rearrange("p j t n -> p j n t"))
-            cols = slice(nb0 * P, (nb0 + 2) * P)
-            nc.vector.quantize_mx(
-                out=w_codes[:, g, cols].bitcast(FP8X4),
-                scales=w_scales[:, g, cols],
-                in_=gw[:].rearrange("p j n t -> p (j n t)"),
-            )
-
-        def prepare_head(i):
-            pair, j = i // 2, i % 2
-            if j == 0 and pair + LOAD_AHEAD < N_HEADS // 2:
-                load_pair(pair + LOAD_AHEAD)
-            q_sb, k_sb, v_sb = pair_tiles[pair]
-            qkT_ps = psum.tile([P, 2, S], BF16, tag="qkT")
-            for which, src in enumerate((q_sb, k_sb)):
-                for t in range(QB):
-                    nc.tensor.transpose(qkT_ps[:, which, t * P : (t + 1) * P], src[:, j, t, :], ident[:])
-            qkT = work.tile([P, 2, S], BF16)
-            nc.scalar.copy(out=qkT[:], in_=qkT_ps[:])
-            transposed[i] = qkT
-            if j == 0:
-                gv = work.tile([P, 2, HD, PACK], BF16, align_bytes=64)
-                for jj in range(2):
-                    nc.vector.tensor_copy(out=gv[:, jj], in_=v_sb[:, jj].rearrange("p t d -> p d t"))
-                v_codes = keep.tile([P, 2, HD], U32, align_bytes=64)
-                v_scales = keep.tile([P, 2, HD], U8, align_bytes=64)
-                nc.vector.quantize_mx(
-                    out=v_codes[:].rearrange("p j d -> p (j d)").bitcast(FP8X4),
-                    scales=v_scales[:].rearrange("p j d -> p (j d)"),
-                    in_=gv[:].rearrange("p j d t -> p (j d t)"),
-                )
-                v_operands[pair] = (v_codes, v_scales)
-
-        def scores(i):
-            qkT = transposed[i]
-            s_a = psum.tile([P, BANK], F32, tag="s_a")
-            s_b = psum.tile([P, BANK], F32, tag="s_b")
-            s_c = psum.tile([P, BANK], F32, tag="s_c")
-            banks = (s_a, s_b, s_c)
-            for qi in SEG_ORDER:
-                bank = banks[SEG_START[qi] // BANK]
-                for kb in range(qi + 1):
-                    col = SEG_START[qi] % BANK + kb * P
-                    nc.tensor.matmul(
-                        out=bank[:, col : col + P],
-                        lhsT=maskT[:, qi - kb, :],
-                        rhs=ident_f32[:],
-                        is_transpose=True,
-                        start=True,
-                        stop=False,
-                    )
-                    nc.tensor.matmul(
-                        out=bank[:, col : col + P],
-                        lhsT=qkT[:, 0, qi * P : (qi + 1) * P],
-                        rhs=qkT[:, 1, kb * P : (kb + 1) * P],
-                        start=False,
-                        stop=True,
-                    )
-            x = work.tile([P, SEG_COLS], F32)
-            negmax = work.tile([P, QB], F32)
-            rowsum = keep.tile([P, QB], F32)
-            e_sb = keep.tile([P, SEG_COLS], BF16)
-            for qi in SEG_ORDER:
-                cols = slice(SEG_START[qi], SEG_START[qi] + (qi + 1) * P)
-                col = SEG_START[qi] % BANK
-                nc.vector.tensor_scalar(
-                    out=x[:, cols],
-                    in0=banks[SEG_START[qi] // BANK][:, col : col + (qi + 1) * P],
-                    scalar1=-SCALE,
-                    scalar2=None,
-                    op0=ALU.mult,
-                    op1=ALU.min,
-                    accum_out=negmax[:, qi : qi + 1],
-                )
-                nc.scalar.activation(
-                    out=e_sb[:, cols],
-                    in_=x[:, cols],
-                    func=ACT.Exp,
-                    scale=-1.0,
-                    bias=negmax[:, qi : qi + 1],
-                    accum_out=rowsum[:, qi : qi + 1],
-                )
-            probs[i] = (e_sb, rowsum)
-
-        def quantise_e(i):
-            e_sb = probs[i][0]
-            eT_x = psum.tile([P, 8, P], BF16, tag="eT_x")
-            eT_y = psum.tile([P, SEG_BLOCKS - 8, P], BF16, tag="eT_y")
-            for block in range(SEG_BLOCKS):
-                dst = eT_x[:, block, :] if block < 8 else eT_y[:, block - 8, :]
-                nc.tensor.transpose(dst, e_sb[:, block * P : (block + 1) * P], ident[:])
-            ge = grouped_e[i % 2]
-            for qi in SEG_ORDER:
-                first = SEG_START[qi] // P
-                src = eT_x[:, first : first + qi + 1, :] if first < 8 else eT_y[:, first - 8 : first - 8 + qi + 1, :]
-                nc.scalar.copy(out=ge[:, qi * P : (qi + 1) * P, 0 : qi + 1], in_=src.rearrange("p t q -> p q t"))
-            e_codes = keep.tile([P, S], U32, align_bytes=64)
-            e_scales = keep.tile([P, S], U8, align_bytes=64)
-            nc.vector.quantize_mx(
-                out=e_codes[:].bitcast(FP8X4), scales=e_scales[:], in_=ge[:].rearrange("p q t -> p (q t)")
-            )
-            e_operands[i] = (e_codes, e_scales)
+            wT_banks[piece] = wT
 
         def attend(i):
-            b, h = i // H, i % H
-            g, t = h // PACK, h % PACK
             e_codes, e_scales = e_operands[i]
-            v_codes, v_scales = v_operands[i // 2]
-            rowsum = probs[i][1]
+            v_codes, v_scales = v_operands[i]
             o_ps = psum.tile([P, QB, HD], F32, tag="o")
             for qi in range(QB):
                 cols = slice(qi * P, (qi + 1) * P)
@@ -224,75 +193,223 @@ def tile_alibiattention_pa_kernel(tc, q, k, v, w_out, b_out, out):
                     out=o_ps[:, qi, :],
                     lhsT=e_codes[:, cols].bitcast(FP8X4),
                     lhsT_scale=e_scales[:, cols],
-                    rhs=v_codes[:, i % 2, :].bitcast(FP8X4),
-                    rhs_scale=v_scales[:, i % 2, :],
+                    rhs=v_codes[:].bitcast(FP8X4),
+                    rhs_scale=v_scales[:],
                     start=True,
                     stop=True,
                 )
+            o_banks[i] = o_ps
+
+        def project(r, tag):
+            b, tb, nh = r // (QB * N_HALVES), (r // N_HALVES) % QB, r % N_HALVES
+            a_codes, a_scales = a_operands[b]
+            acc = psum.tile([P, BANK], F32, tag=tag)
+            for g in range(GROUPS):
+                nc.tensor.matmul_mx(
+                    out=acc[:],
+                    lhsT=a_codes[:, g, tb * P : (tb + 1) * P].bitcast(FP8X4),
+                    lhsT_scale=a_scales[:, g, tb * P : (tb + 1) * P],
+                    rhs=w_codes[:, g, nh * BANK : (nh + 1) * BANK].bitcast(FP8X4),
+                    rhs_scale=w_scales[:, g, nh * BANK : (nh + 1) * BANK],
+                    start=(g == 0),
+                    stop=(g == GROUPS - 1),
+                )
+            acc_banks[r] = acc
+
+        def copy_qk(i):
+            qkT = work.tile([P, 2, S], BF16, bufs=4)
+            nc.scalar.copy(out=qkT[:], in_=qkT_banks[i][:])
+            qkT_tiles[i] = qkT
+
+        def scale_and_min(i, qi):
+            if qi == SEG_ORDER[0]:
+                x_new = work.tile([P, SEG_COLS], F32)
+                negmax_new = work.tile([P, QB], F32)
+                x_tiles[i] = (x_new, negmax_new)
+            x, negmax = x_tiles[i]
+            col = SEG_START[qi] % BANK
+            nc.vector.tensor_scalar(
+                out=x[:, seg(qi)],
+                in0=score_banks[(i, qi)][:, col : col + (qi + 1) * P],
+                scalar1=-SCALE,
+                scalar2=None,
+                op0=ALU.mult,
+                op1=ALU.min,
+                accum_out=negmax[:, qi : qi + 1],
+            )
+
+        def exponentials(i):
+            x, negmax = x_tiles[i]
+            rowsum = work.tile([P, QB], F32, bufs=6)
+            e_sb = work.tile([P, SEG_COLS], BF16)
+            for qi in SEG_ORDER:
+                nc.scalar.activation(
+                    out=e_sb[:, seg(qi)],
+                    in_=x[:, seg(qi)],
+                    func=ACT.Exp,
+                    scale=-1.0,
+                    bias=negmax[:, qi : qi + 1],
+                    accum_out=rowsum[:, qi : qi + 1],
+                )
+            e_tiles[i] = e_sb
+            rowsums[i] = rowsum
+
+        def regroup_e(i):
+            ge = grouped_e[i % 2]
+            for qi in SEG_ORDER:
+                nc.scalar.copy(
+                    out=ge[:, qi * P : (qi + 1) * P, 0 : qi + 1], in_=eT_banks[(i, qi)].rearrange("p t q -> p q t")
+                )
+
+        def quantise_e(i):
+            e_codes = work.tile([P, S], U32, align_bytes=64)
+            e_scales = work.tile([P, S], U8, align_bytes=64)
+            nc.vector.quantize_mx(
+                out=e_codes[:].bitcast(FP8X4),
+                scales=e_scales[:],
+                in_=grouped_e[i % 2][:].rearrange("p q t -> p (q t)"),
+            )
+            e_operands[i] = (e_codes, e_scales)
+
+        def regroup_v(i):
+            v_sb = pair_tiles[i // 2][2]
+            gv = work.tile([P, HD, PACK], BF16, align_bytes=64)
+            nc.vector.tensor_copy(
+                out=gv[:].rearrange("p (c i) t -> p c t i", i=4),
+                in_=v_sb[:, i % 2].rearrange("p t (c i) -> p c t i", i=4),
+            )
+            gv_tiles[i] = gv
+
+        def quantise_v(i):
+            gv = gv_tiles[i]
+            v_codes = work.tile([P, HD], U32, align_bytes=64, bufs=4)
+            v_scales = work.tile([P, HD], U8, align_bytes=64, bufs=4)
+            nc.vector.quantize_mx(
+                out=v_codes[:].bitcast(FP8X4), scales=v_scales[:], in_=gv[:].rearrange("p d t -> p (d t)")
+            )
+            v_operands[i] = (v_codes, v_scales)
+
+        def normalise(i):
+            group, t = i // PACK, i % PACK
             rinv = work.tile([P, QB], F32)
-            nc.vector.reciprocal(out=rinv[:], in_=rowsum[:])
+            nc.vector.reciprocal(out=rinv[:], in_=rowsums[i][:])
             if t == 0:
                 a_new = work.tile([P, PACK, QB, HD], BF16)
-                a_tiles[(b, g)] = a_new
-            a_sb = a_tiles[(b, g)]
+                a_tiles[group] = a_new
             nc.vector.tensor_tensor(
-                out=a_sb[:, t], in0=o_ps[:], in1=rinv[:].unsqueeze(2).to_broadcast([P, QB, HD]), op=ALU.mult
+                out=a_tiles[group][:, t],
+                in0=o_banks[i][:],
+                in1=rinv[:].unsqueeze(2).to_broadcast([P, QB, HD]),
+                op=ALU.mult,
             )
 
-        def quantise_a(b, g):
-            a_sb = a_tiles[(b, g)]
-            if g == 0:
-                a_codes = work.tile([P, GROUPS, S], U32, align_bytes=64)
-                a_scales = work.tile([P, GROUPS, S], U8, align_bytes=64)
-                a_operands[b] = (a_codes, a_scales)
+        def regroup_a(quarter):
+            ga = work.tile([P, P, PACK], BF16, align_bytes=64)
+            nc.scalar.copy(out=ga[:], in_=aT_banks[quarter].rearrange("p t q -> p q t"))
+            ga_tiles[quarter] = ga
+
+        def quantise_a(quarter):
+            group, qi = quarter // QB, quarter % QB
+            b, g = group // GROUPS, group % GROUPS
+            if g == 0 and qi == 0:
+                a_codes_new = work.tile([P, GROUPS, S], U32, align_bytes=64, bufs=2)
+                a_scales_new = work.tile([P, GROUPS, S], U8, align_bytes=64, bufs=2)
+                a_operands[b] = (a_codes_new, a_scales_new)
             a_codes, a_scales = a_operands[b]
-            ga = work.tile([P, QB, P, PACK], BF16, align_bytes=64)
-            for half in range(QB // 2):
-                aT = psum.tile([P, 2, PACK, P], BF16, tag="misc")
-                for j in range(2):
-                    for t in range(PACK):
-                        nc.tensor.transpose(aT[:, j, t, :], a_sb[:, t, 2 * half + j, :], ident[:])
-                nc.scalar.copy(out=ga[:, 2 * half : 2 * half + 2], in_=aT[:].rearrange("p j t q -> p j q t"))
+            cols = slice(qi * P, (qi + 1) * P)
             nc.vector.quantize_mx(
-                out=a_codes[:, g, :].bitcast(FP8X4),
-                scales=a_scales[:, g, :],
-                in_=ga[:].rearrange("p c q t -> p (c q t)"),
+                out=a_codes[:, g, cols].bitcast(FP8X4),
+                scales=a_scales[:, g, cols],
+                in_=ga_tiles[quarter][:].rearrange("p q t -> p (q t)"),
             )
 
-        def project(b):
-            a_codes, a_scales = a_operands[b]
-            for tb in range(QB):
-                out_sb = work.tile([P, D], F32, bufs=3)
-                for nh in range(D // BANK):
-                    acc = psum.tile([P, BANK], F32, tag="s_a" if nh == 0 else "s_b")
-                    n_cols = slice(nh * BANK, (nh + 1) * BANK)
-                    for g in range(GROUPS):
-                        nc.tensor.matmul_mx(
-                            out=acc[:],
-                            lhsT=a_codes[:, g, tb * P : (tb + 1) * P].bitcast(FP8X4),
-                            lhsT_scale=a_scales[:, g, tb * P : (tb + 1) * P],
-                            rhs=w_codes[:, g, n_cols].bitcast(FP8X4),
-                            rhs_scale=w_scales[:, g, n_cols],
-                            start=(g == 0),
-                            stop=(g == GROUPS - 1),
-                        )
-                    nc.vector.tensor_tensor(out=out_sb[:, n_cols], in0=acc[:], in1=bias[:, n_cols], op=ALU.add)
-                nc.gpsimd.dma_start(out=out[b, tb * P : (tb + 1) * P, :], in_=out_sb[:])
+        def regroup_w(piece):
+            gw = work.tile([P, 2, P, PACK], BF16, align_bytes=64)
+            src = wT_banks[piece][:].rearrange("p j t n -> p j n t")
+            if piece % 2 == 0:
+                nc.scalar.copy(out=gw[:], in_=src)
+            else:
+                nc.vector.tensor_copy(out=gw[:], in_=src)
+            gw_tiles[piece] = gw
 
-        W_PIECES = GROUPS * (D // P // 2)
-        for step in range(N_HEADS + 3):
-            done = step - 3
-            if 0 <= done:
-                attend(done)
-                if done % PACK == PACK - 1:
-                    quantise_a(done // H, (done % H) // PACK)
-                if done % H == H - 1:
-                    project(done // H)
-            if 0 <= step - 2 < N_HEADS:
-                quantise_e(step - 2)
-            if 0 <= step - 1 < N_HEADS:
-                scores(step - 1)
-            if step < N_HEADS:
-                prepare_head(step)
-            if step < W_PIECES:
-                prepare_w(step)
+        def quantise_w(piece):
+            g, nb0 = piece // (D // P // 2), 2 * (piece % (D // P // 2))
+            cols = slice(nb0 * P, (nb0 + 2) * P)
+            nc.vector.quantize_mx(
+                out=w_codes[:, g, cols].bitcast(FP8X4),
+                scales=w_scales[:, g, cols],
+                in_=gw_tiles[piece][:].rearrange("p j n t -> p (j n t)"),
+            )
+
+        def add_bias_and_store(r):
+            b, tb, nh = r // (QB * N_HALVES), (r // N_HALVES) % QB, r % N_HALVES
+            n_cols = slice(nh * BANK, (nh + 1) * BANK)
+            out_sb = work.tile([P, BANK], F32, bufs=4)
+            nc.vector.tensor_tensor(out=out_sb[:], in0=acc_banks[r][:], in1=bias[:, n_cols], op=ALU.add)
+            nc.gpsimd.dma_start(out=out[b, tb * P : (tb + 1) * P, n_cols], in_=out_sb[:])
+
+        A_LAG = PACK + 3
+        P_LAG = H + 5
+        for s in range(-3, N_TILES + P_LAG + 1):
+            quarter = s - A_LAG
+            tile_now = s - P_LAG
+            if live(s + 3):
+                if (s + 3) % 2 == 0 and (s + 3) // 2 + LOAD_AHEAD < N_PAIRS:
+                    load_pair((s + 3) // 2 + LOAD_AHEAD)
+                transpose_qk(s + 3)
+            if live(s - 1):
+                eT_x = psum.tile([P, X_BLOCKS, P], BF16, tag="eT_x")
+                transpose_e(s - 1, eT_x, 0, (3, 2, 0))
+            if live(s):
+                scale_and_min(s, 3)
+            if live(s + 1):
+                new_score_bank(s + 1, "s_a", (3,))
+                score_blocks(s + 1, 3)
+            if live(s - 1) or 0 <= quarter < N_QUARTERS:
+                small = psum.tile([P, 2 + PACK, P], BF16, tag="small")
+            if live(s - 1):
+                transpose_e(s - 1, small[:, 0:2, :], X_BLOCKS, (1,))
+            if 0 <= quarter < N_QUARTERS:
+                transpose_a(quarter, small[:, 2 : 2 + PACK, :])
+            if 0 <= s < W_PIECES:
+                transpose_w(s)
+            if live(s):
+                scale_and_min(s, 2)
+                scale_and_min(s, 0)
+            if live(s + 1):
+                new_score_bank(s + 1, "s_b", (2, 0))
+                score_blocks(s + 1, 2)
+                score_blocks(s + 1, 0)
+            if live(s):
+                scale_and_min(s, 1)
+            if live(s + 1):
+                new_score_bank(s + 1, "s_c", (1,))
+                score_blocks(s + 1, 1)
+            if live(s):
+                exponentials(s)
+            if live(s + 3):
+                copy_qk(s + 3)
+            if live(s):
+                regroup_v(s)
+            if live(s - 3):
+                normalise(s - 3)
+            if live(s - 2):
+                quantise_e(s - 2)
+                attend(s - 2)
+            if 0 <= tile_now - 1 < N_TILES:
+                add_bias_and_store(tile_now - 1)
+            if 0 <= tile_now < N_TILES:
+                tags = ("acc", "s_a", "s_b", "s_c") if s >= N_HEADS else ("acc",)
+                project(tile_now, tags[tile_now % len(tags)])
+            if live(s - 1):
+                regroup_e(s - 1)
+            if 0 <= quarter < N_QUARTERS:
+                regroup_a(quarter)
+            if 0 <= s < W_PIECES:
+                regroup_w(s)
+            if live(s):
+                quantise_v(s)
+            if 0 <= quarter - 1 < N_QUARTERS:
+                quantise_a(quarter - 1)
+            if 0 <= s - 1 < W_PIECES:
+                quantise_w(s - 1)

@@ -112,6 +112,7 @@ def tile_alibiattention_pa_kernel(tc, q, k, v, w_out, b_out, out):
         x_tiles = {}
         e_tiles = {}
         rowsums = {}
+        rinv_tiles = {}
         eT_banks = {}
         e_operands = {}
         gv_tiles = {}
@@ -141,23 +142,23 @@ def tile_alibiattention_pa_kernel(tc, q, k, v, w_out, b_out, out):
         def score_blocks(i, qi):
             qkT = qkT_tiles[i]
             bank = score_banks[(i, qi)]
+            col = SEG_START[qi] % BANK
             for kb in range(qi + 1):
-                col = SEG_START[qi] % BANK + kb * P
                 nc.tensor.matmul(
-                    out=bank[:, col : col + P],
+                    out=bank[:, col + kb * P : col + (kb + 1) * P],
                     lhsT=maskT[:, qi - kb, :],
                     rhs=ident_f32[:],
                     is_transpose=True,
-                    start=True,
+                    start=(kb == 0),
                     stop=False,
                 )
-                nc.tensor.matmul(
-                    out=bank[:, col : col + P],
-                    lhsT=qkT[:, 0, qi * P : (qi + 1) * P],
-                    rhs=qkT[:, 1, kb * P : (kb + 1) * P],
-                    start=False,
-                    stop=True,
-                )
+            nc.tensor.matmul(
+                out=bank[:, col : col + (qi + 1) * P],
+                lhsT=qkT[:, 0, qi * P : (qi + 1) * P],
+                rhs=qkT[:, 1, 0 : (qi + 1) * P],
+                start=False,
+                stop=True,
+            )
 
         def transpose_e(i, bank, first_block, blocks):
             e_sb = e_tiles[i]
@@ -289,10 +290,14 @@ def tile_alibiattention_pa_kernel(tc, q, k, v, w_out, b_out, out):
             )
             v_operands[i] = (v_codes, v_scales)
 
-        def normalise(i):
-            group, t = i // PACK, i % PACK
+        def invert_rowsum(i):
             rinv = work.tile([P, QB], F32)
             nc.vector.reciprocal(out=rinv[:], in_=rowsums[i][:])
+            rinv_tiles[i] = rinv
+
+        def normalise(i):
+            group, t = i // PACK, i % PACK
+            rinv = rinv_tiles[i]
             if t == 0:
                 a_new = work.tile([P, PACK, QB, HD], BF16)
                 a_tiles[group] = a_new
@@ -366,7 +371,8 @@ def tile_alibiattention_pa_kernel(tc, q, k, v, w_out, b_out, out):
                 new_score_bank(s + 1, "s_a", (3,))
                 score_blocks(s + 1, 3)
             if live(s - 1) or 0 <= quarter < N_QUARTERS:
-                small = psum.tile([P, 2 + PACK, P], BF16, tag="small")
+                small_tags = ("small",) if live(s - 1) else ("small", "qkT", "eT_x")
+                small = psum.tile([P, 2 + PACK, P], BF16, tag=small_tags[quarter % len(small_tags)])
             if live(s - 1):
                 transpose_e(s - 1, small[:, 0:2, :], X_BLOCKS, (1,))
             if 0 <= quarter < N_QUARTERS:
@@ -380,6 +386,8 @@ def tile_alibiattention_pa_kernel(tc, q, k, v, w_out, b_out, out):
                 new_score_bank(s + 1, "s_b", (2, 0))
                 score_blocks(s + 1, 2)
                 score_blocks(s + 1, 0)
+            if live(s - 3):
+                invert_rowsum(s - 3)
             if live(s):
                 scale_and_min(s, 1)
             if live(s + 1):

@@ -274,10 +274,14 @@ def tile_alibiattention_pa_kernel(tc, q, k, v, w_out, b_out, out):
 
         def regroup_v(i):
             v_sb = pair_tiles[i // 2][2]
-            gv = work.tile([P, HD, PACK], BF16, align_bytes=64)
-            nc.vector.tensor_copy(
-                out=gv[:].rearrange("p (c i) t -> p c t i", i=4),
-                in_=v_sb[:, i % 2].rearrange("p t (c i) -> p c t i", i=4),
+            gv = work.tile([P, HD, PACK], BF16, align_bytes=64, bufs=1)
+            nc.gpsimd.tensor_scalar(
+                out=gv[:],
+                in0=v_sb[:, i % 2].rearrange("p t d -> p d t"),
+                scalar1=1.0,
+                scalar2=0.0,
+                op0=ALU.mult,
+                op1=ALU.add,
             )
             gv_tiles[i] = gv
 
@@ -310,7 +314,11 @@ def tile_alibiattention_pa_kernel(tc, q, k, v, w_out, b_out, out):
 
         def regroup_a(quarter):
             ga = work.tile([P, P, PACK], BF16, align_bytes=64)
-            nc.scalar.copy(out=ga[:], in_=aT_banks[quarter].rearrange("p t q -> p q t"))
+            src = aT_banks[quarter].rearrange("p t q -> p q t")
+            if quarter % QB == QB - 1:
+                nc.vector.tensor_copy(out=ga[:], in_=src)
+            else:
+                nc.scalar.copy(out=ga[:], in_=src)
             ga_tiles[quarter] = ga
 
         def quantise_a(quarter):
@@ -397,8 +405,6 @@ def tile_alibiattention_pa_kernel(tc, q, k, v, w_out, b_out, out):
                 exponentials(s)
             if live(s + 3):
                 copy_qk(s + 3)
-            if live(s):
-                regroup_v(s)
             if live(s - 3):
                 normalise(s - 3)
             if live(s - 2):
@@ -415,9 +421,11 @@ def tile_alibiattention_pa_kernel(tc, q, k, v, w_out, b_out, out):
                 regroup_a(quarter)
             if 0 <= s < W_PIECES:
                 regroup_w(s)
-            if live(s):
-                quantise_v(s)
             if 0 <= quarter - 1 < N_QUARTERS:
                 quantise_a(quarter - 1)
             if 0 <= s - 1 < W_PIECES:
                 quantise_w(s - 1)
+            if live(s):
+                quantise_v(s)
+            if live(s + 1):
+                regroup_v(s + 1)

@@ -139,26 +139,29 @@ def tile_alibiattention_pa_kernel(tc, q, k, v, w_out, b_out, out):
             for qi in blocks:
                 score_banks[(i, qi)] = bank
 
-        def score_blocks(i, qi):
+        def score_blocks(i, blocks):
             qkT = qkT_tiles[i]
-            bank = score_banks[(i, qi)]
-            col = SEG_START[qi] % BANK
-            for kb in range(qi + 1):
+            bank = score_banks[(i, blocks[0])]
+            for qi in blocks:
+                col = SEG_START[qi] % BANK
+                for kb in range(qi + 1):
+                    nc.tensor.matmul(
+                        out=bank[:, col + kb * P : col + (kb + 1) * P],
+                        lhsT=maskT[:, qi - kb, :],
+                        rhs=ident_f32[:],
+                        is_transpose=True,
+                        start=(qi == blocks[0] and kb == 0),
+                        stop=False,
+                    )
+            for qi in blocks:
+                col = SEG_START[qi] % BANK
                 nc.tensor.matmul(
-                    out=bank[:, col + kb * P : col + (kb + 1) * P],
-                    lhsT=maskT[:, qi - kb, :],
-                    rhs=ident_f32[:],
-                    is_transpose=True,
-                    start=(kb == 0),
-                    stop=False,
+                    out=bank[:, col : col + (qi + 1) * P],
+                    lhsT=qkT[:, 0, qi * P : (qi + 1) * P],
+                    rhs=qkT[:, 1, 0 : (qi + 1) * P],
+                    start=False,
+                    stop=(qi == blocks[-1]),
                 )
-            nc.tensor.matmul(
-                out=bank[:, col : col + (qi + 1) * P],
-                lhsT=qkT[:, 0, qi * P : (qi + 1) * P],
-                rhs=qkT[:, 1, 0 : (qi + 1) * P],
-                start=False,
-                stop=True,
-            )
 
         def transpose_e(i, bank, first_block, blocks):
             e_sb = e_tiles[i]
@@ -274,14 +277,10 @@ def tile_alibiattention_pa_kernel(tc, q, k, v, w_out, b_out, out):
 
         def regroup_v(i):
             v_sb = pair_tiles[i // 2][2]
-            gv = work.tile([P, HD, PACK], BF16, align_bytes=64, bufs=1)
-            nc.gpsimd.tensor_scalar(
-                out=gv[:],
-                in0=v_sb[:, i % 2].rearrange("p t d -> p d t"),
-                scalar1=1.0,
-                scalar2=0.0,
-                op0=ALU.mult,
-                op1=ALU.add,
+            gv = work.tile([P, HD, PACK], BF16, align_bytes=64)
+            nc.vector.tensor_copy(
+                out=gv[:].rearrange("p (c i) t -> p c t i", i=4),
+                in_=v_sb[:, i % 2].rearrange("p t (c i) -> p c t i", i=4),
             )
             gv_tiles[i] = gv
 
@@ -314,11 +313,7 @@ def tile_alibiattention_pa_kernel(tc, q, k, v, w_out, b_out, out):
 
         def regroup_a(quarter):
             ga = work.tile([P, P, PACK], BF16, align_bytes=64)
-            src = aT_banks[quarter].rearrange("p t q -> p q t")
-            if quarter % QB == QB - 1:
-                nc.vector.tensor_copy(out=ga[:], in_=src)
-            else:
-                nc.scalar.copy(out=ga[:], in_=src)
+            nc.scalar.copy(out=ga[:], in_=aT_banks[quarter].rearrange("p t q -> p q t"))
             ga_tiles[quarter] = ga
 
         def quantise_a(quarter):
@@ -359,7 +354,7 @@ def tile_alibiattention_pa_kernel(tc, q, k, v, w_out, b_out, out):
             n_cols = slice(nh * BANK, (nh + 1) * BANK)
             out_sb = work.tile([P, BANK], F32, bufs=4)
             nc.vector.tensor_tensor(out=out_sb[:], in0=acc_banks[r][:], in1=bias[:, n_cols], op=ALU.add)
-            nc.gpsimd.dma_start(out=out[b, tb * P : (tb + 1) * P, n_cols], in_=out_sb[:])
+            nc.sync.dma_start(out=out[b, tb * P : (tb + 1) * P, n_cols], in_=out_sb[:])
 
         A_LAG = PACK + 3
         P_LAG = H + 5
@@ -377,7 +372,7 @@ def tile_alibiattention_pa_kernel(tc, q, k, v, w_out, b_out, out):
                 scale_and_min(s, 3)
             if live(s + 1):
                 new_score_bank(s + 1, "s_a", (3,))
-                score_blocks(s + 1, 3)
+                score_blocks(s + 1, (3,))
             if live(s - 1) or 0 <= quarter < N_QUARTERS:
                 small_tags = ("small",) if live(s - 1) else ("small", "qkT", "eT_x")
                 small = psum.tile([P, 2 + PACK, P], BF16, tag=small_tags[quarter % len(small_tags)])
@@ -392,19 +387,20 @@ def tile_alibiattention_pa_kernel(tc, q, k, v, w_out, b_out, out):
                 scale_and_min(s, 0)
             if live(s + 1):
                 new_score_bank(s + 1, "s_b", (2, 0))
-                score_blocks(s + 1, 2)
-                score_blocks(s + 1, 0)
+                score_blocks(s + 1, (2, 0))
             if live(s - 3):
                 invert_rowsum(s - 3)
             if live(s):
                 scale_and_min(s, 1)
             if live(s + 1):
                 new_score_bank(s + 1, "s_c", (1,))
-                score_blocks(s + 1, 1)
+                score_blocks(s + 1, (1,))
             if live(s):
                 exponentials(s)
             if live(s + 3):
                 copy_qk(s + 3)
+            if live(s):
+                regroup_v(s)
             if live(s - 3):
                 normalise(s - 3)
             if live(s - 2):
@@ -421,11 +417,9 @@ def tile_alibiattention_pa_kernel(tc, q, k, v, w_out, b_out, out):
                 regroup_a(quarter)
             if 0 <= s < W_PIECES:
                 regroup_w(s)
+            if live(s):
+                quantise_v(s)
             if 0 <= quarter - 1 < N_QUARTERS:
                 quantise_a(quarter - 1)
             if 0 <= s - 1 < W_PIECES:
                 quantise_w(s - 1)
-            if live(s):
-                quantise_v(s)
-            if live(s + 1):
-                regroup_v(s + 1)

@@ -18,6 +18,7 @@ P = 128
 PACK = 4
 BANK = 512
 QB = S // P
+HALVES = PACK // 2
 GROUPS = H // PACK
 N_HEADS = B * H
 N_PAIRS = N_HEADS // 2
@@ -26,10 +27,12 @@ FAR = 1.0e30
 
 FLOPS = 2 * (2 * B * H * S * S * HD) + 2 * B * S * D * D
 
+E_START = {3: 0, 2: 512, 1: 1024, 0: 1280}
+E_COLS = 1536
+
 SEG_ORDER = (3, 2, 0, 1)
 SEG_START = {3: 0, 2: 512, 0: 896, 1: 1024}
 SEG_COLS = 1280
-X_BLOCKS = 8
 LOAD_AHEAD = 3
 W_PIECES = GROUPS * (D // P // 2)
 N_HALVES = D // BANK
@@ -61,8 +64,12 @@ def tile_alibiattention_pa_kernel(tc, q, k, v, w_out, b_out, out):
             q_sb = loads.tile([P, 2, QB, HD], BF16)
             k_sb = loads.tile([P, 2, QB, HD], BF16)
             v_sb = loads.tile([P, 2, QB, HD], BF16)
-            for dst, src in ((q_sb, q), (k_sb, k), (v_sb, v)):
+            for dst, src in ((q_sb, q), (k_sb, k)):
                 nc.sync.dma_start(out=dst[:], in_=src[b, h0 : h0 + 2].rearrange("h (t p) d -> p h t d", p=P))
+            nc.sync.dma_start(
+                out=v_sb[:].rearrange("p h (u e) d -> p h u (e d)", e=2),
+                in_=v[b, h0 : h0 + 2].rearrange("h (u p e) d -> p h u (e d)", p=P, e=2),
+            )
             pair_tiles[pair] = (q_sb, k_sb, v_sb)
 
         load_pair(0)
@@ -99,9 +106,14 @@ def tile_alibiattention_pa_kernel(tc, q, k, v, w_out, b_out, out):
 
         grouped_e = []
         for parity in range(2):
-            ge = const.tile([P, S, PACK], BF16, name="ge%d" % parity, align_bytes=64)
+            ge = const.tile([P, S * PACK], BF16, name="ge%d" % parity, align_bytes=64)
             nc.vector.memset(ge[:], 0.0)
             grouped_e.append(ge)
+        e_tiles = []
+        for turn in range(3):
+            e_sb = const.tile([P, E_COLS], BF16, name="e_sb%d" % turn)
+            nc.vector.memset(e_sb[:], 0.0)
+            e_tiles.append(e_sb)
 
         w_codes = const.tile([P, GROUPS, D], U32, align_bytes=64)
         w_scales = const.tile([P, GROUPS, D], U8, align_bytes=64)
@@ -110,7 +122,6 @@ def tile_alibiattention_pa_kernel(tc, q, k, v, w_out, b_out, out):
         qkT_tiles = {}
         score_banks = {}
         x_tiles = {}
-        e_tiles = {}
         rowsums = {}
         rinv_tiles = {}
         eT_banks = {}
@@ -163,28 +174,32 @@ def tile_alibiattention_pa_kernel(tc, q, k, v, w_out, b_out, out):
                     stop=(qi == blocks[-1]),
                 )
 
-        def transpose_e(i, bank, first_block, blocks):
-            e_sb = e_tiles[i]
+        def transpose_e(i, bank, blocks):
+            e_words = e_tiles[i % 3][:].bitcast(F32)
+            at = 0
             for qi in blocks:
-                at = SEG_START[qi] // P - first_block
-                for t in range(qi + 1):
-                    col = SEG_START[qi] + t * P
-                    nc.tensor.transpose(bank[:, at + t, :], e_sb[:, col : col + P], ident[:])
-                eT_banks[(i, qi)] = bank[:, at : at + qi + 1, :]
+                n = (qi + 2) // 2
+                for u in range(n):
+                    w0 = E_START[qi] // 2 + u * P
+                    nc.tensor.transpose(bank[:, at + u, :], e_words[:, w0 : w0 + P], ident_f32[:])
+                eT_banks[(i, qi)] = bank[:, at : at + n, :]
+                at += n
 
         def transpose_a(quarter, bank):
             group, qi = quarter // QB, quarter % QB
-            for t in range(PACK):
-                nc.tensor.transpose(bank[:, t, :], a_tiles[group][:, t, qi, :], ident[:])
+            words = a_tiles[group][:, qi, :].bitcast(F32)
+            for u in range(HALVES):
+                nc.tensor.transpose(bank[:, u, :], words[:, u * P : (u + 1) * P], ident_f32[:])
             aT_banks[quarter] = bank
 
         def transpose_w(piece):
             g, nb0 = piece // (D // P // 2), 2 * (piece % (D // P // 2))
-            wT = psum.tile([P, 2, PACK, P], BF16, tag="acc")
+            wT = psum.tile([P, 2, HALVES, P], F32, tag="acc")
             for j in range(2):
-                for t in range(PACK):
-                    f0 = (PACK * g + t) * P
-                    nc.tensor.transpose(wT[:, j, t, :], w_sb[:, nb0 + j, f0 : f0 + P], ident[:])
+                words = w_sb[:, nb0 + j, :].bitcast(F32)
+                for u in range(HALVES):
+                    w0 = (HALVES * g + u) * P
+                    nc.tensor.transpose(wT[:, j, u, :], words[:, w0 : w0 + P], ident_f32[:])
             wT_banks[piece] = wT
 
         def attend(i):
@@ -245,24 +260,24 @@ def tile_alibiattention_pa_kernel(tc, q, k, v, w_out, b_out, out):
         def exponentials(i):
             x, negmax = x_tiles[i]
             rowsum = work.tile([P, QB], F32, bufs=6)
-            e_sb = work.tile([P, SEG_COLS], BF16)
+            e_sb = e_tiles[i % 3]
             for qi in SEG_ORDER:
                 nc.scalar.activation(
-                    out=e_sb[:, seg(qi)],
+                    out=e_sb[:, E_START[qi] : E_START[qi] + (qi + 1) * P],
                     in_=x[:, seg(qi)],
                     func=ACT.Exp,
                     scale=-1.0,
                     bias=negmax[:, qi : qi + 1],
                     accum_out=rowsum[:, qi : qi + 1],
                 )
-            e_tiles[i] = e_sb
             rowsums[i] = rowsum
 
         def regroup_e(i):
-            ge = grouped_e[i % 2]
+            ge_words = grouped_e[i % 2][:].bitcast(F32).rearrange("p (q u) -> p q u", u=HALVES)
             for qi in SEG_ORDER:
+                src = eT_banks[(i, qi)]
                 nc.scalar.copy(
-                    out=ge[:, qi * P : (qi + 1) * P, 0 : qi + 1], in_=eT_banks[(i, qi)].rearrange("p t q -> p q t")
+                    out=ge_words[:, qi * P : (qi + 1) * P, 0 : src.shape[1]], in_=src.rearrange("p u q -> p q u")
                 )
 
         def quantise_e(i):
@@ -271,7 +286,7 @@ def tile_alibiattention_pa_kernel(tc, q, k, v, w_out, b_out, out):
             nc.vector.quantize_mx(
                 out=e_codes[:].bitcast(FP8X4),
                 scales=e_scales[:],
-                in_=grouped_e[i % 2][:].rearrange("p q t -> p (q t)"),
+                in_=grouped_e[i % 2][:],
             )
             e_operands[i] = (e_codes, e_scales)
 
@@ -302,18 +317,21 @@ def tile_alibiattention_pa_kernel(tc, q, k, v, w_out, b_out, out):
             group, t = i // PACK, i % PACK
             rinv = rinv_tiles[i]
             if t == 0:
-                a_new = work.tile([P, PACK, QB, HD], BF16)
+                a_new = work.tile([P, QB, PACK * HD], BF16)
                 a_tiles[group] = a_new
             nc.vector.tensor_tensor(
-                out=a_tiles[group][:, t],
+                out=a_tiles[group][:, :, t * HD : (t + 1) * HD],
                 in0=o_banks[i][:],
                 in1=rinv[:].unsqueeze(2).to_broadcast([P, QB, HD]),
                 op=ALU.mult,
             )
 
         def regroup_a(quarter):
-            ga = work.tile([P, P, PACK], BF16, align_bytes=64)
-            nc.scalar.copy(out=ga[:], in_=aT_banks[quarter].rearrange("p t q -> p q t"))
+            ga = work.tile([P, P * PACK], BF16, align_bytes=64)
+            nc.scalar.copy(
+                out=ga[:].bitcast(F32).rearrange("p (q u) -> p q u", u=HALVES),
+                in_=aT_banks[quarter].rearrange("p u q -> p q u"),
+            )
             ga_tiles[quarter] = ga
 
         def quantise_a(quarter):
@@ -328,16 +346,17 @@ def tile_alibiattention_pa_kernel(tc, q, k, v, w_out, b_out, out):
             nc.vector.quantize_mx(
                 out=a_codes[:, g, cols].bitcast(FP8X4),
                 scales=a_scales[:, g, cols],
-                in_=ga_tiles[quarter][:].rearrange("p q t -> p (q t)"),
+                in_=ga_tiles[quarter][:],
             )
 
         def regroup_w(piece):
-            gw = work.tile([P, 2, P, PACK], BF16, align_bytes=64)
-            src = wT_banks[piece][:].rearrange("p j t n -> p j n t")
+            gw = work.tile([P, 2 * P * PACK], BF16, align_bytes=64)
+            dst = gw[:].bitcast(F32).rearrange("p (j n u) -> p j n u", j=2, u=HALVES)
+            src = wT_banks[piece][:].rearrange("p j u n -> p j n u")
             if piece % 2 == 0:
-                nc.scalar.copy(out=gw[:], in_=src)
+                nc.scalar.copy(out=dst, in_=src)
             else:
-                nc.vector.tensor_copy(out=gw[:], in_=src)
+                nc.vector.tensor_copy(out=dst, in_=src)
             gw_tiles[piece] = gw
 
         def quantise_w(piece):
@@ -346,7 +365,7 @@ def tile_alibiattention_pa_kernel(tc, q, k, v, w_out, b_out, out):
             nc.vector.quantize_mx(
                 out=w_codes[:, g, cols].bitcast(FP8X4),
                 scales=w_scales[:, g, cols],
-                in_=gw_tiles[piece][:].rearrange("p j n t -> p (j n t)"),
+                in_=gw_tiles[piece][:],
             )
 
         def add_bias_and_store(r):
@@ -366,8 +385,8 @@ def tile_alibiattention_pa_kernel(tc, q, k, v, w_out, b_out, out):
                     load_pair((s + 3) // 2 + LOAD_AHEAD)
                 transpose_qk(s + 3)
             if live(s - 1):
-                eT_x = psum.tile([P, X_BLOCKS, P], BF16, tag="eT_x")
-                transpose_e(s - 1, eT_x, 0, (3, 2, 0))
+                eT_x = psum.tile([P, 2 * HALVES, P], F32, tag="eT_x")
+                transpose_e(s - 1, eT_x, (3, 2))
             if live(s):
                 scale_and_min(s, 3)
             if live(s + 1):
@@ -375,11 +394,11 @@ def tile_alibiattention_pa_kernel(tc, q, k, v, w_out, b_out, out):
                 score_blocks(s + 1, (3,))
             if live(s - 1) or 0 <= quarter < N_QUARTERS:
                 small_tags = ("small",) if live(s - 1) else ("small", "qkT", "eT_x")
-                small = psum.tile([P, 2 + PACK, P], BF16, tag=small_tags[quarter % len(small_tags)])
+                small = psum.tile([P, 2 + HALVES, P], F32, tag=small_tags[quarter % len(small_tags)])
             if live(s - 1):
-                transpose_e(s - 1, small[:, 0:2, :], X_BLOCKS, (1,))
+                transpose_e(s - 1, small[:, 0:2, :], (1, 0))
             if 0 <= quarter < N_QUARTERS:
-                transpose_a(quarter, small[:, 2 : 2 + PACK, :])
+                transpose_a(quarter, small[:, 2 : 2 + HALVES, :])
             if 0 <= s < W_PIECES:
                 transpose_w(s)
             if live(s):

@@ -11,6 +11,7 @@ U8 = mybir.dt.uint8
 FP8X4 = mybir.dt.float8_e4m3fn_x4
 ALU = mybir.AluOpType
 ACT = mybir.ActivationFunctionType
+AX = mybir.AxisListType
 
 B, H, S, HD = 4, 8, 512, 128
 D = H * HD
@@ -21,6 +22,8 @@ QB = S // P
 HALVES = PACK // 2
 GROUPS = H // PACK
 N_HEADS = B * H
+E_START = {3: 0, 2: 512, 1: 1024, 0: 1280}
+E_COLS = 1536
 N_PAIRS = N_HEADS // 2
 SCALE = 1.0 / math.sqrt(HD)
 FAR = 1.0e30
@@ -30,18 +33,13 @@ FLOPS = 2 * (2 * B * H * S * S * HD) + 2 * B * S * D * D
 E_START = {3: 0, 2: 512, 1: 1024, 0: 1280}
 E_COLS = 1536
 
-SEG_ORDER = (3, 2, 0, 1)
-SEG_START = {3: 0, 2: 512, 0: 896, 1: 1024}
-SEG_COLS = 1280
+SCORE_BANKS = {"s_a": (3,), "s_b": (2, 0), "s_c": (1,)}
+SCORE_COL = {3: 0, 2: 0, 0: 384, 1: 0}
 LOAD_AHEAD = 3
 W_PIECES = GROUPS * (D // P // 2)
 N_HALVES = D // BANK
 N_TILES = B * QB * N_HALVES
 N_QUARTERS = B * GROUPS * QB
-
-
-def seg(qi):
-    return slice(SEG_START[qi], SEG_START[qi] + (qi + 1) * P)
 
 
 def live(i):
@@ -64,21 +62,24 @@ def tile_alibiattention_pa_kernel(tc, q, k, v, w_out, b_out, out):
             q_sb = loads.tile([P, 2, QB, HD], BF16)
             k_sb = loads.tile([P, 2, QB, HD], BF16)
             v_sb = loads.tile([P, 2, QB, HD], BF16)
-            for dst, src in ((q_sb, q), (k_sb, k)):
-                nc.sync.dma_start(out=dst[:], in_=src[b, h0 : h0 + 2].rearrange("h (t p) d -> p h t d", p=P))
+            heads = ((0, 2),) if pair else ((0, 1), (1, 2))
+            for lo, hi in heads:
+                for dst, src in ((q_sb, q), (k_sb, k)):
+                    nc.sync.dma_start(
+                        out=dst[:, lo:hi], in_=src[b, h0 + lo : h0 + hi].rearrange("h (t p) d -> p h t d", p=P)
+                    )
             nc.sync.dma_start(
                 out=v_sb[:].rearrange("p h (u e) d -> p h u (e d)", e=2),
                 in_=v[b, h0 : h0 + 2].rearrange("h (u p e) d -> p h u (e d)", p=P, e=2),
             )
             pair_tiles[pair] = (q_sb, k_sb, v_sb)
 
-        load_pair(0)
-        load_pair(1)
+        for pair in range(LOAD_AHEAD):
+            load_pair(pair)
         w_sb = const.tile([P, D // P, D], BF16)
         nc.sync.dma_start(out=w_sb[:], in_=w_out.rearrange("(nb p) f -> p nb f", p=P))
         bias = const.tile([P, D], BF16)
         nc.sync.dma_start(out=bias[:], in_=b_out.partition_broadcast(P))
-        load_pair(2)
 
         ident = const.tile([P, P], BF16)
         make_identity(nc, ident[:])
@@ -107,13 +108,21 @@ def tile_alibiattention_pa_kernel(tc, q, k, v, w_out, b_out, out):
         grouped_e = []
         for parity in range(2):
             ge = const.tile([P, S * PACK], BF16, name="ge%d" % parity, align_bytes=64)
-            nc.vector.memset(ge[:], 0.0)
+            nc.gpsimd.memset(ge[:].bitcast(F32), 0.0)
             grouped_e.append(ge)
         e_tiles = []
         for turn in range(3):
             e_sb = const.tile([P, E_COLS], BF16, name="e_sb%d" % turn)
-            nc.vector.memset(e_sb[:], 0.0)
+            for qi in (2, 0):
+                pad = E_START[qi] + (qi + 1) * P
+                nc.gpsimd.memset(e_sb[:, pad : pad + P].bitcast(F32), 0.0)
             e_tiles.append(e_sb)
+        zeros = const.tile([P, P], F32)
+        nc.vector.memset(zeros[:], 0.0)
+
+        eT_low = psum.tile([P, HALVES, 2, P], F32, tag="eT_low")
+        for block in range(2):
+            nc.tensor.transpose(eT_low[:, 1, block, :], zeros[:], ident_f32[:])
 
         w_codes = const.tile([P, GROUPS, D], U32, align_bytes=64)
         w_scales = const.tile([P, GROUPS, D], U8, align_bytes=64)
@@ -121,10 +130,11 @@ def tile_alibiattention_pa_kernel(tc, q, k, v, w_out, b_out, out):
         qkT_banks = {}
         qkT_tiles = {}
         score_banks = {}
-        x_tiles = {}
+        lowest_tiles = {}
+        negmax_tiles = {}
         rowsums = {}
         rinv_tiles = {}
-        eT_banks = {}
+        eT_high_banks = {}
         e_operands = {}
         gv_tiles = {}
         v_operands = {}
@@ -145,16 +155,12 @@ def tile_alibiattention_pa_kernel(tc, q, k, v, w_out, b_out, out):
                     nc.tensor.transpose(qkT_ps[:, which, t * P : (t + 1) * P], src[:, i % 2, t, :], ident[:])
             qkT_banks[i] = qkT_ps
 
-        def new_score_bank(i, tag, blocks):
+        def masks(i, tag):
+            blocks = SCORE_BANKS[tag]
             bank = psum.tile([P, BANK], F32, tag=tag)
             for qi in blocks:
-                score_banks[(i, qi)] = bank
-
-        def score_blocks(i, blocks):
-            qkT = qkT_tiles[i]
-            bank = score_banks[(i, blocks[0])]
-            for qi in blocks:
-                col = SEG_START[qi] % BANK
+                col = SCORE_COL[qi]
+                score_banks[(i, qi)] = bank[:, col : col + (qi + 1) * P]
                 for kb in range(qi + 1):
                     nc.tensor.matmul(
                         out=bank[:, col + kb * P : col + (kb + 1) * P],
@@ -164,33 +170,37 @@ def tile_alibiattention_pa_kernel(tc, q, k, v, w_out, b_out, out):
                         start=(qi == blocks[0] and kb == 0),
                         stop=False,
                     )
+            return bank
+
+        def products(i, tag):
+            qkT = qkT_tiles[i]
+            blocks = SCORE_BANKS[tag]
             for qi in blocks:
-                col = SEG_START[qi] % BANK
                 nc.tensor.matmul(
-                    out=bank[:, col : col + (qi + 1) * P],
+                    out=score_banks[(i, qi)],
                     lhsT=qkT[:, 0, qi * P : (qi + 1) * P],
                     rhs=qkT[:, 1, 0 : (qi + 1) * P],
                     start=False,
                     stop=(qi == blocks[-1]),
                 )
 
-        def transpose_e(i, bank, blocks):
+        def transpose_e(i):
             e_words = e_tiles[i % 3][:].bitcast(F32)
-            at = 0
-            for qi in blocks:
-                n = (qi + 2) // 2
-                for u in range(n):
+            eT_high = psum.tile([P, 2, HALVES, P], F32, tag="eT_high")
+            for qi in range(QB):
+                for u in range((qi + 2) // 2):
+                    dst = eT_low[:, u, qi, :] if qi < 2 else eT_high[:, qi - 2, u, :]
                     w0 = E_START[qi] // 2 + u * P
-                    nc.tensor.transpose(bank[:, at + u, :], e_words[:, w0 : w0 + P], ident_f32[:])
-                eT_banks[(i, qi)] = bank[:, at : at + n, :]
-                at += n
+                    nc.tensor.transpose(dst, e_words[:, w0 : w0 + P], ident_f32[:])
+            eT_high_banks[i] = eT_high
 
-        def transpose_a(quarter, bank):
+        def transpose_a(quarter, bank, half=1):
             group, qi = quarter // QB, quarter % QB
             words = a_tiles[group][:, qi, :].bitcast(F32)
             for u in range(HALVES):
-                nc.tensor.transpose(bank[:, u, :], words[:, u * P : (u + 1) * P], ident_f32[:])
-            aT_banks[quarter] = bank
+                col = (HALVES * half + u) * P
+                nc.tensor.transpose(bank[:, col : col + P], words[:, u * P : (u + 1) * P], ident_f32[:])
+            aT_banks[quarter] = bank[:, half * BANK // 2 : (half + 1) * BANK // 2]
 
         def transpose_w(piece):
             g, nb0 = piece // (D // P // 2), 2 * (piece % (D // P // 2))
@@ -202,10 +212,10 @@ def tile_alibiattention_pa_kernel(tc, q, k, v, w_out, b_out, out):
                     nc.tensor.transpose(wT[:, j, u, :], words[:, w0 : w0 + P], ident_f32[:])
             wT_banks[piece] = wT
 
-        def attend(i):
+        def attend(i, tag="o"):
             e_codes, e_scales = e_operands[i]
             v_codes, v_scales = v_operands[i]
-            o_ps = psum.tile([P, QB, HD], F32, tag="o")
+            o_ps = psum.tile([P, QB, HD], F32, tag=tag)
             for qi in range(QB):
                 cols = slice(qi * P, (qi + 1) * P)
                 nc.tensor.matmul_mx(
@@ -219,13 +229,15 @@ def tile_alibiattention_pa_kernel(tc, q, k, v, w_out, b_out, out):
                 )
             o_banks[i] = o_ps
 
-        def project(r, tag):
+        def project(r, tag=None, groups=range(GROUPS)):
             b, tb, nh = r // (QB * N_HALVES), (r // N_HALVES) % QB, r % N_HALVES
             a_codes, a_scales = a_operands[b]
-            acc = psum.tile([P, BANK], F32, tag=tag)
-            for g in range(GROUPS):
+            if tag:
+                acc_new = psum.tile([P, BANK], F32, tag=tag)
+                acc_banks[r] = acc_new
+            for g in groups:
                 nc.tensor.matmul_mx(
-                    out=acc[:],
+                    out=acc_banks[r][:],
                     lhsT=a_codes[:, g, tb * P : (tb + 1) * P].bitcast(FP8X4),
                     lhsT_scale=a_scales[:, g, tb * P : (tb + 1) * P],
                     rhs=w_codes[:, g, nh * BANK : (nh + 1) * BANK].bitcast(FP8X4),
@@ -233,52 +245,45 @@ def tile_alibiattention_pa_kernel(tc, q, k, v, w_out, b_out, out):
                     start=(g == 0),
                     stop=(g == GROUPS - 1),
                 )
-            acc_banks[r] = acc
 
         def copy_qk(i):
             qkT = work.tile([P, 2, S], BF16, bufs=4)
             nc.scalar.copy(out=qkT[:], in_=qkT_banks[i][:])
             qkT_tiles[i] = qkT
 
-        def scale_and_min(i, qi):
-            if qi == SEG_ORDER[0]:
-                x_new = work.tile([P, SEG_COLS], F32)
-                negmax_new = work.tile([P, QB], F32)
-                x_tiles[i] = (x_new, negmax_new)
-            x, negmax = x_tiles[i]
-            col = SEG_START[qi] % BANK
-            nc.vector.tensor_scalar(
-                out=x[:, seg(qi)],
-                in0=score_banks[(i, qi)][:, col : col + (qi + 1) * P],
-                scalar1=-SCALE,
-                scalar2=None,
-                op0=ALU.mult,
-                op1=ALU.min,
-                accum_out=negmax[:, qi : qi + 1],
-            )
+        def row_maxima(i, tag):
+            blocks = SCORE_BANKS[tag]
+            lowest = work.tile([P, len(blocks)], F32, name="lowest_" + tag)
+            for j, qi in enumerate(blocks):
+                nc.vector.tensor_reduce(
+                    out=lowest[:, j : j + 1], in_=score_banks[(i, qi)], axis=AX.X, op=ALU.max, negate=True
+                )
+            lowest_tiles[(i, tag)] = lowest
 
-        def exponentials(i):
-            x, negmax = x_tiles[i]
-            rowsum = work.tile([P, QB], F32, bufs=6)
+        def exp_bias(i, tag):
+            negmax = work.tile([P, len(SCORE_BANKS[tag])], F32, name="negmax_" + tag)
+            nc.gpsimd.tensor_scalar(out=negmax[:], in0=lowest_tiles[(i, tag)][:], scalar1=SCALE, scalar2=0.0, op0=ALU.mult, op1=ALU.add)
+            negmax_tiles[(i, tag)] = negmax
+
+        def exponentials(i, tag):
+            if i not in rowsums:
+                rowsum_new = work.tile([P, QB], F32, bufs=6)
+                rowsums[i] = rowsum_new
             e_sb = e_tiles[i % 3]
-            for qi in SEG_ORDER:
+            for j, qi in enumerate(SCORE_BANKS[tag]):
                 nc.scalar.activation(
                     out=e_sb[:, E_START[qi] : E_START[qi] + (qi + 1) * P],
-                    in_=x[:, seg(qi)],
+                    in_=score_banks[(i, qi)],
                     func=ACT.Exp,
-                    scale=-1.0,
-                    bias=negmax[:, qi : qi + 1],
-                    accum_out=rowsum[:, qi : qi + 1],
+                    scale=SCALE,
+                    bias=negmax_tiles[(i, tag)][:, j : j + 1],
+                    accum_out=rowsums[i][:, qi : qi + 1],
                 )
-            rowsums[i] = rowsum
 
-        def regroup_e(i):
-            ge_words = grouped_e[i % 2][:].bitcast(F32).rearrange("p (q u) -> p q u", u=HALVES)
-            for qi in SEG_ORDER:
-                src = eT_banks[(i, qi)]
-                nc.scalar.copy(
-                    out=ge_words[:, qi * P : (qi + 1) * P, 0 : src.shape[1]], in_=src.rearrange("p u q -> p q u")
-                )
+        def regroup_e(i, half, copy):
+            ge_words = grouped_e[i % 2][:].bitcast(F32).rearrange("p (b q u) -> p b q u", b=QB, u=HALVES)
+            src = eT_high_banks[i][:].rearrange("p b u q -> p b q u") if half else eT_low[:].rearrange("p u b q -> p b q u")
+            copy(out=ge_words[:, 2 * half : 2 * half + 2], in_=src)
 
         def quantise_e(i):
             e_codes = work.tile([P, S], U32, align_bytes=64)
@@ -313,24 +318,37 @@ def tile_alibiattention_pa_kernel(tc, q, k, v, w_out, b_out, out):
             nc.vector.reciprocal(out=rinv[:], in_=rowsums[i][:])
             rinv_tiles[i] = rinv
 
-        def normalise(i):
+        def normalise(i, blocks=range(QB)):
             group, t = i // PACK, i % PACK
-            rinv = rinv_tiles[i]
-            if t == 0:
+            if group not in a_tiles:
                 a_new = work.tile([P, QB, PACK * HD], BF16)
                 a_tiles[group] = a_new
+            lo, hi = blocks[0], blocks[-1] + 1
             nc.vector.tensor_tensor(
-                out=a_tiles[group][:, :, t * HD : (t + 1) * HD],
-                in0=o_banks[i][:],
-                in1=rinv[:].unsqueeze(2).to_broadcast([P, QB, HD]),
+                out=a_tiles[group][:, lo:hi, t * HD : (t + 1) * HD],
+                in0=o_banks[i][:, lo:hi],
+                in1=rinv_tiles[i][:, lo:hi].unsqueeze(2).to_broadcast([P, hi - lo, HD]),
                 op=ALU.mult,
             )
 
-        def regroup_a(quarter):
-            ga = work.tile([P, P * PACK], BF16, align_bytes=64)
-            nc.scalar.copy(
+        def normalise_on_scalar(i, blocks):
+            group, t = i // PACK, i % PACK
+            if group not in a_tiles:
+                a_new = work.tile([P, QB, PACK * HD], BF16, name="a_new")
+                a_tiles[group] = a_new
+            for qi in blocks:
+                nc.scalar.activation(
+                    out=a_tiles[group][:, qi, t * HD : (t + 1) * HD],
+                    in_=o_banks[i][:, qi],
+                    func=ACT.Copy,
+                    scale=rinv_tiles[i][:, qi : qi + 1],
+                )
+
+        def regroup_a(quarter, copy):
+            ga = work.tile([P, P * PACK], BF16, align_bytes=64, bufs=9)
+            copy(
                 out=ga[:].bitcast(F32).rearrange("p (q u) -> p q u", u=HALVES),
-                in_=aT_banks[quarter].rearrange("p u q -> p q u"),
+                in_=aT_banks[quarter].rearrange("p (u q) -> p q u", u=HALVES),
             )
             ga_tiles[quarter] = ga
 
@@ -368,77 +386,162 @@ def tile_alibiattention_pa_kernel(tc, q, k, v, w_out, b_out, out):
                 in_=gw_tiles[piece][:],
             )
 
-        def add_bias_and_store(r):
+        def add_bias_and_store(r, on_gpsimd=False):
             b, tb, nh = r // (QB * N_HALVES), (r // N_HALVES) % QB, r % N_HALVES
             n_cols = slice(nh * BANK, (nh + 1) * BANK)
-            out_sb = work.tile([P, BANK], F32, bufs=4)
-            nc.vector.tensor_tensor(out=out_sb[:], in0=acc_banks[r][:], in1=bias[:, n_cols], op=ALU.add)
+            out_sb = work.tile([P, BANK], F32, bufs=14)
+            if on_gpsimd:
+                sums = work.tile([P, BANK], F32, bufs=4)
+                nc.scalar.copy(out=sums[:], in_=acc_banks[r][:])
+                nc.gpsimd.tensor_tensor(out=out_sb[:], in0=sums[:], in1=bias[:, n_cols], op=ALU.add)
+            else:
+                nc.vector.tensor_tensor(out=out_sb[:], in0=acc_banks[r][:], in1=bias[:, n_cols], op=ALU.add)
             nc.sync.dma_start(out=out[b, tb * P : (tb + 1) * P, n_cols], in_=out_sb[:])
 
         A_LAG = PACK + 3
+        W_LAG = 2
         P_LAG = H + 5
-        for s in range(-3, N_TILES + P_LAG + 1):
+        a_bank = None
+        for s in range(-3, N_HEADS - 1):
             quarter = s - A_LAG
             tile_now = s - P_LAG
-            if live(s + 3):
-                if (s + 3) % 2 == 0 and (s + 3) // 2 + LOAD_AHEAD < N_PAIRS:
-                    load_pair((s + 3) // 2 + LOAD_AHEAD)
-                transpose_qk(s + 3)
-            if live(s - 1):
-                eT_x = psum.tile([P, 2 * HALVES, P], F32, tag="eT_x")
-                transpose_e(s - 1, eT_x, (3, 2))
+            if live(s + 3) and (s + 3) % 2 == 0 and (s + 3) // 2 + LOAD_AHEAD < N_PAIRS:
+                load_pair((s + 3) // 2 + LOAD_AHEAD)
             if live(s):
-                scale_and_min(s, 3)
+                exponentials(s, "s_a")
+                exponentials(s, "s_b")
             if live(s + 1):
-                new_score_bank(s + 1, "s_a", (3,))
-                score_blocks(s + 1, (3,))
-            if live(s - 1) or 0 <= quarter < N_QUARTERS:
-                small_tags = ("small",) if live(s - 1) else ("small", "qkT", "eT_x")
-                small = psum.tile([P, 2 + HALVES, P], F32, tag=small_tags[quarter % len(small_tags)])
-            if live(s - 1):
-                transpose_e(s - 1, small[:, 0:2, :], (1, 0))
+                masks(s + 1, "s_a")
             if 0 <= quarter < N_QUARTERS:
-                transpose_a(quarter, small[:, 2 : 2 + HALVES, :])
-            if 0 <= s < W_PIECES:
-                transpose_w(s)
+                transpose_a(quarter, a_bank)
             if live(s):
-                scale_and_min(s, 2)
-                scale_and_min(s, 0)
+                exponentials(s, "s_c")
+            if 0 <= quarter < N_QUARTERS:
+                regroup_a(quarter, nc.scalar.copy)
             if live(s + 1):
-                new_score_bank(s + 1, "s_b", (2, 0))
-                score_blocks(s + 1, (2, 0))
+                masks(s + 1, "s_b")
+                products(s + 1, "s_a")
             if live(s - 3):
-                invert_rowsum(s - 3)
-            if live(s):
-                scale_and_min(s, 1)
+                attend(s - 3)
+            if 0 <= tile_now < N_TILES:
+                project(tile_now, "acc")
             if live(s + 1):
-                new_score_bank(s + 1, "s_c", (1,))
-                score_blocks(s + 1, (1,))
-            if live(s):
-                exponentials(s)
-            if live(s + 3):
-                copy_qk(s + 3)
-            if live(s):
-                regroup_v(s)
-            if live(s - 3):
-                normalise(s - 3)
+                products(s + 1, "s_b")
+                a_bank = masks(s + 1, "s_c")
+                products(s + 1, "s_c")
+            if live(s + 2):
+                copy_qk(s + 2)
             if live(s - 2):
                 quantise_e(s - 2)
-                attend(s - 2)
-            if 0 <= tile_now - 1 < N_TILES:
-                add_bias_and_store(tile_now - 1)
-            if 0 <= tile_now < N_TILES:
-                tags = ("acc", "s_a", "s_b", "s_c") if s >= N_HEADS else ("acc",)
-                project(tile_now, tags[tile_now % len(tags)])
-            if live(s - 1):
-                regroup_e(s - 1)
-            if 0 <= quarter < N_QUARTERS:
-                regroup_a(quarter)
-            if 0 <= s < W_PIECES:
-                regroup_w(s)
             if live(s):
                 quantise_v(s)
+            if live(s + 1):
+                row_maxima(s + 1, "s_a")
+                exp_bias(s + 1, "s_a")
+            if live(s - 3):
+                normalise(s - 3)
+            if live(s + 1):
+                row_maxima(s + 1, "s_b")
+                exp_bias(s + 1, "s_b")
+                row_maxima(s + 1, "s_c")
+                exp_bias(s + 1, "s_c")
+            if 0 <= tile_now < N_TILES:
+                add_bias_and_store(tile_now)
             if 0 <= quarter - 1 < N_QUARTERS:
                 quantise_a(quarter - 1)
-            if 0 <= s - 1 < W_PIECES:
-                quantise_w(s - 1)
+            if 0 <= s - 2 - W_LAG < W_PIECES:
+                quantise_w(s - 2 - W_LAG)
+            if live(s + 1):
+                regroup_v(s + 1)
+            if live(s - 2):
+                invert_rowsum(s - 2)
+            if live(s - 1):
+                regroup_e(s - 1, 1, nc.scalar.copy)
+                regroup_e(s - 1, 0, nc.scalar.copy)
+            if 0 <= s - 1 - W_LAG < W_PIECES:
+                regroup_w(s - 1 - W_LAG)
+            if live(s + 3):
+                transpose_qk(s + 3)
+            if live(s):
+                transpose_e(s)
+            if 0 <= s - W_LAG < W_PIECES:
+                transpose_w(s - W_LAG)
+
+        SC, VC = nc.scalar.copy, nc.vector.tensor_copy
+        L = N_HEADS - 1
+
+        def new_bank(tag):
+            bank = psum.tile([P, BANK], F32, tag=tag)
+            return bank
+
+        exponentials(L, "s_a")
+        regroup_e(L - 1, 1, SC)
+        exponentials(L, "s_b")
+        transpose_a(24, a_bank)
+        x = new_bank("qkT")
+        transpose_a(25, x, 0)
+        transpose_a(26, x, 1)
+        exponentials(L, "s_c")
+        attend(L - 3)
+        project(18, "acc")
+        quantise_e(L - 2)
+        quantise_v(L)
+        regroup_e(L - 1, 0, SC)
+        invert_rowsum(L - 2)
+        invert_rowsum(L - 1)
+        attend(L - 2, "s_a")
+        transpose_e(L)
+        normalise(L - 3)
+        quantise_e(L - 1)
+        project(19, "s_b")
+        regroup_e(L, 1, SC)
+        regroup_e(L, 0, VC)
+        attend(L - 1, "o")
+        normalise_on_scalar(L - 2, range(QB))
+        quantise_e(L)
+        regroup_a(24, SC)
+        regroup_a(25, SC)
+        regroup_a(26, SC)
+        invert_rowsum(L)
+        project(20, "eT_high")
+        attend(L, "s_a")
+        normalise(L - 1)
+        normalise(L, (0, 1))
+        normalise_on_scalar(L, (2, 3))
+        add_bias_and_store(18)
+        y = new_bank("acc")
+        z = new_bank("s_c")
+        transpose_a(28, z, 0)
+        transpose_a(29, z, 1)
+        transpose_a(30, x, 0)
+        transpose_a(31, x, 1)
+        transpose_a(27, y, 0)
+        regroup_a(28, VC)
+        regroup_a(30, SC)
+        regroup_a(29, VC)
+        regroup_a(31, SC)
+        project(21, "o")
+        quantise_a(23)
+        quantise_a(24)
+        quantise_a(28)
+        quantise_a(25)
+        quantise_a(29)
+        regroup_a(27, SC)
+        quantise_a(26)
+        quantise_a(30)
+        quantise_a(27)
+        quantise_a(31)
+        add_bias_and_store(19, True)
+        add_bias_and_store(20)
+        project(24, "s_a")
+        project(25, "s_c")
+        add_bias_and_store(21, True)
+        project(22, "s_b")
+        project(23, "eT_high")
+        add_bias_and_store(24)
+        add_bias_and_store(25, True)
+        add_bias_and_store(22)
+        add_bias_and_store(23, True)
+        for j, r in enumerate(range(26, 32)):
+            project(r, ("qkT", "acc", "o", "s_a", "s_c", "s_b", "eT_high")[j % 7])
+            add_bias_and_store(r, j % 2 == 1)

@@ -22,8 +22,6 @@ QB = S // P
 HALVES = PACK // 2
 GROUPS = H // PACK
 N_HEADS = B * H
-E_START = {3: 0, 2: 512, 1: 1024, 0: 1280}
-E_COLS = 1536
 N_PAIRS = N_HEADS // 2
 SCALE = 1.0 / math.sqrt(HD)
 FAR = 1.0e30
@@ -32,6 +30,8 @@ FLOPS = 2 * (2 * B * H * S * S * HD) + 2 * B * S * D * D
 
 E_START = {3: 0, 2: 512, 1: 1024, 0: 1280}
 E_COLS = 1536
+X_START = {3: 0, 2: 512, 0: 896, 1: 1024}
+X_COLS = 1280
 
 SCORE_BANKS = {"s_a": (3,), "s_b": (2, 0), "s_c": (1,)}
 SCORE_COL = {3: 0, 2: 0, 0: 384, 1: 0}
@@ -130,8 +130,7 @@ def tile_alibiattention_pa_kernel(tc, q, k, v, w_out, b_out, out):
         qkT_banks = {}
         qkT_tiles = {}
         score_banks = {}
-        lowest_tiles = {}
-        negmax_tiles = {}
+        x_tiles = {}
         rowsums = {}
         rinv_tiles = {}
         eT_high_banks = {}
@@ -251,32 +250,36 @@ def tile_alibiattention_pa_kernel(tc, q, k, v, w_out, b_out, out):
             nc.scalar.copy(out=qkT[:], in_=qkT_banks[i][:])
             qkT_tiles[i] = qkT
 
-        def row_maxima(i, tag):
-            blocks = SCORE_BANKS[tag]
-            lowest = work.tile([P, len(blocks)], F32, name="lowest_" + tag)
-            for j, qi in enumerate(blocks):
-                nc.vector.tensor_reduce(
-                    out=lowest[:, j : j + 1], in_=score_banks[(i, qi)], axis=AX.X, op=ALU.max, negate=True
+        def scale_and_min(i, tag):
+            if i not in x_tiles:
+                x_new = work.tile([P, X_COLS], F32)
+                negmax_new = work.tile([P, QB], F32)
+                x_tiles[i] = (x_new, negmax_new)
+            x, negmax = x_tiles[i]
+            for qi in SCORE_BANKS[tag]:
+                nc.vector.tensor_scalar(
+                    out=x[:, X_START[qi] : X_START[qi] + (qi + 1) * P],
+                    in0=score_banks[(i, qi)],
+                    scalar1=-SCALE,
+                    scalar2=None,
+                    op0=ALU.mult,
+                    op1=ALU.min,
+                    accum_out=negmax[:, qi : qi + 1],
                 )
-            lowest_tiles[(i, tag)] = lowest
-
-        def exp_bias(i, tag):
-            negmax = work.tile([P, len(SCORE_BANKS[tag])], F32, name="negmax_" + tag)
-            nc.gpsimd.tensor_scalar(out=negmax[:], in0=lowest_tiles[(i, tag)][:], scalar1=SCALE, scalar2=0.0, op0=ALU.mult, op1=ALU.add)
-            negmax_tiles[(i, tag)] = negmax
 
         def exponentials(i, tag):
             if i not in rowsums:
                 rowsum_new = work.tile([P, QB], F32, bufs=6)
                 rowsums[i] = rowsum_new
+            x, negmax = x_tiles[i]
             e_sb = e_tiles[i % 3]
-            for j, qi in enumerate(SCORE_BANKS[tag]):
+            for qi in SCORE_BANKS[tag]:
                 nc.scalar.activation(
                     out=e_sb[:, E_START[qi] : E_START[qi] + (qi + 1) * P],
-                    in_=score_banks[(i, qi)],
+                    in_=x[:, X_START[qi] : X_START[qi] + (qi + 1) * P],
                     func=ACT.Exp,
-                    scale=SCALE,
-                    bias=negmax_tiles[(i, tag)][:, j : j + 1],
+                    scale=-1.0,
+                    bias=negmax[:, qi : qi + 1],
                     accum_out=rowsums[i][:, qi : qi + 1],
                 )
 
@@ -410,15 +413,12 @@ def tile_alibiattention_pa_kernel(tc, q, k, v, w_out, b_out, out):
             if live(s):
                 exponentials(s, "s_a")
                 exponentials(s, "s_b")
-            if live(s + 1):
-                masks(s + 1, "s_a")
-            if 0 <= quarter < N_QUARTERS:
-                transpose_a(quarter, a_bank)
-            if live(s):
                 exponentials(s, "s_c")
             if 0 <= quarter < N_QUARTERS:
+                transpose_a(quarter, a_bank)
                 regroup_a(quarter, nc.scalar.copy)
             if live(s + 1):
+                masks(s + 1, "s_a")
                 masks(s + 1, "s_b")
                 products(s + 1, "s_a")
             if live(s - 3):
@@ -436,15 +436,12 @@ def tile_alibiattention_pa_kernel(tc, q, k, v, w_out, b_out, out):
             if live(s):
                 quantise_v(s)
             if live(s + 1):
-                row_maxima(s + 1, "s_a")
-                exp_bias(s + 1, "s_a")
+                scale_and_min(s + 1, "s_a")
             if live(s - 3):
-                normalise(s - 3)
+                normalise(s - 3, (0, 1))
             if live(s + 1):
-                row_maxima(s + 1, "s_b")
-                exp_bias(s + 1, "s_b")
-                row_maxima(s + 1, "s_c")
-                exp_bias(s + 1, "s_c")
+                scale_and_min(s + 1, "s_b")
+                scale_and_min(s + 1, "s_c")
             if 0 <= tile_now < N_TILES:
                 add_bias_and_store(tile_now)
             if 0 <= quarter - 1 < N_QUARTERS:
@@ -458,6 +455,8 @@ def tile_alibiattention_pa_kernel(tc, q, k, v, w_out, b_out, out):
             if live(s - 1):
                 regroup_e(s - 1, 1, nc.scalar.copy)
                 regroup_e(s - 1, 0, nc.scalar.copy)
+            if live(s - 3):
+                normalise_on_scalar(s - 3, (2, 3))
             if 0 <= s - 1 - W_LAG < W_PIECES:
                 regroup_w(s - 1 - W_LAG)
             if live(s + 3):

@@ -51,7 +51,7 @@ def tile_alibiattention_pa_kernel(tc, q, k, v, w_out, b_out, out):
     with ExitStack() as ctx:
         ctx.enter_context(tc.manual_schedule())
         const = ctx.enter_context(tc.tile_pool(name="const", bufs=1))
-        loads = ctx.enter_context(tc.tile_pool(name="loads", bufs=LOAD_AHEAD + 3))
+        loads = ctx.enter_context(tc.tile_pool(name="loads", bufs=LOAD_AHEAD + 5))
         work = ctx.enter_context(tc.tile_pool(name="work", bufs=3))
         psum = ctx.enter_context(tc.psum_pool(name="psum", bufs=1))
 
@@ -83,6 +83,8 @@ def tile_alibiattention_pa_kernel(tc, q, k, v, w_out, b_out, out):
 
         ident = const.tile([P, P], BF16)
         make_identity(nc, ident[:])
+        zeros = const.tile([P, P], F32)
+        nc.vector.memset(zeros[:], 0.0)
         ident_f32 = const.tile([P, P], F32)
         make_identity(nc, ident_f32[:])
 
@@ -117,13 +119,7 @@ def tile_alibiattention_pa_kernel(tc, q, k, v, w_out, b_out, out):
                 pad = E_START[qi] + (qi + 1) * P
                 nc.gpsimd.memset(e_sb[:, pad : pad + P].bitcast(F32), 0.0)
             e_tiles.append(e_sb)
-        zeros = const.tile([P, P], F32)
-        nc.vector.memset(zeros[:], 0.0)
-
         eT_low = psum.tile([P, HALVES, 2, P], F32, tag="eT_low")
-        for block in range(2):
-            nc.tensor.transpose(eT_low[:, 1, block, :], zeros[:], ident_f32[:])
-
         w_codes = const.tile([P, GROUPS, D], U32, align_bytes=64)
         w_scales = const.tile([P, GROUPS, D], U8, align_bytes=64)
 
@@ -211,11 +207,15 @@ def tile_alibiattention_pa_kernel(tc, q, k, v, w_out, b_out, out):
                     nc.tensor.transpose(wT[:, j, u, :], words[:, w0 : w0 + P], ident_f32[:])
             wT_banks[piece] = wT
 
-        def attend(i, tag="o"):
+        def zero_low_bank():
+            for block in range(2):
+                nc.tensor.transpose(eT_low[:, 1, block, :], zeros[:], ident_f32[:])
+
+        def attend(i, tag="o", blocks=range(QB)):
             e_codes, e_scales = e_operands[i]
             v_codes, v_scales = v_operands[i]
             o_ps = psum.tile([P, QB, HD], F32, tag=tag)
-            for qi in range(QB):
+            for qi in blocks:
                 cols = slice(qi * P, (qi + 1) * P)
                 nc.tensor.matmul_mx(
                     out=o_ps[:, qi, :],
@@ -269,7 +269,7 @@ def tile_alibiattention_pa_kernel(tc, q, k, v, w_out, b_out, out):
 
         def exponentials(i, tag):
             if i not in rowsums:
-                rowsum_new = work.tile([P, QB], F32, bufs=6)
+                rowsum_new = work.tile([P, QB], F32, bufs=8)
                 rowsums[i] = rowsum_new
             x, negmax = x_tiles[i]
             e_sb = e_tiles[i % 3]
@@ -317,7 +317,7 @@ def tile_alibiattention_pa_kernel(tc, q, k, v, w_out, b_out, out):
             v_operands[i] = (v_codes, v_scales)
 
         def invert_rowsum(i):
-            rinv = work.tile([P, QB], F32)
+            rinv = work.tile([P, QB], F32, bufs=6)
             nc.vector.reciprocal(out=rinv[:], in_=rowsums[i][:])
             rinv_tiles[i] = rinv
 
@@ -374,10 +374,7 @@ def tile_alibiattention_pa_kernel(tc, q, k, v, w_out, b_out, out):
             gw = work.tile([P, 2 * P * PACK], BF16, align_bytes=64)
             dst = gw[:].bitcast(F32).rearrange("p (j n u) -> p j n u", j=2, u=HALVES)
             src = wT_banks[piece][:].rearrange("p j u n -> p j n u")
-            if piece % 2 == 0:
-                nc.scalar.copy(out=dst, in_=src)
-            else:
-                nc.vector.tensor_copy(out=dst, in_=src)
+            nc.scalar.copy(out=dst, in_=src)
             gw_tiles[piece] = gw
 
         def quantise_w(piece):
@@ -401,70 +398,69 @@ def tile_alibiattention_pa_kernel(tc, q, k, v, w_out, b_out, out):
                 nc.vector.tensor_tensor(out=out_sb[:], in0=acc_banks[r][:], in1=bias[:, n_cols], op=ALU.add)
             nc.sync.dma_start(out=out[b, tb * P : (tb + 1) * P, n_cols], in_=out_sb[:])
 
-        A_LAG = PACK + 3
+        A_LAG = PACK + 5
         W_LAG = 2
-        P_LAG = H + 5
+        P_LAG = H + 6
         a_bank = None
-        for s in range(-3, N_HEADS - 1):
+        for s in range(-3, N_HEADS):
             quarter = s - A_LAG
             tile_now = s - P_LAG
             if live(s + 3) and (s + 3) % 2 == 0 and (s + 3) // 2 + LOAD_AHEAD < N_PAIRS:
                 load_pair((s + 3) // 2 + LOAD_AHEAD)
             if live(s):
-                exponentials(s, "s_a")
-                exponentials(s, "s_b")
-                exponentials(s, "s_c")
+                scale_and_min(s, "s_c")
+                scale_and_min(s, "s_a")
+                scale_and_min(s, "s_b")
+            if live(s - 5):
+                normalise(s - 5, (0, 1, 2, 3) if tile_now < 0 else (0, 1))
             if 0 <= quarter < N_QUARTERS:
                 transpose_a(quarter, a_bank)
+            if live(s - 2):
+                transpose_e(s - 2)
+            if live(s + 2):
+                copy_qk(s + 2)
+            if 0 <= quarter < N_QUARTERS:
                 regroup_a(quarter, nc.scalar.copy)
+            if 0 <= s - 1 - W_LAG < W_PIECES:
+                regroup_w(s - 1 - W_LAG)
+            if live(s - 5):
+                normalise_on_scalar(s - 5, () if tile_now < 0 else (2, 3))
             if live(s + 1):
                 masks(s + 1, "s_a")
-                masks(s + 1, "s_b")
                 products(s + 1, "s_a")
-            if live(s - 3):
-                attend(s - 3)
-            if 0 <= tile_now < N_TILES:
-                project(tile_now, "acc")
-            if live(s + 1):
+                masks(s + 1, "s_b")
                 products(s + 1, "s_b")
                 a_bank = masks(s + 1, "s_c")
                 products(s + 1, "s_c")
-            if live(s + 2):
-                copy_qk(s + 2)
+            if 0 <= tile_now - 1 < N_TILES:
+                add_bias_and_store(tile_now - 1)
             if live(s - 2):
-                quantise_e(s - 2)
+                regroup_e(s - 2, 1, nc.scalar.copy)
+                regroup_e(s - 2, 0, nc.scalar.copy)
             if live(s):
-                quantise_v(s)
-            if live(s + 1):
-                scale_and_min(s + 1, "s_a")
+                exponentials(s, "s_c")
+                exponentials(s, "s_a")
+                exponentials(s, "s_b")
             if live(s - 3):
-                normalise(s - 3, (0, 1))
-            if live(s + 1):
-                scale_and_min(s + 1, "s_b")
-                scale_and_min(s + 1, "s_c")
-            if 0 <= tile_now < N_TILES:
-                add_bias_and_store(tile_now)
-            if 0 <= quarter - 1 < N_QUARTERS:
-                quantise_a(quarter - 1)
+                quantise_e(s - 3)
+                quantise_v(s - 3)
+            if 0 <= quarter < N_QUARTERS:
+                quantise_a(quarter)
             if 0 <= s - 2 - W_LAG < W_PIECES:
                 quantise_w(s - 2 - W_LAG)
-            if live(s + 1):
-                regroup_v(s + 1)
             if live(s - 2):
+                regroup_v(s - 2)
                 invert_rowsum(s - 2)
-            if live(s - 1):
-                regroup_e(s - 1, 1, nc.scalar.copy)
-                regroup_e(s - 1, 0, nc.scalar.copy)
-            if live(s - 3):
-                normalise_on_scalar(s - 3, (2, 3))
-            if 0 <= s - 1 - W_LAG < W_PIECES:
-                regroup_w(s - 1 - W_LAG)
-            if live(s + 3):
-                transpose_qk(s + 3)
-            if live(s):
-                transpose_e(s)
+            if live(s - 4):
+                attend(s - 4)
+            if 0 <= tile_now < N_TILES:
+                project(tile_now, "acc")
             if 0 <= s - W_LAG < W_PIECES:
                 transpose_w(s - W_LAG)
+            if live(s + 3):
+                transpose_qk(s + 3)
+            if s == -2:
+                zero_low_bank()
 
         SC, VC = nc.scalar.copy, nc.vector.tensor_copy
         L = N_HEADS - 1
@@ -473,74 +469,73 @@ def tile_alibiattention_pa_kernel(tc, q, k, v, w_out, b_out, out):
             bank = psum.tile([P, BANK], F32, tag=tag)
             return bank
 
-        exponentials(L, "s_a")
-        regroup_e(L - 1, 1, SC)
-        exponentials(L, "s_b")
-        transpose_a(24, a_bank)
-        x = new_bank("qkT")
-        transpose_a(25, x, 0)
-        transpose_a(26, x, 1)
-        exponentials(L, "s_c")
-        attend(L - 3)
-        project(18, "acc")
+        transpose_e(L - 1)
+        regroup_v(L - 1)
+        regroup_v(L)
         quantise_e(L - 2)
+        quantise_v(L - 2)
+        quantise_v(L - 1)
         quantise_v(L)
+        normalise(L - 4)
+        attend(L - 3, "s_a")
+        attend(L - 2, "s_b")
+        transpose_a(23, a_bank)
         regroup_e(L - 1, 0, SC)
-        invert_rowsum(L - 2)
+        regroup_e(L - 1, 1, VC)
+        project(18, "qkT")
         invert_rowsum(L - 1)
-        attend(L - 2, "s_a")
+        invert_rowsum(L)
         transpose_e(L)
-        normalise(L - 3)
+        x = new_bank("o")
+        transpose_a(24, x, 0)
+        transpose_a(25, x, 1)
+        normalise_on_scalar(L - 3, range(QB))
         quantise_e(L - 1)
-        project(19, "s_b")
+        add_bias_and_store(17)
+        normalise(L - 2)
+        regroup_a(23, SC)
+        project(19, "acc")
+        attend(L - 1, "s_a")
         regroup_e(L, 1, SC)
         regroup_e(L, 0, VC)
-        attend(L - 1, "o")
-        normalise_on_scalar(L - 2, range(QB))
         quantise_e(L)
         regroup_a(24, SC)
         regroup_a(25, SC)
-        regroup_a(26, SC)
-        invert_rowsum(L)
-        project(20, "eT_high")
-        attend(L, "s_a")
-        normalise(L - 1)
-        normalise(L, (0, 1))
-        normalise_on_scalar(L, (2, 3))
+        attend(L, "s_b")
+        normalise_on_scalar(L - 1, range(QB))
         add_bias_and_store(18)
-        y = new_bank("acc")
-        z = new_bank("s_c")
-        transpose_a(28, z, 0)
-        transpose_a(29, z, 1)
-        transpose_a(30, x, 0)
-        transpose_a(31, x, 1)
-        transpose_a(27, y, 0)
-        regroup_a(28, VC)
-        regroup_a(30, SC)
-        regroup_a(29, VC)
-        regroup_a(31, SC)
-        project(21, "o")
+        y = new_bank("s_c")
+        transpose_a(26, y, 0)
+        transpose_a(27, y, 1)
+        project(20, "eT_high")
         quantise_a(23)
         quantise_a(24)
-        quantise_a(28)
-        quantise_a(25)
-        quantise_a(29)
+        normalise(L)
+        add_bias_and_store(19)
+        regroup_a(26, SC)
         regroup_a(27, SC)
-        quantise_a(26)
-        quantise_a(30)
-        quantise_a(27)
-        quantise_a(31)
-        add_bias_and_store(19, True)
-        add_bias_and_store(20)
-        project(24, "s_a")
-        project(25, "s_c")
-        add_bias_and_store(21, True)
-        project(22, "s_b")
-        project(23, "eT_high")
-        add_bias_and_store(24)
-        add_bias_and_store(25, True)
-        add_bias_and_store(22)
-        add_bias_and_store(23, True)
-        for j, r in enumerate(range(26, 32)):
-            project(r, ("qkT", "acc", "o", "s_a", "s_c", "s_b", "eT_high")[j % 7])
-            add_bias_and_store(r, j % 2 == 1)
+        z = new_bank("o")
+        w = new_bank("qkT")
+        transpose_a(28, z, 0)
+        transpose_a(29, z, 1)
+        transpose_a(30, w, 0)
+        transpose_a(31, w, 1)
+        project(21, "acc")
+        for q in (25, 26, 27):
+            quantise_a(q)
+        add_bias_and_store(20, True)
+        regroup_a(28, SC)
+        regroup_a(29, SC)
+        regroup_a(30, VC)
+        regroup_a(31, VC)
+        project(22, "s_a")
+        project(23, "s_b")
+        for q in (28, 29, 30, 31):
+            quantise_a(q)
+        add_bias_and_store(21)
+        add_bias_and_store(22, True)
+        add_bias_and_store(23)
+        tags = ("eT_high", "s_c", "o", "acc", "qkT", "s_a", "s_b", "eT_high")
+        for j, r in enumerate(range(24, 32)):
+            project(r, tags[j])
+            add_bias_and_store(r, r in (25,))

@@ -11,7 +11,6 @@ U8 = mybir.dt.uint8
 FP8X4 = mybir.dt.float8_e4m3fn_x4
 ALU = mybir.AluOpType
 ACT = mybir.ActivationFunctionType
-AX = mybir.AxisListType
 
 B, H, S, HD = 4, 8, 512, 128
 D = H * HD
@@ -28,18 +27,30 @@ FAR = 1.0e30
 
 FLOPS = 2 * (2 * B * H * S * S * HD) + 2 * B * S * D * D
 
-E_START = {3: 0, 2: 512, 1: 1024, 0: 1280}
-E_COLS = 1536
-X_START = {3: 0, 2: 512, 0: 896, 1: 1024}
-X_COLS = 1280
-
-SCORE_BANKS = {"s_a": (3,), "s_b": (2, 0), "s_c": (1,)}
-SCORE_COL = {3: 0, 2: 0, 0: 384, 1: 0}
 LOAD_AHEAD = 3
 W_PIECES = GROUPS * (D // P // 2)
 N_HALVES = D // BANK
 N_TILES = B * QB * N_HALVES
 N_QUARTERS = B * GROUPS * QB
+
+SCORE_BANKS = (("s_a", (3,)), ("s_b", (2, 0)), ("s_c", (1,)))
+
+
+def n_keys(qi):
+    return (qi + 1) * P
+
+
+def x_cols(qi):
+    start = sum(n_keys(i) for i in range(qi))
+    return slice(start, start + n_keys(qi))
+
+
+def n_groups(qi):
+    return -(-n_keys(qi) // 256)
+
+
+def e_start(qi):
+    return 256 * sum(n_groups(i) for i in range(qi))
 
 
 def live(i):
@@ -51,35 +62,39 @@ def tile_alibiattention_pa_kernel(tc, q, k, v, w_out, b_out, out):
     with ExitStack() as ctx:
         ctx.enter_context(tc.manual_schedule())
         const = ctx.enter_context(tc.tile_pool(name="const", bufs=1))
-        loads = ctx.enter_context(tc.tile_pool(name="loads", bufs=LOAD_AHEAD + 5))
+        loads = ctx.enter_context(tc.tile_pool(name="loads", bufs=LOAD_AHEAD + 6))
         work = ctx.enter_context(tc.tile_pool(name="work", bufs=3))
         psum = ctx.enter_context(tc.psum_pool(name="psum", bufs=1))
 
         pair_tiles = {}
 
-        def load_pair(pair):
+        def load_qk(pair, heads=((0, 2),)):
             b, h0 = pair // (H // 2), 2 * (pair % (H // 2))
             q_sb = loads.tile([P, 2, QB, HD], BF16)
             k_sb = loads.tile([P, 2, QB, HD], BF16)
-            v_sb = loads.tile([P, 2, QB, HD], BF16)
-            heads = ((0, 2),) if pair else ((0, 1), (1, 2))
             for lo, hi in heads:
                 for dst, src in ((q_sb, q), (k_sb, k)):
                     nc.sync.dma_start(
                         out=dst[:, lo:hi], in_=src[b, h0 + lo : h0 + hi].rearrange("h (t p) d -> p h t d", p=P)
                     )
+            pair_tiles[pair] = [q_sb, k_sb]
+
+        def load_v(pair):
+            b, h0 = pair // (H // 2), 2 * (pair % (H // 2))
+            v_sb = loads.tile([P, 2, QB, HD], BF16)
             nc.sync.dma_start(
                 out=v_sb[:].rearrange("p h (u e) d -> p h u (e d)", e=2),
                 in_=v[b, h0 : h0 + 2].rearrange("h (u p e) d -> p h u (e d)", p=P, e=2),
             )
-            pair_tiles[pair] = (q_sb, k_sb, v_sb)
+            pair_tiles[pair].append(v_sb)
 
-        for pair in range(LOAD_AHEAD):
-            load_pair(pair)
+        load_qk(0, ((0, 1), (1, 2)))
+        load_qk(1)
+        load_v(0)
+        load_qk(2)
+        load_v(1)
         w_sb = const.tile([P, D // P, D], BF16)
-        nc.sync.dma_start(out=w_sb[:], in_=w_out.rearrange("(nb p) f -> p nb f", p=P))
         bias = const.tile([P, D], BF16)
-        nc.sync.dma_start(out=bias[:], in_=b_out.partition_broadcast(P))
 
         ident = const.tile([P, P], BF16)
         make_identity(nc, ident[:])
@@ -107,19 +122,20 @@ def tile_alibiattention_pa_kernel(tc, q, k, v, w_out, b_out, out):
         )
         nc.vector.tensor_scalar_mul(out=maskT[:], in0=maskT[:], scalar1=math.sqrt(HD))
 
+        e_tiles = []
+        for turn in range(3):
+            e_sb = const.tile([P, e_start(QB)], BF16, name="e_sb%d" % turn)
+            for qi in (0, 2):
+                pad = e_start(qi) + n_keys(qi)
+                nc.gpsimd.memset(e_sb[:, pad : pad + P].bitcast(F32), 0.0)
+            e_tiles.append(e_sb)
+
         grouped_e = []
         for parity in range(2):
             ge = const.tile([P, S * PACK], BF16, name="ge%d" % parity, align_bytes=64)
-            nc.gpsimd.memset(ge[:].bitcast(F32), 0.0)
             grouped_e.append(ge)
-        e_tiles = []
-        for turn in range(3):
-            e_sb = const.tile([P, E_COLS], BF16, name="e_sb%d" % turn)
-            for qi in (2, 0):
-                pad = E_START[qi] + (qi + 1) * P
-                nc.gpsimd.memset(e_sb[:, pad : pad + P].bitcast(F32), 0.0)
-            e_tiles.append(e_sb)
         eT_low = psum.tile([P, HALVES, 2, P], F32, tag="eT_low")
+
         w_codes = const.tile([P, GROUPS, D], U32, align_bytes=64)
         w_scales = const.tile([P, GROUPS, D], U8, align_bytes=64)
 
@@ -129,7 +145,7 @@ def tile_alibiattention_pa_kernel(tc, q, k, v, w_out, b_out, out):
         x_tiles = {}
         rowsums = {}
         rinv_tiles = {}
-        eT_high_banks = {}
+        eT_banks = {}
         e_operands = {}
         gv_tiles = {}
         v_operands = {}
@@ -142,52 +158,63 @@ def tile_alibiattention_pa_kernel(tc, q, k, v, w_out, b_out, out):
         gw_tiles = {}
         acc_banks = {}
 
-        def transpose_qk(i):
-            q_sb, k_sb, v_sb = pair_tiles[i // 2]
-            qkT_ps = psum.tile([P, 2, S], BF16, tag="qkT")
+        def transpose_qk(i, tag="qkT"):
+            q_sb, k_sb = pair_tiles[i // 2][0:2]
+            qkT_ps = psum.tile([P, 2, S], BF16, tag=tag)
             for which, src in enumerate((q_sb, k_sb)):
                 for t in range(QB):
                     nc.tensor.transpose(qkT_ps[:, which, t * P : (t + 1) * P], src[:, i % 2, t, :], ident[:])
             qkT_banks[i] = qkT_ps
 
-        def masks(i, tag):
-            blocks = SCORE_BANKS[tag]
+        def masks(i, bank_no):
+            tag, blocks = SCORE_BANKS[bank_no]
             bank = psum.tile([P, BANK], F32, tag=tag)
+            col = 0
             for qi in blocks:
-                col = SCORE_COL[qi]
-                score_banks[(i, qi)] = bank[:, col : col + (qi + 1) * P]
+                score_banks[(i, qi)] = bank[:, col : col + n_keys(qi)]
                 for kb in range(qi + 1):
                     nc.tensor.matmul(
-                        out=bank[:, col + kb * P : col + (kb + 1) * P],
+                        out=bank[:, col : col + P],
                         lhsT=maskT[:, qi - kb, :],
                         rhs=ident_f32[:],
                         is_transpose=True,
-                        start=(qi == blocks[0] and kb == 0),
+                        start=(col == 0),
                         stop=False,
                     )
+                    col += P
             return bank
 
-        def products(i, tag):
+        def products(i, bank_no):
+            blocks = SCORE_BANKS[bank_no][1]
             qkT = qkT_tiles[i]
-            blocks = SCORE_BANKS[tag]
             for qi in blocks:
                 nc.tensor.matmul(
                     out=score_banks[(i, qi)],
                     lhsT=qkT[:, 0, qi * P : (qi + 1) * P],
-                    rhs=qkT[:, 1, 0 : (qi + 1) * P],
+                    rhs=qkT[:, 1, 0 : n_keys(qi)],
                     start=False,
                     stop=(qi == blocks[-1]),
                 )
 
-        def transpose_e(i):
+        def transpose_e(i, half, tag=None):
             e_words = e_tiles[i % 3][:].bitcast(F32)
-            eT_high = psum.tile([P, 2, HALVES, P], F32, tag="eT_high")
-            for qi in range(QB):
-                for u in range((qi + 2) // 2):
-                    dst = eT_low[:, u, qi, :] if qi < 2 else eT_high[:, qi - 2, u, :]
-                    w0 = E_START[qi] // 2 + u * P
-                    nc.tensor.transpose(dst, e_words[:, w0 : w0 + P], ident_f32[:])
-            eT_high_banks[i] = eT_high
+            if half == 0 and tag is None:
+                bank = eT_low
+            else:
+                bank = psum.tile([P, HALVES, 2, P], F32, tag=tag or "eT_high")
+            for b in range(2):
+                qi = 2 * half + b
+                for g in range(n_groups(qi)):
+                    w0 = e_start(qi) // 2 + g * P
+                    nc.tensor.transpose(bank[:, g, b, :], e_words[:, w0 : w0 + P], ident_f32[:])
+                if tag:
+                    for g in range(n_groups(qi), HALVES):
+                        nc.tensor.transpose(bank[:, g, b, :], zeros[:], ident_f32[:])
+            eT_banks[(i, half)] = bank
+
+        def zero_low_bank():
+            for block in range(2):
+                nc.tensor.transpose(eT_low[:, 1, block, :], zeros[:], ident_f32[:])
 
         def transpose_a(quarter, bank, half=1):
             group, qi = quarter // QB, quarter % QB
@@ -207,26 +234,21 @@ def tile_alibiattention_pa_kernel(tc, q, k, v, w_out, b_out, out):
                     nc.tensor.transpose(wT[:, j, u, :], words[:, w0 : w0 + P], ident_f32[:])
             wT_banks[piece] = wT
 
-        def zero_low_bank():
-            for block in range(2):
-                nc.tensor.transpose(eT_low[:, 1, block, :], zeros[:], ident_f32[:])
-
         def attend(i, tag="o", blocks=range(QB)):
-            e_codes, e_scales = e_operands[i]
             v_codes, v_scales = v_operands[i]
             o_ps = psum.tile([P, QB, HD], F32, tag=tag)
             for qi in blocks:
-                cols = slice(qi * P, (qi + 1) * P)
+                e_codes, e_scales = e_operands[(i, qi)]
                 nc.tensor.matmul_mx(
                     out=o_ps[:, qi, :],
-                    lhsT=e_codes[:, cols].bitcast(FP8X4),
-                    lhsT_scale=e_scales[:, cols],
+                    lhsT=e_codes.bitcast(FP8X4),
+                    lhsT_scale=e_scales,
                     rhs=v_codes[:].bitcast(FP8X4),
                     rhs_scale=v_scales[:],
                     start=True,
                     stop=True,
                 )
-            o_banks[i] = o_ps
+                o_banks[(i, qi)] = o_ps
 
         def project(r, tag=None, groups=range(GROUPS)):
             b, tb, nh = r // (QB * N_HALVES), (r // N_HALVES) % QB, r % N_HALVES
@@ -246,19 +268,19 @@ def tile_alibiattention_pa_kernel(tc, q, k, v, w_out, b_out, out):
                 )
 
         def copy_qk(i):
-            qkT = work.tile([P, 2, S], BF16, bufs=4)
+            qkT = work.tile([P, 2, S], BF16, bufs=9)
             nc.scalar.copy(out=qkT[:], in_=qkT_banks[i][:])
             qkT_tiles[i] = qkT
 
-        def scale_and_min(i, tag):
+        def scale_and_min(i, bank_no):
             if i not in x_tiles:
-                x_new = work.tile([P, X_COLS], F32)
+                x_new = work.tile([P, x_cols(QB - 1).stop], F32)
                 negmax_new = work.tile([P, QB], F32)
                 x_tiles[i] = (x_new, negmax_new)
             x, negmax = x_tiles[i]
-            for qi in SCORE_BANKS[tag]:
+            for qi in SCORE_BANKS[bank_no][1]:
                 nc.vector.tensor_scalar(
-                    out=x[:, X_START[qi] : X_START[qi] + (qi + 1) * P],
+                    out=x[:, x_cols(qi)],
                     in0=score_banks[(i, qi)],
                     scalar1=-SCALE,
                     scalar2=None,
@@ -267,16 +289,15 @@ def tile_alibiattention_pa_kernel(tc, q, k, v, w_out, b_out, out):
                     accum_out=negmax[:, qi : qi + 1],
                 )
 
-        def exponentials(i, tag):
+        def exponentials(i, blocks):
             if i not in rowsums:
                 rowsum_new = work.tile([P, QB], F32, bufs=8)
                 rowsums[i] = rowsum_new
             x, negmax = x_tiles[i]
-            e_sb = e_tiles[i % 3]
-            for qi in SCORE_BANKS[tag]:
+            for qi in blocks:
                 nc.scalar.activation(
-                    out=e_sb[:, E_START[qi] : E_START[qi] + (qi + 1) * P],
-                    in_=x[:, X_START[qi] : X_START[qi] + (qi + 1) * P],
+                    out=e_tiles[i % 3][:, e_start(qi) : e_start(qi) + n_keys(qi)],
+                    in_=x[:, x_cols(qi)],
                     func=ACT.Exp,
                     scale=-1.0,
                     bias=negmax[:, qi : qi + 1],
@@ -284,23 +305,27 @@ def tile_alibiattention_pa_kernel(tc, q, k, v, w_out, b_out, out):
                 )
 
         def regroup_e(i, half, copy):
-            ge_words = grouped_e[i % 2][:].bitcast(F32).rearrange("p (b q u) -> p b q u", b=QB, u=HALVES)
-            src = eT_high_banks[i][:].rearrange("p b u q -> p b q u") if half else eT_low[:].rearrange("p u b q -> p b q u")
-            copy(out=ge_words[:, 2 * half : 2 * half + 2], in_=src)
+            ge_words = grouped_e[i % 2][:].bitcast(F32).rearrange("p (b q g) -> p b q g", b=QB, g=HALVES)
+            copy(
+                out=ge_words[:, 2 * half : 2 * half + 2], in_=eT_banks[(i, half)][:].rearrange("p g b q -> p b q g")
+            )
 
-        def quantise_e(i):
-            e_codes = work.tile([P, S], U32, align_bytes=64)
-            e_scales = work.tile([P, S], U8, align_bytes=64)
+        def quantise_e(i, lo=0, hi=QB):
+            n = (hi - lo) * P
+            e_codes = work.tile([P, n], U32, align_bytes=64, bufs=4, name="e_codes%d" % n)
+            e_scales = work.tile([P, n], U8, align_bytes=64, bufs=4, name="e_scales%d" % n)
             nc.vector.quantize_mx(
                 out=e_codes[:].bitcast(FP8X4),
                 scales=e_scales[:],
-                in_=grouped_e[i % 2][:],
+                in_=grouped_e[i % 2][:, lo * P * PACK : hi * P * PACK],
             )
-            e_operands[i] = (e_codes, e_scales)
+            for qi in range(lo, hi):
+                cols = slice((qi - lo) * P, (qi - lo + 1) * P)
+                e_operands[(i, qi)] = (e_codes[:, cols], e_scales[:, cols])
 
         def regroup_v(i):
             v_sb = pair_tiles[i // 2][2]
-            gv = work.tile([P, HD, PACK], BF16, align_bytes=64)
+            gv = work.tile([P, HD, PACK], BF16, align_bytes=64, bufs=5)
             nc.vector.tensor_copy(
                 out=gv[:].rearrange("p (c i) t -> p c t i", i=4),
                 in_=v_sb[:, i % 2].rearrange("p t (c i) -> p c t i", i=4),
@@ -309,42 +334,41 @@ def tile_alibiattention_pa_kernel(tc, q, k, v, w_out, b_out, out):
 
         def quantise_v(i):
             gv = gv_tiles[i]
-            v_codes = work.tile([P, HD], U32, align_bytes=64, bufs=4)
-            v_scales = work.tile([P, HD], U8, align_bytes=64, bufs=4)
+            v_codes = work.tile([P, HD], U32, align_bytes=64, bufs=8)
+            v_scales = work.tile([P, HD], U8, align_bytes=64, bufs=8)
             nc.vector.quantize_mx(
                 out=v_codes[:].bitcast(FP8X4), scales=v_scales[:], in_=gv[:].rearrange("p d t -> p (d t)")
             )
             v_operands[i] = (v_codes, v_scales)
 
-        def invert_rowsum(i):
+        def invert_rowsum(i, lo=0, hi=QB):
             rinv = work.tile([P, QB], F32, bufs=6)
-            nc.vector.reciprocal(out=rinv[:], in_=rowsums[i][:])
-            rinv_tiles[i] = rinv
+            nc.vector.reciprocal(out=rinv[:, lo:hi], in_=rowsums[i][:, lo:hi])
+            for qi in range(lo, hi):
+                rinv_tiles[(i, qi)] = rinv
 
-        def normalise(i, blocks=range(QB)):
+        def a_of_head(i):
             group, t = i // PACK, i % PACK
             if group not in a_tiles:
                 a_new = work.tile([P, QB, PACK * HD], BF16)
                 a_tiles[group] = a_new
-            lo, hi = blocks[0], blocks[-1] + 1
+            return a_tiles[group][:, :, t * HD : (t + 1) * HD]
+
+        def normalise(i, lo, hi):
             nc.vector.tensor_tensor(
-                out=a_tiles[group][:, lo:hi, t * HD : (t + 1) * HD],
-                in0=o_banks[i][:, lo:hi],
-                in1=rinv_tiles[i][:, lo:hi].unsqueeze(2).to_broadcast([P, hi - lo, HD]),
+                out=a_of_head(i)[:, lo:hi],
+                in0=o_banks[(i, lo)][:, lo:hi],
+                in1=rinv_tiles[(i, lo)][:, lo:hi].unsqueeze(2).to_broadcast([P, hi - lo, HD]),
                 op=ALU.mult,
             )
 
-        def normalise_on_scalar(i, blocks):
-            group, t = i // PACK, i % PACK
-            if group not in a_tiles:
-                a_new = work.tile([P, QB, PACK * HD], BF16, name="a_new")
-                a_tiles[group] = a_new
-            for qi in blocks:
+        def normalise_on_scalar(i, lo, hi):
+            for qi in range(lo, hi):
                 nc.scalar.activation(
-                    out=a_tiles[group][:, qi, t * HD : (t + 1) * HD],
-                    in_=o_banks[i][:, qi],
+                    out=a_of_head(i)[:, qi],
+                    in_=o_banks[(i, qi)][:, qi],
                     func=ACT.Copy,
-                    scale=rinv_tiles[i][:, qi : qi + 1],
+                    scale=rinv_tiles[(i, qi)][:, qi : qi + 1],
                 )
 
         def regroup_a(quarter, copy):
@@ -358,32 +382,27 @@ def tile_alibiattention_pa_kernel(tc, q, k, v, w_out, b_out, out):
         def quantise_a(quarter):
             group, qi = quarter // QB, quarter % QB
             b, g = group // GROUPS, group % GROUPS
-            if g == 0 and qi == 0:
+            if b not in a_operands:
                 a_codes_new = work.tile([P, GROUPS, S], U32, align_bytes=64, bufs=2)
                 a_scales_new = work.tile([P, GROUPS, S], U8, align_bytes=64, bufs=2)
                 a_operands[b] = (a_codes_new, a_scales_new)
             a_codes, a_scales = a_operands[b]
             cols = slice(qi * P, (qi + 1) * P)
             nc.vector.quantize_mx(
-                out=a_codes[:, g, cols].bitcast(FP8X4),
-                scales=a_scales[:, g, cols],
-                in_=ga_tiles[quarter][:],
+                out=a_codes[:, g, cols].bitcast(FP8X4), scales=a_scales[:, g, cols], in_=ga_tiles[quarter][:]
             )
 
         def regroup_w(piece):
             gw = work.tile([P, 2 * P * PACK], BF16, align_bytes=64)
             dst = gw[:].bitcast(F32).rearrange("p (j n u) -> p j n u", j=2, u=HALVES)
-            src = wT_banks[piece][:].rearrange("p j u n -> p j n u")
-            nc.scalar.copy(out=dst, in_=src)
+            nc.scalar.copy(out=dst, in_=wT_banks[piece][:].rearrange("p j u n -> p j n u"))
             gw_tiles[piece] = gw
 
         def quantise_w(piece):
             g, nb0 = piece // (D // P // 2), 2 * (piece % (D // P // 2))
             cols = slice(nb0 * P, (nb0 + 2) * P)
             nc.vector.quantize_mx(
-                out=w_codes[:, g, cols].bitcast(FP8X4),
-                scales=w_scales[:, g, cols],
-                in_=gw_tiles[piece][:],
+                out=w_codes[:, g, cols].bitcast(FP8X4), scales=w_scales[:, g, cols], in_=gw_tiles[piece][:]
             )
 
         def add_bias_and_store(r, on_gpsimd=False):
@@ -399,48 +418,56 @@ def tile_alibiattention_pa_kernel(tc, q, k, v, w_out, b_out, out):
             nc.sync.dma_start(out=out[b, tb * P : (tb + 1) * P, n_cols], in_=out_sb[:])
 
         A_LAG = PACK + 5
-        W_LAG = 2
+        W_LAG = 5
         P_LAG = H + 6
+        SC, VC = nc.scalar.copy, nc.vector.tensor_copy
+        W_STEP = -1
         a_bank = None
         for s in range(-3, N_HEADS):
             quarter = s - A_LAG
             tile_now = s - P_LAG
-            if live(s + 3) and (s + 3) % 2 == 0 and (s + 3) // 2 + LOAD_AHEAD < N_PAIRS:
-                load_pair((s + 3) // 2 + LOAD_AHEAD)
+            pair = (s + 3) // 2 + LOAD_AHEAD
+            if s % 2 == 1 and pair < N_PAIRS + 1:
+                if pair < N_PAIRS:
+                    load_qk(pair)
+                load_v(pair - 1)
+            if s == W_STEP:
+                nc.sync.dma_start(out=w_sb[:], in_=w_out.rearrange("(nb p) f -> p nb f", p=P))
+                nc.sync.dma_start(out=bias[:], in_=b_out.partition_broadcast(P))
             if live(s):
-                scale_and_min(s, "s_c")
-                scale_and_min(s, "s_a")
-                scale_and_min(s, "s_b")
+                scale_and_min(s, 2)
+                scale_and_min(s, 0)
+                scale_and_min(s, 1)
             if live(s - 5):
-                normalise(s - 5, (0, 1, 2, 3) if tile_now < 0 else (0, 1))
+                normalise(s - 5, 0, QB if tile_now < 0 else 2)
             if 0 <= quarter < N_QUARTERS:
                 transpose_a(quarter, a_bank)
             if live(s - 2):
-                transpose_e(s - 2)
+                transpose_e(s - 2, 0)
+                transpose_e(s - 2, 1)
+            if live(s) and s < 3:
+                exponentials(s, (1, 3, 2, 0))
             if live(s + 2):
                 copy_qk(s + 2)
             if 0 <= quarter < N_QUARTERS:
-                regroup_a(quarter, nc.scalar.copy)
+                regroup_a(quarter, SC)
             if 0 <= s - 1 - W_LAG < W_PIECES:
                 regroup_w(s - 1 - W_LAG)
-            if live(s - 5):
-                normalise_on_scalar(s - 5, () if tile_now < 0 else (2, 3))
+            if live(s - 5) and tile_now >= 0:
+                normalise_on_scalar(s - 5, 2, QB)
             if live(s + 1):
-                masks(s + 1, "s_a")
-                products(s + 1, "s_a")
-                masks(s + 1, "s_b")
-                products(s + 1, "s_b")
-                a_bank = masks(s + 1, "s_c")
-                products(s + 1, "s_c")
+                for bank_no in (2, 0, 1) if quarter < 0 else (0, 1, 2):
+                    bank = masks(s + 1, bank_no)
+                    products(s + 1, bank_no)
+                    if bank_no == 2:
+                        a_bank = bank
             if 0 <= tile_now - 1 < N_TILES:
                 add_bias_and_store(tile_now - 1)
             if live(s - 2):
-                regroup_e(s - 2, 1, nc.scalar.copy)
-                regroup_e(s - 2, 0, nc.scalar.copy)
-            if live(s):
-                exponentials(s, "s_c")
-                exponentials(s, "s_a")
-                exponentials(s, "s_b")
+                regroup_e(s - 2, 1, SC)
+                regroup_e(s - 2, 0, SC)
+            if live(s) and s >= 3:
+                exponentials(s, (1, 3, 2, 0))
             if live(s - 3):
                 quantise_e(s - 3)
                 quantise_v(s - 3)
@@ -462,21 +489,21 @@ def tile_alibiattention_pa_kernel(tc, q, k, v, w_out, b_out, out):
             if s == -2:
                 zero_low_bank()
 
-        SC, VC = nc.scalar.copy, nc.vector.tensor_copy
         L = N_HEADS - 1
 
         def new_bank(tag):
             bank = psum.tile([P, BANK], F32, tag=tag)
             return bank
 
-        transpose_e(L - 1)
+        transpose_e(L - 1, 0)
+        transpose_e(L - 1, 1)
         regroup_v(L - 1)
         regroup_v(L)
         quantise_e(L - 2)
         quantise_v(L - 2)
         quantise_v(L - 1)
         quantise_v(L)
-        normalise(L - 4)
+        normalise(L - 4, 0, QB)
         attend(L - 3, "s_a")
         attend(L - 2, "s_b")
         transpose_a(23, a_bank)
@@ -485,14 +512,15 @@ def tile_alibiattention_pa_kernel(tc, q, k, v, w_out, b_out, out):
         project(18, "qkT")
         invert_rowsum(L - 1)
         invert_rowsum(L)
-        transpose_e(L)
+        transpose_e(L, 0)
+        transpose_e(L, 1)
         x = new_bank("o")
         transpose_a(24, x, 0)
         transpose_a(25, x, 1)
-        normalise_on_scalar(L - 3, range(QB))
+        normalise_on_scalar(L - 3, 0, QB)
         quantise_e(L - 1)
         add_bias_and_store(17)
-        normalise(L - 2)
+        normalise(L - 2, 0, QB)
         regroup_a(23, SC)
         project(19, "acc")
         attend(L - 1, "s_a")
@@ -502,7 +530,7 @@ def tile_alibiattention_pa_kernel(tc, q, k, v, w_out, b_out, out):
         regroup_a(24, SC)
         regroup_a(25, SC)
         attend(L, "s_b")
-        normalise_on_scalar(L - 1, range(QB))
+        normalise_on_scalar(L - 1, 0, QB)
         add_bias_and_store(18)
         y = new_bank("s_c")
         transpose_a(26, y, 0)
@@ -510,7 +538,7 @@ def tile_alibiattention_pa_kernel(tc, q, k, v, w_out, b_out, out):
         project(20, "eT_high")
         quantise_a(23)
         quantise_a(24)
-        normalise(L)
+        normalise(L, 0, QB)
         add_bias_and_store(19)
         regroup_a(26, SC)
         regroup_a(27, SC)

@@ -445,7 +445,7 @@ def tile_alibiattention_pa_kernel(tc, q, k, v, w_out, b_out, out):
             if live(s - 2):
                 transpose_e(s - 2, 0)
                 transpose_e(s - 2, 1)
-            if live(s) and s < 3:
+            if live(s) and s < 2:
                 exponentials(s, (1, 3, 2, 0))
             if live(s + 2):
                 copy_qk(s + 2)
@@ -466,7 +466,7 @@ def tile_alibiattention_pa_kernel(tc, q, k, v, w_out, b_out, out):
             if live(s - 2):
                 regroup_e(s - 2, 1, SC)
                 regroup_e(s - 2, 0, SC)
-            if live(s) and s >= 3:
+            if live(s) and s >= 2:
                 exponentials(s, (1, 3, 2, 0))
             if live(s - 3):
                 quantise_e(s - 3)
@@ -551,7 +551,7 @@ def tile_alibiattention_pa_kernel(tc, q, k, v, w_out, b_out, out):
         project(21, "acc")
         for q in (25, 26, 27):
             quantise_a(q)
-        add_bias_and_store(20, True)
+        add_bias_and_store(20)
         regroup_a(28, SC)
         regroup_a(29, SC)
         regroup_a(30, VC)
@@ -561,9 +561,9 @@ def tile_alibiattention_pa_kernel(tc, q, k, v, w_out, b_out, out):
         for q in (28, 29, 30, 31):
             quantise_a(q)
         add_bias_and_store(21)
-        add_bias_and_store(22, True)
+        add_bias_and_store(22)
         add_bias_and_store(23)
         tags = ("eT_high", "s_c", "o", "acc", "qkT", "s_a", "s_b", "eT_high")
         for j, r in enumerate(range(24, 32)):
             project(r, tags[j])
-            add_bias_and_store(r, r in (25,))
+            add_bias_and_store(r)

@@ -323,13 +323,24 @@ def tile_alibiattention_pa_kernel(tc, q, k, v, w_out, b_out, out):
                 cols = slice((qi - lo) * P, (qi - lo + 1) * P)
                 e_operands[(i, qi)] = (e_codes[:, cols], e_scales[:, cols])
 
-        def regroup_v(i):
+        def regroup_v(i, on_vector=False):
             v_sb = pair_tiles[i // 2][2]
-            gv = work.tile([P, HD, PACK], BF16, align_bytes=64, bufs=5)
-            nc.vector.tensor_copy(
-                out=gv[:].rearrange("p (c i) t -> p c t i", i=4),
-                in_=v_sb[:, i % 2].rearrange("p t (c i) -> p c t i", i=4),
-            )
+            if on_vector:
+                gv = work.tile([P, HD, PACK], BF16, align_bytes=64, bufs=2, name="gv_vector")
+                nc.vector.tensor_copy(
+                    out=gv[:].rearrange("p (c i) t -> p c t i", i=4),
+                    in_=v_sb[:, i % 2].rearrange("p t (c i) -> p c t i", i=4),
+                )
+            else:
+                gv = work.tile([P, HD, PACK], BF16, align_bytes=64, bufs=1)
+                nc.gpsimd.tensor_scalar(
+                    out=gv[:],
+                    in0=v_sb[:, i % 2].rearrange("p t d -> p d t"),
+                    scalar1=1.0,
+                    scalar2=0.0,
+                    op0=ALU.mult,
+                    op1=ALU.add,
+                )
             gv_tiles[i] = gv
 
         def quantise_v(i):
@@ -439,55 +450,63 @@ def tile_alibiattention_pa_kernel(tc, q, k, v, w_out, b_out, out):
                 scale_and_min(s, 0)
                 scale_and_min(s, 1)
             if live(s - 5):
-                normalise(s - 5, 0, QB if tile_now < 0 else 2)
+                normalise(s - 5, 0, QB if tile_now < 0 else 3)
             if 0 <= quarter < N_QUARTERS:
                 transpose_a(quarter, a_bank)
-            if live(s - 2):
-                transpose_e(s - 2, 0)
-                transpose_e(s - 2, 1)
-            if live(s) and s < 2:
+            e_now = s - 1 if s <= 2 else s - 2
+            if s == 3:
+                e_now = -1
+            if live(e_now):
+                transpose_e(e_now, 0)
+                transpose_e(e_now, 1)
+            if live(s) and s < 3:
                 exponentials(s, (1, 3, 2, 0))
-            if live(s + 2):
-                copy_qk(s + 2)
             if 0 <= quarter < N_QUARTERS:
                 regroup_a(quarter, SC)
+            if live(s + 2):
+                copy_qk(s + 2)
             if 0 <= s - 1 - W_LAG < W_PIECES:
                 regroup_w(s - 1 - W_LAG)
             if live(s - 5) and tile_now >= 0:
-                normalise_on_scalar(s - 5, 2, QB)
+                normalise_on_scalar(s - 5, 3, QB)
             if live(s + 1):
                 for bank_no in (2, 0, 1) if quarter < 0 else (0, 1, 2):
-                    bank = masks(s + 1, bank_no)
+                    if s >= 0:
+                        bank = masks(s + 1, bank_no)
                     products(s + 1, bank_no)
                     if bank_no == 2:
                         a_bank = bank
             if 0 <= tile_now - 1 < N_TILES:
                 add_bias_and_store(tile_now - 1)
-            if live(s - 2):
-                regroup_e(s - 2, 1, SC)
-                regroup_e(s - 2, 0, SC)
-            if live(s) and s >= 2:
+            if live(e_now):
+                regroup_e(e_now, 1, SC)
+                regroup_e(e_now, 0, SC)
+            if live(s) and s >= 3:
                 exponentials(s, (1, 3, 2, 0))
             if live(s - 3):
                 quantise_e(s - 3)
-                quantise_v(s - 3)
             if 0 <= quarter < N_QUARTERS:
                 quantise_a(quarter)
             if 0 <= s - 2 - W_LAG < W_PIECES:
                 quantise_w(s - 2 - W_LAG)
             if live(s - 2):
-                regroup_v(s - 2)
                 invert_rowsum(s - 2)
+            if live(s - 3):
+                quantise_v(s - 3)
+            if live(s - 2):
+                regroup_v(s - 2)
             if live(s - 4):
                 attend(s - 4)
             if 0 <= tile_now < N_TILES:
                 project(tile_now, "acc")
             if 0 <= s - W_LAG < W_PIECES:
                 transpose_w(s - W_LAG)
+            if s == -3:
+                zero_low_bank()
+                for bank_no in (2, 0, 1):
+                    bank = masks(0, bank_no)
             if live(s + 3):
                 transpose_qk(s + 3)
-            if s == -2:
-                zero_low_bank()
 
         L = N_HEADS - 1
 
@@ -497,8 +516,8 @@ def tile_alibiattention_pa_kernel(tc, q, k, v, w_out, b_out, out):
 
         transpose_e(L - 1, 0)
         transpose_e(L - 1, 1)
-        regroup_v(L - 1)
-        regroup_v(L)
+        regroup_v(L - 1, True)
+        regroup_v(L, True)
         quantise_e(L - 2)
         quantise_v(L - 2)
         quantise_v(L - 1)

@@ -432,17 +432,16 @@ def tile_alibiattention_pa_kernel(tc, q, k, v, w_out, b_out, out):
         W_LAG = 5
         P_LAG = H + 6
         SC, VC = nc.scalar.copy, nc.vector.tensor_copy
-        W_STEP = -1
         a_bank = None
-        for s in range(-3, N_HEADS):
+        for s in range(-2, N_HEADS):
             quarter = s - A_LAG
             tile_now = s - P_LAG
-            pair = (s + 3) // 2 + LOAD_AHEAD
-            if s % 2 == 1 and pair < N_PAIRS + 1:
+            pair = (s + 2) // 2 + LOAD_AHEAD
+            if s % 2 == 0 and pair < N_PAIRS + 1:
                 if pair < N_PAIRS:
                     load_qk(pair)
                 load_v(pair - 1)
-            if s == W_STEP:
+            if s == 0:
                 nc.sync.dma_start(out=w_sb[:], in_=w_out.rearrange("(nb p) f -> p nb f", p=P))
                 nc.sync.dma_start(out=bias[:], in_=b_out.partition_broadcast(P))
             if live(s):
@@ -451,37 +450,39 @@ def tile_alibiattention_pa_kernel(tc, q, k, v, w_out, b_out, out):
                 scale_and_min(s, 1)
             if live(s - 5):
                 normalise(s - 5, 0, QB if tile_now < 0 else 3)
-            if 0 <= quarter < N_QUARTERS:
-                transpose_a(quarter, a_bank)
-            e_now = s - 1 if s <= 2 else s - 2
-            if s == 3:
-                e_now = -1
-            if live(e_now):
-                transpose_e(e_now, 0)
-                transpose_e(e_now, 1)
-            if live(s) and s < 3:
+            if live(s) and s < 2:
                 exponentials(s, (1, 3, 2, 0))
             if 0 <= quarter < N_QUARTERS:
+                transpose_a(quarter, a_bank)
                 regroup_a(quarter, SC)
             if live(s + 2):
+                transpose_qk(s + 2)
                 copy_qk(s + 2)
+            if live(s - 2):
+                transpose_e(s - 2, 0)
+                transpose_e(s - 2, 1)
             if 0 <= s - 1 - W_LAG < W_PIECES:
                 regroup_w(s - 1 - W_LAG)
             if live(s - 5) and tile_now >= 0:
                 normalise_on_scalar(s - 5, 3, QB)
             if live(s + 1):
-                for bank_no in (2, 0, 1) if quarter < 0 else (0, 1, 2):
-                    if s >= 0:
+                if quarter < 0:
+                    for bank_no in (2, 0, 1):
                         bank = masks(s + 1, bank_no)
-                    products(s + 1, bank_no)
-                    if bank_no == 2:
-                        a_bank = bank
+                        products(s + 1, bank_no)
+                        if bank_no == 2:
+                            a_bank = bank
+                else:
+                    for bank_no in (0, 1, 2):
+                        a_bank = masks(s + 1, bank_no)
+                    for bank_no in (2, 0, 1):
+                        products(s + 1, bank_no)
             if 0 <= tile_now - 1 < N_TILES:
                 add_bias_and_store(tile_now - 1)
-            if live(e_now):
-                regroup_e(e_now, 1, SC)
-                regroup_e(e_now, 0, SC)
-            if live(s) and s >= 3:
+            if live(s - 2):
+                regroup_e(s - 2, 1, SC)
+                regroup_e(s - 2, 0, SC)
+            if live(s) and s >= 2:
                 exponentials(s, (1, 3, 2, 0))
             if live(s - 3):
                 quantise_e(s - 3)
@@ -501,12 +502,8 @@ def tile_alibiattention_pa_kernel(tc, q, k, v, w_out, b_out, out):
                 project(tile_now, "acc")
             if 0 <= s - W_LAG < W_PIECES:
                 transpose_w(s - W_LAG)
-            if s == -3:
+            if s == -1:
                 zero_low_bank()
-                for bank_no in (2, 0, 1):
-                    bank = masks(0, bank_no)
-            if live(s + 3):
-                transpose_qk(s + 3)
 
         L = N_HEADS - 1
 

@@ -406,7 +406,8 @@ def tile_alibiattention_pa_kernel(tc, q, k, v, w_out, b_out, out):
         def regroup_w(piece):
             gw = work.tile([P, 2 * P * PACK], BF16, align_bytes=64)
             dst = gw[:].bitcast(F32).rearrange("p (j n u) -> p j n u", j=2, u=HALVES)
-            nc.scalar.copy(out=dst, in_=wT_banks[piece][:].rearrange("p j u n -> p j n u"))
+            copy = nc.vector.tensor_copy if piece % 2 else nc.scalar.copy
+            copy(out=dst, in_=wT_banks[piece][:].rearrange("p j u n -> p j n u"))
             gw_tiles[piece] = gw
 
         def quantise_w(piece):

import math
from contextlib import ExitStack

import concourse.mybir as mybir
from concourse.masks import make_identity

F32 = mybir.dt.float32
BF16 = mybir.dt.bfloat16
U32 = mybir.dt.uint32
U8 = mybir.dt.uint8
FP8X4 = mybir.dt.float8_e4m3fn_x4
ALU = mybir.AluOpType
ACT = mybir.ActivationFunctionType

B, H, S, HD = 4, 8, 512, 128
D = H * HD
P = 128
PACK = 4
BANK = 512
QB = S // P
HALVES = PACK // 2
GROUPS = H // PACK
N_HEADS = B * H
N_PAIRS = N_HEADS // 2
SCALE = 1.0 / math.sqrt(HD)
FAR = 1.0e30

FLOPS = 2 * (2 * B * H * S * S * HD) + 2 * B * S * D * D

LOAD_AHEAD = 3
W_PIECES = GROUPS * (D // P // 2)
N_HALVES = D // BANK
N_TILES = B * QB * N_HALVES
N_QUARTERS = B * GROUPS * QB

SCORE_BANKS = (("s_a", (3,)), ("s_b", (2, 0)), ("s_c", (1,)))


def n_keys(qi):
    return (qi + 1) * P


def x_cols(qi):
    start = sum(n_keys(i) for i in range(qi))
    return slice(start, start + n_keys(qi))


def n_groups(qi):
    return -(-n_keys(qi) // 256)


def e_start(qi):
    return 256 * sum(n_groups(i) for i in range(qi))


def live(i):
    return 0 <= i < N_HEADS


def tile_alibiattention_pa_kernel(tc, q, k, v, w_out, b_out, out):
    nc = tc.nc
    with ExitStack() as ctx:
        ctx.enter_context(tc.manual_schedule())
        const = ctx.enter_context(tc.tile_pool(name="const", bufs=1))
        loads = ctx.enter_context(tc.tile_pool(name="loads", bufs=LOAD_AHEAD + 6))
        work = ctx.enter_context(tc.tile_pool(name="work", bufs=3))
        psum = ctx.enter_context(tc.psum_pool(name="psum", bufs=1))

        pair_tiles = {}

        def load_qk(pair, heads=((0, 2),)):
            b, h0 = pair // (H // 2), 2 * (pair % (H // 2))
            q_sb = loads.tile([P, 2, QB, HD], BF16)
            k_sb = loads.tile([P, 2, QB, HD], BF16)
            for lo, hi in heads:
                for dst, src in ((q_sb, q), (k_sb, k)):
                    nc.sync.dma_start(
                        out=dst[:, lo:hi], in_=src[b, h0 + lo : h0 + hi].rearrange("h (t p) d -> p h t d", p=P)
                    )
            pair_tiles[pair] = [q_sb, k_sb]

        def load_v(pair):
            b, h0 = pair // (H // 2), 2 * (pair % (H // 2))
            v_sb = loads.tile([P, 2, QB, HD], BF16)
            nc.sync.dma_start(
                out=v_sb[:].rearrange("p h (u e) d -> p h u (e d)", e=2),
                in_=v[b, h0 : h0 + 2].rearrange("h (u p e) d -> p h u (e d)", p=P, e=2),
            )
            pair_tiles[pair].append(v_sb)

        load_qk(0, ((0, 1), (1, 2)))
        load_qk(1)
        load_v(0)
        load_qk(2)
        load_v(1)
        w_sb = const.tile([P, D // P, D], BF16)
        bias = const.tile([P, D], BF16)

        ident = const.tile([P, P], BF16)
        make_identity(nc, ident[:])
        zeros = const.tile([P, P], F32)
        nc.vector.memset(zeros[:], 0.0)
        ident_f32 = const.tile([P, P], F32)
        make_identity(nc, ident_f32[:])

        maskT = const.tile([P, QB, P], F32)
        nc.gpsimd.iota(
            maskT[:],
            pattern=[[-P, QB], [-1, P]],
            base=0,
            channel_multiplier=1,
            allow_small_or_imprecise_dtypes=True,
        )
        nc.gpsimd.affine_select(
            out=maskT[:, 0, :],
            in_=maskT[:, 0, :],
            pattern=[[1, P]],
            compare_op=ALU.is_ge,
            fill=-FAR,
            base=0,
            channel_multiplier=-1,
        )
        nc.vector.tensor_scalar_mul(out=maskT[:], in0=maskT[:], scalar1=math.sqrt(HD))

        e_tiles = []
        for turn in range(3):
            e_sb = const.tile([P, e_start(QB)], BF16, name="e_sb%d" % turn)
            for qi in (0, 2):
                pad = e_start(qi) + n_keys(qi)
                nc.gpsimd.memset(e_sb[:, pad : pad + P].bitcast(F32), 0.0)
            e_tiles.append(e_sb)

        grouped_e = []
        for parity in range(2):
            ge = const.tile([P, S * PACK], BF16, name="ge%d" % parity, align_bytes=64)
            grouped_e.append(ge)
        eT_low = psum.tile([P, HALVES, 2, P], F32, tag="eT_low")

        w_codes = const.tile([P, GROUPS, D], U32, align_bytes=64)
        w_scales = const.tile([P, GROUPS, D], U8, align_bytes=64)

        qkT_banks = {}
        qkT_tiles = {}
        score_banks = {}
        x_tiles = {}
        rowsums = {}
        rinv_tiles = {}
        eT_banks = {}
        e_operands = {}
        gv_tiles = {}
        v_operands = {}
        o_banks = {}
        a_tiles = {}
        aT_banks = {}
        ga_tiles = {}
        a_operands = {}
        wT_banks = {}
        gw_tiles = {}
        acc_banks = {}

        def transpose_qk(i, tag="qkT"):
            q_sb, k_sb = pair_tiles[i // 2][0:2]
            qkT_ps = psum.tile([P, 2, S], BF16, tag=tag)
            for which, src in enumerate((q_sb, k_sb)):
                for t in range(QB):
                    nc.tensor.transpose(qkT_ps[:, which, t * P : (t + 1) * P], src[:, i % 2, t, :], ident[:])
            qkT_banks[i] = qkT_ps

        def masks(i, bank_no):
            tag, blocks = SCORE_BANKS[bank_no]
            bank = psum.tile([P, BANK], F32, tag=tag)
            col = 0
            for qi in blocks:
                score_banks[(i, qi)] = bank[:, col : col + n_keys(qi)]
                for kb in range(qi + 1):
                    nc.tensor.matmul(
                        out=bank[:, col : col + P],
                        lhsT=maskT[:, qi - kb, :],
                        rhs=ident_f32[:],
                        is_transpose=True,
                        start=(col == 0),
                        stop=False,
                    )
                    col += P
            return bank

        def products(i, bank_no):
            blocks = SCORE_BANKS[bank_no][1]
            qkT = qkT_tiles[i]
            for qi in blocks:
                nc.tensor.matmul(
                    out=score_banks[(i, qi)],
                    lhsT=qkT[:, 0, qi * P : (qi + 1) * P],
                    rhs=qkT[:, 1, 0 : n_keys(qi)],
                    start=False,
                    stop=(qi == blocks[-1]),
                )

        def transpose_e(i, half, tag=None):
            e_words = e_tiles[i % 3][:].bitcast(F32)
            if half == 0 and tag is None:
                bank = eT_low
            else:
                bank = psum.tile([P, HALVES, 2, P], F32, tag=tag or "eT_high")
            for b in range(2):
                qi = 2 * half + b
                for g in range(n_groups(qi)):
                    w0 = e_start(qi) // 2 + g * P
                    nc.tensor.transpose(bank[:, g, b, :], e_words[:, w0 : w0 + P], ident_f32[:])
                if tag:
                    for g in range(n_groups(qi), HALVES):
                        nc.tensor.transpose(bank[:, g, b, :], zeros[:], ident_f32[:])
            eT_banks[(i, half)] = bank

        def zero_low_bank():
            for block in range(2):
                nc.tensor.transpose(eT_low[:, 1, block, :], zeros[:], ident_f32[:])

        def transpose_a(quarter, bank, half=1):
            group, qi = quarter // QB, quarter % QB
            words = a_tiles[group][:, qi, :].bitcast(F32)
            for u in range(HALVES):
                col = (HALVES * half + u) * P
                nc.tensor.transpose(bank[:, col : col + P], words[:, u * P : (u + 1) * P], ident_f32[:])
            aT_banks[quarter] = bank[:, half * BANK // 2 : (half + 1) * BANK // 2]

        def transpose_w(piece):
            g, nb0 = piece // (D // P // 2), 2 * (piece % (D // P // 2))
            wT = psum.tile([P, 2, HALVES, P], F32, tag="acc")
            for j in range(2):
                words = w_sb[:, nb0 + j, :].bitcast(F32)
                for u in range(HALVES):
                    w0 = (HALVES * g + u) * P
                    nc.tensor.transpose(wT[:, j, u, :], words[:, w0 : w0 + P], ident_f32[:])
            wT_banks[piece] = wT

        def attend(i, tag="o", blocks=range(QB)):
            v_codes, v_scales = v_operands[i]
            o_ps = psum.tile([P, QB, HD], F32, tag=tag)
            for qi in blocks:
                e_codes, e_scales = e_operands[(i, qi)]
                nc.tensor.matmul_mx(
                    out=o_ps[:, qi, :],
                    lhsT=e_codes.bitcast(FP8X4),
                    lhsT_scale=e_scales,
                    rhs=v_codes[:].bitcast(FP8X4),
                    rhs_scale=v_scales[:],
                    start=True,
                    stop=True,
                )
                o_banks[(i, qi)] = o_ps

        def project(r, tag=None, groups=range(GROUPS)):
            b, tb, nh = r // (QB * N_HALVES), (r // N_HALVES) % QB, r % N_HALVES
            a_codes, a_scales = a_operands[b]
            if tag:
                acc_new = psum.tile([P, BANK], F32, tag=tag)
                acc_banks[r] = acc_new
            for g in groups:
                nc.tensor.matmul_mx(
                    out=acc_banks[r][:],
                    lhsT=a_codes[:, g, tb * P : (tb + 1) * P].bitcast(FP8X4),
                    lhsT_scale=a_scales[:, g, tb * P : (tb + 1) * P],
                    rhs=w_codes[:, g, nh * BANK : (nh + 1) * BANK].bitcast(FP8X4),
                    rhs_scale=w_scales[:, g, nh * BANK : (nh + 1) * BANK],
                    start=(g == 0),
                    stop=(g == GROUPS - 1),
                )

        def copy_qk(i):
            qkT = work.tile([P, 2, S], BF16, bufs=9)
            nc.scalar.copy(out=qkT[:], in_=qkT_banks[i][:])
            qkT_tiles[i] = qkT

        def scale_and_min(i, bank_no):
            if i not in x_tiles:
                x_new = work.tile([P, x_cols(QB - 1).stop], F32)
                negmax_new = work.tile([P, QB], F32)
                x_tiles[i] = (x_new, negmax_new)
            x, negmax = x_tiles[i]
            for qi in SCORE_BANKS[bank_no][1]:
                nc.vector.tensor_scalar(
                    out=x[:, x_cols(qi)],
                    in0=score_banks[(i, qi)],
                    scalar1=-SCALE,
                    scalar2=None,
                    op0=ALU.mult,
                    op1=ALU.min,
                    accum_out=negmax[:, qi : qi + 1],
                )

        def exponentials(i, blocks):
            if i not in rowsums:
                rowsum_new = work.tile([P, QB], F32, bufs=8)
                rowsums[i] = rowsum_new
            x, negmax = x_tiles[i]
            for qi in blocks:
                nc.scalar.activation(
                    out=e_tiles[i % 3][:, e_start(qi) : e_start(qi) + n_keys(qi)],
                    in_=x[:, x_cols(qi)],
                    func=ACT.Exp,
                    scale=-1.0,
                    bias=negmax[:, qi : qi + 1],
                    accum_out=rowsums[i][:, qi : qi + 1],
                )

        def regroup_e(i, half, copy):
            ge_words = grouped_e[i % 2][:].bitcast(F32).rearrange("p (b q g) -> p b q g", b=QB, g=HALVES)
            copy(
                out=ge_words[:, 2 * half : 2 * half + 2], in_=eT_banks[(i, half)][:].rearrange("p g b q -> p b q g")
            )

        def quantise_e(i, lo=0, hi=QB):
            n = (hi - lo) * P
            e_codes = work.tile([P, n], U32, align_bytes=64, bufs=4, name="e_codes%d" % n)
            e_scales = work.tile([P, n], U8, align_bytes=64, bufs=4, name="e_scales%d" % n)
            nc.vector.quantize_mx(
                out=e_codes[:].bitcast(FP8X4),
                scales=e_scales[:],
                in_=grouped_e[i % 2][:, lo * P * PACK : hi * P * PACK],
            )
            for qi in range(lo, hi):
                cols = slice((qi - lo) * P, (qi - lo + 1) * P)
                e_operands[(i, qi)] = (e_codes[:, cols], e_scales[:, cols])

        def regroup_v(i, on_vector=False):
            v_sb = pair_tiles[i // 2][2]
            if on_vector:
                gv = work.tile([P, HD, PACK], BF16, align_bytes=64, bufs=2, name="gv_vector")
                nc.vector.tensor_copy(
                    out=gv[:].rearrange("p (c i) t -> p c t i", i=4),
                    in_=v_sb[:, i % 2].rearrange("p t (c i) -> p c t i", i=4),
                )
            else:
                gv = work.tile([P, HD, PACK], BF16, align_bytes=64, bufs=1)
                nc.gpsimd.tensor_scalar(
                    out=gv[:],
                    in0=v_sb[:, i % 2].rearrange("p t d -> p d t"),
                    scalar1=1.0,
                    scalar2=0.0,
                    op0=ALU.mult,
                    op1=ALU.add,
                )
            gv_tiles[i] = gv

        def quantise_v(i):
            gv = gv_tiles[i]
            v_codes = work.tile([P, HD], U32, align_bytes=64, bufs=8)
            v_scales = work.tile([P, HD], U8, align_bytes=64, bufs=8)
            nc.vector.quantize_mx(
                out=v_codes[:].bitcast(FP8X4), scales=v_scales[:], in_=gv[:].rearrange("p d t -> p (d t)")
            )
            v_operands[i] = (v_codes, v_scales)

        def invert_rowsum(i, lo=0, hi=QB):
            rinv = work.tile([P, QB], F32, bufs=6)
            nc.vector.reciprocal(out=rinv[:, lo:hi], in_=rowsums[i][:, lo:hi])
            for qi in range(lo, hi):
                rinv_tiles[(i, qi)] = rinv

        def a_of_head(i):
            group, t = i // PACK, i % PACK
            if group not in a_tiles:
                a_new = work.tile([P, QB, PACK * HD], BF16)
                a_tiles[group] = a_new
            return a_tiles[group][:, :, t * HD : (t + 1) * HD]

        def normalise(i, lo, hi):
            nc.vector.tensor_tensor(
                out=a_of_head(i)[:, lo:hi],
                in0=o_banks[(i, lo)][:, lo:hi],
                in1=rinv_tiles[(i, lo)][:, lo:hi].unsqueeze(2).to_broadcast([P, hi - lo, HD]),
                op=ALU.mult,
            )

        def normalise_on_scalar(i, lo, hi):
            for qi in range(lo, hi):
                nc.scalar.activation(
                    out=a_of_head(i)[:, qi],
                    in_=o_banks[(i, qi)][:, qi],
                    func=ACT.Copy,
                    scale=rinv_tiles[(i, qi)][:, qi : qi + 1],
                )

        def regroup_a(quarter, copy):
            ga = work.tile([P, P * PACK], BF16, align_bytes=64, bufs=9)
            copy(
                out=ga[:].bitcast(F32).rearrange("p (q u) -> p q u", u=HALVES),
                in_=aT_banks[quarter].rearrange("p (u q) -> p q u", u=HALVES),
            )
            ga_tiles[quarter] = ga

        def quantise_a(quarter):
            group, qi = quarter // QB, quarter % QB
            b, g = group // GROUPS, group % GROUPS
            if b not in a_operands:
                a_codes_new = work.tile([P, GROUPS, S], U32, align_bytes=64, bufs=2)
                a_scales_new = work.tile([P, GROUPS, S], U8, align_bytes=64, bufs=2)
                a_operands[b] = (a_codes_new, a_scales_new)
            a_codes, a_scales = a_operands[b]
            cols = slice(qi * P, (qi + 1) * P)
            nc.vector.quantize_mx(
                out=a_codes[:, g, cols].bitcast(FP8X4), scales=a_scales[:, g, cols], in_=ga_tiles[quarter][:]
            )

        def regroup_w(piece):
            gw = work.tile([P, 2 * P * PACK], BF16, align_bytes=64)
            dst = gw[:].bitcast(F32).rearrange("p (j n u) -> p j n u", j=2, u=HALVES)
            copy = nc.vector.tensor_copy if piece % 2 else nc.scalar.copy
            copy(out=dst, in_=wT_banks[piece][:].rearrange("p j u n -> p j n u"))
            gw_tiles[piece] = gw

        def quantise_w(piece):
            g, nb0 = piece // (D // P // 2), 2 * (piece % (D // P // 2))
            cols = slice(nb0 * P, (nb0 + 2) * P)
            nc.vector.quantize_mx(
                out=w_codes[:, g, cols].bitcast(FP8X4), scales=w_scales[:, g, cols], in_=gw_tiles[piece][:]
            )

        def add_bias_and_store(r, on_gpsimd=False):
            b, tb, nh = r // (QB * N_HALVES), (r // N_HALVES) % QB, r % N_HALVES
            n_cols = slice(nh * BANK, (nh + 1) * BANK)
            out_sb = work.tile([P, BANK], F32, bufs=14)
            if on_gpsimd:
                sums = work.tile([P, BANK], F32, bufs=4)
                nc.scalar.copy(out=sums[:], in_=acc_banks[r][:])
                nc.gpsimd.tensor_tensor(out=out_sb[:], in0=sums[:], in1=bias[:, n_cols], op=ALU.add)
            else:
                nc.vector.tensor_tensor(out=out_sb[:], in0=acc_banks[r][:], in1=bias[:, n_cols], op=ALU.add)
            nc.sync.dma_start(out=out[b, tb * P : (tb + 1) * P, n_cols], in_=out_sb[:])

        A_LAG = PACK + 5
        W_LAG = 5
        P_LAG = H + 6
        SC, VC = nc.scalar.copy, nc.vector.tensor_copy
        a_bank = None
        for s in range(-2, N_HEADS):
            quarter = s - A_LAG
            tile_now = s - P_LAG
            pair = (s + 2) // 2 + LOAD_AHEAD
            if s % 2 == 0 and pair < N_PAIRS + 1:
                if pair < N_PAIRS:
                    load_qk(pair)
                load_v(pair - 1)
            if s == 0:
                nc.sync.dma_start(out=w_sb[:], in_=w_out.rearrange("(nb p) f -> p nb f", p=P))
                nc.sync.dma_start(out=bias[:], in_=b_out.partition_broadcast(P))
            if live(s):
                scale_and_min(s, 2)
                scale_and_min(s, 0)
                scale_and_min(s, 1)
            if live(s - 5):
                normalise(s - 5, 0, QB if tile_now < 0 else 3)
            if live(s) and s < 2:
                exponentials(s, (1, 3, 2, 0))
            if 0 <= quarter < N_QUARTERS:
                transpose_a(quarter, a_bank)
                regroup_a(quarter, SC)
            if live(s + 2):
                transpose_qk(s + 2)
                copy_qk(s + 2)
            if live(s - 2):
                transpose_e(s - 2, 0)
                transpose_e(s - 2, 1)
            if 0 <= s - 1 - W_LAG < W_PIECES:
                regroup_w(s - 1 - W_LAG)
            if live(s - 5) and tile_now >= 0:
                normalise_on_scalar(s - 5, 3, QB)
            if live(s + 1):
                if quarter < 0:
                    for bank_no in (2, 0, 1):
                        bank = masks(s + 1, bank_no)
                        products(s + 1, bank_no)
                        if bank_no == 2:
                            a_bank = bank
                else:
                    for bank_no in (0, 1, 2):
                        a_bank = masks(s + 1, bank_no)
                    for bank_no in (2, 0, 1):
                        products(s + 1, bank_no)
            if 0 <= tile_now - 1 < N_TILES:
                add_bias_and_store(tile_now - 1)
            if live(s - 2):
                regroup_e(s - 2, 1, SC)
                regroup_e(s - 2, 0, SC)
            if live(s) and s >= 2:
                exponentials(s, (1, 3, 2, 0))
            if live(s - 3):
                quantise_e(s - 3)
            if 0 <= quarter < N_QUARTERS:
                quantise_a(quarter)
            if 0 <= s - 2 - W_LAG < W_PIECES:
                quantise_w(s - 2 - W_LAG)
            if live(s - 2):
                invert_rowsum(s - 2)
            if live(s - 3):
                quantise_v(s - 3)
            if live(s - 2):
                regroup_v(s - 2)
            if live(s - 4):
                attend(s - 4)
            if 0 <= tile_now < N_TILES:
                project(tile_now, "acc")
            if 0 <= s - W_LAG < W_PIECES:
                transpose_w(s - W_LAG)
            if s == -1:
                zero_low_bank()

        L = N_HEADS - 1

        def new_bank(tag):
            bank = psum.tile([P, BANK], F32, tag=tag)
            return bank

        transpose_e(L - 1, 0)
        transpose_e(L - 1, 1)
        regroup_v(L - 1, True)
        regroup_v(L, True)
        quantise_e(L - 2)
        quantise_v(L - 2)
        quantise_v(L - 1)
        quantise_v(L)
        normalise(L - 4, 0, QB)
        attend(L - 3, "s_a")
        attend(L - 2, "s_b")
        transpose_a(23, a_bank)
        regroup_e(L - 1, 0, SC)
        regroup_e(L - 1, 1, VC)
        project(18, "qkT")
        invert_rowsum(L - 1)
        invert_rowsum(L)
        transpose_e(L, 0)
        transpose_e(L, 1)
        x = new_bank("o")
        transpose_a(24, x, 0)
        transpose_a(25, x, 1)
        normalise_on_scalar(L - 3, 0, QB)
        quantise_e(L - 1)
        add_bias_and_store(17)
        normalise(L - 2, 0, QB)
        regroup_a(23, SC)
        project(19, "acc")
        attend(L - 1, "s_a")
        regroup_e(L, 1, SC)
        regroup_e(L, 0, VC)
        quantise_e(L)
        regroup_a(24, SC)
        regroup_a(25, SC)
        attend(L, "s_b")
        normalise_on_scalar(L - 1, 0, QB)
        add_bias_and_store(18)
        y = new_bank("s_c")
        transpose_a(26, y, 0)
        transpose_a(27, y, 1)
        project(20, "eT_high")
        quantise_a(23)
        quantise_a(24)
        normalise(L, 0, QB)
        add_bias_and_store(19)
        regroup_a(26, SC)
        regroup_a(27, SC)
        z = new_bank("o")
        w = new_bank("qkT")
        transpose_a(28, z, 0)
        transpose_a(29, z, 1)
        transpose_a(30, w, 0)
        transpose_a(31, w, 1)
        project(21, "acc")
        for q in (25, 26, 27):
            quantise_a(q)
        add_bias_and_store(20)
        regroup_a(28, SC)
        regroup_a(29, SC)
        regroup_a(30, VC)
        regroup_a(31, VC)
        project(22, "s_a")
        project(23, "s_b")
        for q in (28, 29, 30, 31):
            quantise_a(q)
        add_bias_and_store(21)
        add_bias_and_store(22)
        add_bias_and_store(23)
        tags = ("eT_high", "s_c", "o", "acc", "qkT", "s_a", "s_b", "eT_high")
        for j, r in enumerate(range(24, 32)):
            project(r, tags[j])
            add_bias_and_store(r)
